import numpy as np
import ml_dtypes


def mxq(x, axis, fmt="e4m3"):
    dtype, down = {"e4m3": (ml_dtypes.float8_e4m3fn, 7), "e5m2": (ml_dtypes.float8_e5m2, 14)}[fmt]
    v = np.moveaxis(np.asarray(x, np.float32).astype(ml_dtypes.bfloat16).astype(np.float64), axis, -1)
    blocks = v.reshape(v.shape[:-1] + (-1, 32))
    amax = np.abs(blocks).max(-1, keepdims=True)
    byte = np.maximum(np.where(amax > 0, np.frexp(amax)[1] - 1 + 127, 0) - down, 1)
    scale = np.exp2(byte - 127.0)
    codes = (blocks / scale).astype(np.float32).astype(dtype).astype(np.float64)
    return np.moveaxis((codes * scale).reshape(v.shape), -1, axis)


WIDE = False


def mx_kscale(k):
    if not WIDE:
        return np.ones(k)
    levels = np.array([10, -10, 5, -5, 0])
    a = np.random.permutation(np.resize(levels, k // 512 * 4)).reshape(k // 512, 4)
    idx = np.arange(k)
    return np.exp2(a[idx // 512, idx % 128 // 32])


BF16 = ml_dtypes.bfloat16


def bf(x):
    return np.asarray(x, np.float32).astype(BF16)


def f64(x):
    return np.asarray(x).astype(np.float64)


N, K, IN, HID, OUT = 512, 32, 512, 512, 512
NEG_SLOPE = 0.01


def leaky_relu(v):
    return np.where(v >= 0, v, NEG_SLOPE * v)


def safediv(a, b):
    return a / np.where(b == 0, np.ones_like(b), b)


def setup_inputs():
    s = mx_kscale(IN)
    u = mx_kscale(IN + HID)
    un, t = u[:IN], u[IN:]
    g = np.concatenate([np.full(IN, 1.0), np.full(HID, 3.0)])
    centre = np.random.standard_normal((N, 1, IN))
    return {"h_node": bf(np.random.standard_normal((N, IN)) * un),
            "h_ngbrs": bf((0.7 * centre + 0.7 * np.random.standard_normal((N, K, IN))) * s),
            "alpha": bf(np.random.uniform(0.0, 1.0, (N, K, 1))),
            "Wq": bf(np.random.standard_normal((HID, IN)) / np.sqrt(IN) * t[:, None] / s[None, :]),
            "bq": bf((-0.5 + 0.3 * np.random.standard_normal(HID)) * t),
            "Ww": bf(np.random.standard_normal((OUT, IN + HID)) * g[None, :] / np.sqrt(IN + HID) / u[None, :]),
            "bw": bf(-0.8 + 0.3 * np.random.standard_normal(OUT))}


def reference(h_node, h_ngbrs, alpha, Wq, bq, Ww, bw):
    a = f64(alpha)
    h1 = leaky_relu((mxq(f64(h_ngbrs), 2, "e4m3") @ mxq(f64(Wq), 1, "e4m3").T) + f64(bq))
    h_agg = safediv((a * h1).sum(axis=1), a.sum(axis=1))
    h_concat = np.concatenate([f64(h_node), h_agg], axis=-1)
    h2 = leaky_relu((mxq(h_concat, 1, "e4m3") @ mxq(f64(Ww), 1, "e4m3").T) + f64(bw))
    nrm = np.sqrt((h2 ** 2).sum(axis=-1, keepdims=True))
    return safediv(h2, nrm)

@@ -1,0 +1,259 @@
+from contextlib import ExitStack
+
+import concourse.bass as bass
+import concourse.mybir as mybir
+import concourse.tile as tile
+from concourse.masks import make_identity
+
+F32 = mybir.dt.float32
+BF16 = mybir.dt.bfloat16
+U32 = mybir.dt.uint32
+U8 = mybir.dt.uint8
+FP8X4 = mybir.dt.float8_e4m3fn_x4
+ALU = mybir.AluOpType
+ACT = mybir.ActivationFunctionType
+AX = mybir.AxisListType
+
+P = 128
+N_NODES, K_NGB, D_IN, D_HID, D_OUT = 512, 32, 512, 512, 512
+SLOPE = 0.01
+GROUPS = N_NODES // P
+KQ = 4
+QUADS = K_NGB // KQ
+HC = D_HID // P
+KG = 3
+
+FLOPS = 2 * N_NODES * K_NGB * D_IN * D_HID + 2 * N_NODES * (D_IN + D_HID) * D_OUT
+
+
+def tile_pinsageconv_t_kernel(tc, h_node, h_ngbrs, alpha, Wq, bq, Ww, bw, out):
+    nc = tc.nc
+    with ExitStack() as ctx:
+        const = ctx.enter_context(tc.tile_pool(name="const", bufs=1))
+        xin = ctx.enter_context(tc.tile_pool(name="xin", bufs=4))
+        grp = ctx.enter_context(tc.tile_pool(name="grp", bufs=3))
+        qnt = ctx.enter_context(tc.tile_pool(name="qnt", bufs=3))
+        ypool = ctx.enter_context(tc.tile_pool(name="ypool", bufs=3))
+        epool = ctx.enter_context(tc.tile_pool(name="epool", bufs=8))
+        tail = ctx.enter_context(tc.tile_pool(name="tail", bufs=2))
+        pxt = ctx.enter_context(tc.psum_pool(name="pxt", bufs=2))
+        pz = ctx.enter_context(tc.psum_pool(name="pz", bufs=2))
+        pe = ctx.enter_context(tc.psum_pool(name="pe", bufs=2))
+        pacc = ctx.enter_context(tc.psum_pool(name="pacc", bufs=2))
+        eapool = ctx.enter_context(tc.tile_pool(name="eapool", bufs=8))
+
+        wq_raw = const.tile([P, HC, D_IN], BF16)
+        nc.sync.dma_start(out=wq_raw[:], in_=Wq.rearrange("(b p) i -> p b i", p=P))
+
+        b_rows = const.tile([P, P], BF16)
+        nc.vector.memset(b_rows[:], 0.0)
+        nc.scalar.dma_start(out=b_rows[0:HC, :], in_=bq.rearrange("(b p) -> b p", p=P))
+        a_raw = const.tile([P, GROUPS, K_NGB], BF16)
+        nc.scalar.dma_start(out=a_raw[:], in_=alpha.rearrange("(g p) k o -> p g (k o)", p=P))
+
+        a_bc = const.tile([P, N_NODES, K_NGB], BF16)
+        a_flat = alpha.rearrange("(g n) k o -> g (n k o)", g=GROUPS)
+        for g in range(GROUPS):
+            nc.gpsimd.dma_start(
+                out=a_bc[:, g * P : (g + 1) * P, :].rearrange("p n k -> p (n k)"),
+                in_=a_flat[g].partition_broadcast(P),
+            )
+
+        ww_raw = const.tile([P, D_OUT // P, D_IN + D_HID], BF16)
+        nc.gpsimd.dma_start(out=ww_raw[:], in_=Ww.rearrange("(b p) c -> p b c", p=P))
+        hn_raw = const.tile([P, GROUPS, D_IN], BF16)
+        nc.gpsimd.dma_start(out=hn_raw[:], in_=h_node.rearrange("(g p) i -> p g i", p=P))
+        bw_bc = const.tile([P, D_OUT], BF16)
+        nc.gpsimd.dma_start(out=bw_bc[:], in_=bw.partition_broadcast(P))
+
+        ident_f = const.tile([P, P], F32)
+        make_identity(nc, ident_f[:])
+        ident_b = const.tile([P, P], BF16)
+        make_identity(nc, ident_b[:])
+        one = const.tile([P, 1], F32)
+        nc.vector.memset(one[:], 1.0)
+        one_s = const.tile([P, 1], F32)
+        nc.scalar.sqrt(out=one_s[:], in_=one[:])
+
+        def words_to_mx(src_words, codes, scales):
+            grouped = grp.tile([P, 4 * P, 4], BF16, align_bytes=64, tag="grouped")
+            g_words = grouped[:].bitcast(F32)
+            for half in range(2):
+                xt = pxt.tile([P, 2, 2, P], F32, tag="xt")
+                for b in range(2):
+                    for u in range(2):
+                        nc.tensor.transpose(
+                            xt[:, b, u, :], src_words[:, 2 * half + b, u * P : (u + 1) * P], ident_f[:]
+                        )
+                nc.scalar.copy(
+                    out=g_words[:, 2 * half * P : (2 * half + 2) * P, :].rearrange(
+                        "p (b c) u -> p b c u", b=2
+                    ),
+                    in_=xt[:].rearrange("p b u c -> p b c u"),
+                )
+            nc.vector.quantize_mx(
+                out=codes.bitcast(FP8X4),
+                scales=scales,
+                in_=grouped[:].rearrange("p c t -> p (c t)"),
+            )
+
+        wq_c = const.tile([P, D_HID], U32, align_bytes=64)
+        wq_s = const.tile([P, D_HID], U8, align_bytes=64)
+        words_to_mx(wq_raw[:].bitcast(F32), wq_c[:], wq_s[:])
+
+        bT = pxt.tile([P, P], BF16, tag="xt")
+        nc.tensor.transpose(bT[:], b_rows[:], ident_b[:])
+        b_col = const.tile([P, HC], F32)
+        nc.vector.tensor_copy(out=b_col[:], in_=bT[:, 0:HC])
+        b_low = const.tile([P, HC], F32)
+        nc.vector.tensor_scalar(out=b_low[:], in0=b_col[:], scalar1=SLOPE, scalar2=None, op0=ALU.mult)
+
+        a_f = const.tile([P, GROUPS, K_NGB], F32)
+        nc.vector.tensor_copy(out=a_f[:], in_=a_raw[:])
+        a_sum = const.tile([P, GROUPS], F32)
+        nc.vector.tensor_reduce(out=a_sum[:], in_=a_f[:], axis=AX.X, op=ALU.add)
+        a_den = const.tile([P, GROUPS], F32)
+        nc.vector.scalar_tensor_tensor(
+            out=a_den[:], in0=a_sum[:], scalar=0.0, in1=a_sum[:], op0=ALU.is_equal, op1=ALU.add
+        )
+        a_rec = const.tile([P, GROUPS], F32)
+        nc.vector.reciprocal(out=a_rec[:], in_=a_den[:])
+        a_n = const.tile([P, GROUPS, K_NGB], F32)
+        nc.vector.tensor_tensor(
+            out=a_n[:],
+            in0=a_f[:],
+            in1=a_rec[:].unsqueeze(2).to_broadcast([P, GROUPS, K_NGB]),
+            op=ALU.mult,
+        )
+
+        w0_c = const.tile([P, D_OUT], U32, align_bytes=64)
+        w0_s = const.tile([P, D_OUT], U8, align_bytes=64)
+        w1_c = const.tile([P, D_OUT], U32, align_bytes=64)
+        w1_s = const.tile([P, D_OUT], U8, align_bytes=64)
+        hn_c = const.tile([P, N_NODES], U32, align_bytes=64)
+        hn_s = const.tile([P, N_NODES], U8, align_bytes=64)
+
+        def prepare_second_layer():
+            words_to_mx(ww_raw[:].bitcast(F32)[:, :, 0 : D_IN // 2], w0_c[:], w0_s[:])
+            words_to_mx(hn_raw[:].bitcast(F32), hn_c[:], hn_s[:])
+            grouped = grp.tile([P, 4 * P, 4], BF16, align_bytes=64, tag="grouped")
+            for ob in range(4):
+                wt = pxt.tile([P, 4, P], BF16, tag="xt")
+                for t in range(4):
+                    nc.tensor.transpose(
+                        wt[:, t, :], ww_raw[:, ob, D_IN + t * P : D_IN + (t + 1) * P], ident_b[:]
+                    )
+                nc.scalar.copy(
+                    out=grouped[:, ob * P : (ob + 1) * P, :], in_=wt[:].rearrange("p t c -> p c t")
+                )
+            nc.vector.quantize_mx(
+                out=w1_c[:].bitcast(FP8X4), scales=w1_s[:], in_=grouped[:].rearrange("p c t -> p (c t)")
+            )
+
+        def second_layer(g, acc, accp):
+            hagg = tail.tile([P, D_HID], F32)
+            nc.vector.scalar_tensor_tensor(
+                out=hagg[:], in0=accp[:], scalar=a_rec[:, g : g + 1], in1=acc[:], op0=ALU.mult, op1=ALU.add
+            )
+            hT = pxt.tile([P, 4, P], F32, tag="xt")
+            for t in range(4):
+                nc.tensor.transpose(hT[:, t, :], hagg[:, t * P : (t + 1) * P], ident_f[:])
+            hg = tail.tile([P, P, 4], BF16, align_bytes=64)
+            nc.scalar.copy(out=hg[:], in_=hT[:].rearrange("p t c -> p c t"))
+            ha_c = tail.tile([P, P], U32, align_bytes=64)
+            ha_s = tail.tile([P, P], U8, align_bytes=64)
+            nc.vector.quantize_mx(
+                out=ha_c[:].bitcast(FP8X4), scales=ha_s[:], in_=hg[:].rearrange("p c t -> p (c t)")
+            )
+            z2 = pz.tile([P, D_OUT], F32, tag="z")
+            cols = slice(g * P, (g + 1) * P)
+            nc.tensor.matmul_mx(
+                out=z2[:], lhsT=hn_c[:, cols].bitcast(FP8X4), lhsT_scale=hn_s[:, cols],
+                rhs=w0_c[:].bitcast(FP8X4), rhs_scale=w0_s[:], start=True, stop=False,
+            )
+            nc.tensor.matmul_mx(
+                out=z2[:], lhsT=ha_c[:].bitcast(FP8X4), lhsT_scale=ha_s[:],
+                rhs=w1_c[:].bitcast(FP8X4), rhs_scale=w1_s[:], start=False, stop=True,
+            )
+            v2 = tail.tile([P, D_OUT], F32)
+            nc.vector.tensor_tensor(out=v2[:], in0=z2[:], in1=bw_bc[:], op=ALU.add)
+            h2 = tail.tile([P, D_OUT], F32)
+            nc.vector.scalar_tensor_tensor(
+                out=h2[:], in0=v2[:], scalar=SLOPE, in1=v2[:], op0=ALU.mult, op1=ALU.max
+            )
+            sq = tail.tile([P, D_OUT], F32)
+            ss = tail.tile([P, 1], F32)
+            nc.scalar.activation(out=sq[:], in_=h2[:], func=ACT.Square, accum_out=ss[:])
+            nrm = tail.tile([P, 1], F32)
+            nc.scalar.sqrt(out=nrm[:], in_=ss[:])
+            den = tail.tile([P, 1], F32)
+            nc.vector.scalar_tensor_tensor(
+                out=den[:], in0=nrm[:], scalar=0.0, in1=nrm[:], op0=ALU.is_equal, op1=ALU.add
+            )
+            rec = tail.tile([P, 1], F32)
+            nc.vector.reciprocal(out=rec[:], in_=den[:])
+            res = tail.tile([P, D_OUT], F32)
+            nc.vector.tensor_scalar(out=res[:], in0=h2[:], scalar1=rec[:, 0:1], scalar2=None, op0=ALU.mult)
+            nc.sync.dma_start(out=out[g * P : (g + 1) * P, :], in_=res[:])
+
+        for g in range(GROUPS):
+            acc = const.tile([P, D_HID], F32, name="acc%d" % g)
+            accp = pacc.tile([P, D_HID], F32)
+            for q in range(QUADS):
+                x_sb = xin.tile([P, KQ, D_IN], BF16)
+                nc.sync.dma_start(
+                    out=x_sb[:], in_=h_ngbrs[g * P : (g + 1) * P, q * KQ : (q + 1) * KQ, :]
+                )
+                x_c = qnt.tile([P, KQ * P], U32, align_bytes=64)
+                x_s = qnt.tile([P, KQ * P], U8, align_bytes=64)
+                words_to_mx(x_sb[:].bitcast(F32), x_c[:], x_s[:])
+                e_tiles = []
+                for hc in range(HC):
+                    cols = slice(hc * P, (hc + 1) * P)
+                    z = pz.tile([P, KQ * P], F32, tag="z")
+                    nc.tensor.matmul_mx(
+                        out=z[:], lhsT=wq_c[:, cols].bitcast(FP8X4), lhsT_scale=wq_s[:, cols],
+                        rhs=x_c[:].bitcast(FP8X4), rhs_scale=x_s[:], start=True, stop=True,
+                    )
+                    y = ypool.tile([P, KQ * P], F32)
+                    nc.scalar.activation(
+                        out=y[:], in_=z[:], func=ACT.Identity, bias=b_low[:, hc : hc + 1], scale=SLOPE
+                    )
+                    e = epool.tile([P, KQ * P], F32)
+                    nc.vector.scalar_tensor_tensor(
+                        out=e[:], in0=z[:], scalar=b_col[:, hc : hc + 1], in1=y[:], op0=ALU.add, op1=ALU.max
+                    )
+                    e_tiles.append(e)
+                    ea = eapool.tile([P, KG * P], F32)
+                    nc.gpsimd.tensor_tensor(
+                        out=ea[:].rearrange("p (k n) -> p k n", k=KG),
+                        in0=e[:, 0 : KG * P].rearrange("p (k n) -> p k n", k=KG),
+                        in1=a_bc[:, g * P : (g + 1) * P, q * KQ : q * KQ + KG].rearrange("p n k -> p k n"),
+                        op=ALU.mult,
+                    )
+                    for kk in range(KG):
+                        nc.tensor.matmul(
+                            out=accp[:, hc * P : (hc + 1) * P], lhsT=ea[:, kk * P : (kk + 1) * P], rhs=ident_f[:],
+                            is_transpose=True,
+                            start=(q == 0 and hc == 0 and kk == 0),
+                            stop=(q == QUADS - 1 and hc == HC - 1 and kk == KG - 1),
+                        )
+                for kk in range(KG, KQ):
+                    eT = pe.tile([P, D_HID], F32)
+                    for hc in range(HC):
+                        nc.tensor.transpose(
+                            eT[:, hc * P : (hc + 1) * P], e_tiles[hc][:, kk * P : (kk + 1) * P], ident_f[:]
+                        )
+                    k = q * KQ + kk
+                    if k == KG:
+                        nc.vector.tensor_scalar(
+                            out=acc[:], in0=eT[:], scalar1=a_n[:, g, k : k + 1], scalar2=None, op0=ALU.mult
+                        )
+                    else:
+                        nc.vector.scalar_tensor_tensor(
+                            out=acc[:], in0=eT[:], scalar=a_n[:, g, k : k + 1], in1=acc[:],
+                            op0=ALU.mult, op1=ALU.add,
+                        )
+                if g == 0 and q == 1:
+                    prepare_second_layer()
+            second_layer(g, acc, accp)

@@ -1,8 +1,6 @@
 from contextlib import ExitStack
 
-import concourse.bass as bass
 import concourse.mybir as mybir
-import concourse.tile as tile
 from concourse.masks import make_identity
 
 F32 = mybir.dt.float32
@@ -20,93 +18,133 @@ SLOPE = 0.01
 GROUPS = N_NODES // P
 KQ = 4
 QUADS = K_NGB // KQ
+NQ = GROUPS * QUADS
 HC = D_HID // P
-KG = 3
+NT = NQ * HC
+NSTEP = NT // 2
+KG_PATTERN = (3,)
+MANUAL = True
+RES_ON_SCALAR = True
+PREP0 = 6
 
 FLOPS = 2 * N_NODES * K_NGB * D_IN * D_HID + 2 * N_NODES * (D_IN + D_HID) * D_OUT
+
+
+def kg_of(qd):
+    return KG_PATTERN[qd % len(KG_PATTERN)]
 
 
 def tile_pinsageconv_t_kernel(tc, h_node, h_ngbrs, alpha, Wq, bq, Ww, bw, out):
     nc = tc.nc
     with ExitStack() as ctx:
         const = ctx.enter_context(tc.tile_pool(name="const", bufs=1))
-        xin = ctx.enter_context(tc.tile_pool(name="xin", bufs=4))
+        xin = ctx.enter_context(tc.tile_pool(name="xin", bufs=6))
         grp = ctx.enter_context(tc.tile_pool(name="grp", bufs=3))
         qnt = ctx.enter_context(tc.tile_pool(name="qnt", bufs=3))
         ypool = ctx.enter_context(tc.tile_pool(name="ypool", bufs=3))
-        epool = ctx.enter_context(tc.tile_pool(name="epool", bufs=8))
+        epool = ctx.enter_context(tc.tile_pool(name="epool", bufs=10))
+        eapool = ctx.enter_context(tc.tile_pool(name="eapool", bufs=8))
         tail = ctx.enter_context(tc.tile_pool(name="tail", bufs=2))
-        pxt = ctx.enter_context(tc.psum_pool(name="pxt", bufs=2))
-        pz = ctx.enter_context(tc.psum_pool(name="pz", bufs=2))
+        pxt = ctx.enter_context(tc.psum_pool(name="pxt", bufs=1))
+        pz = ctx.enter_context(tc.psum_pool(name="pz", bufs=3))
         pe = ctx.enter_context(tc.psum_pool(name="pe", bufs=2))
         pacc = ctx.enter_context(tc.psum_pool(name="pacc", bufs=2))
-        eapool = ctx.enter_context(tc.tile_pool(name="eapool", bufs=8))
-
-        wq_raw = const.tile([P, HC, D_IN], BF16)
-        nc.sync.dma_start(out=wq_raw[:], in_=Wq.rearrange("(b p) i -> p b i", p=P))
-
-        b_rows = const.tile([P, P], BF16)
-        nc.vector.memset(b_rows[:], 0.0)
-        nc.scalar.dma_start(out=b_rows[0:HC, :], in_=bq.rearrange("(b p) -> b p", p=P))
-        a_raw = const.tile([P, GROUPS, K_NGB], BF16)
-        nc.scalar.dma_start(out=a_raw[:], in_=alpha.rearrange("(g p) k o -> p g (k o)", p=P))
-
-        a_bc = const.tile([P, N_NODES, K_NGB], BF16)
-        a_flat = alpha.rearrange("(g n) k o -> g (n k o)", g=GROUPS)
-        for g in range(GROUPS):
-            nc.gpsimd.dma_start(
-                out=a_bc[:, g * P : (g + 1) * P, :].rearrange("p n k -> p (n k)"),
-                in_=a_flat[g].partition_broadcast(P),
-            )
-
-        ww_raw = const.tile([P, D_OUT // P, D_IN + D_HID], BF16)
-        nc.gpsimd.dma_start(out=ww_raw[:], in_=Ww.rearrange("(b p) c -> p b c", p=P))
-        hn_raw = const.tile([P, GROUPS, D_IN], BF16)
-        nc.gpsimd.dma_start(out=hn_raw[:], in_=h_node.rearrange("(g p) i -> p g i", p=P))
-        bw_bc = const.tile([P, D_OUT], BF16)
-        nc.gpsimd.dma_start(out=bw_bc[:], in_=bw.partition_broadcast(P))
+        if MANUAL:
+            ctx.enter_context(tc.manual_schedule())
 
         ident_f = const.tile([P, P], F32)
         make_identity(nc, ident_f[:])
         ident_b = const.tile([P, P], BF16)
         make_identity(nc, ident_b[:])
+
+        wq_raw = const.tile([P, HC, D_IN], BF16)
+        nc.sync.dma_start(out=wq_raw[:], in_=Wq.rearrange("(b p) i -> p b i", p=P))
+
+        x_sb = {}
+
+        def load(qd):
+            g, q = divmod(qd, QUADS)
+            x_sb[qd] = xin.tile([P, KQ, D_IN], BF16, name="x_sb")
+            nc.sync.dma_start(
+                out=x_sb[qd][:], in_=h_ngbrs[g * P : (g + 1) * P, q * KQ : (q + 1) * KQ, :]
+            )
+
+        a_bc = const.tile([P, N_NODES, K_NGB], BF16)
+        a_flat = alpha.rearrange("(g n) k o -> g (n k o)", g=GROUPS)
+
+        def load_a_bc(g):
+            nc.sync.dma_start(
+                out=a_bc[:, g * P : (g + 1) * P, :].rearrange("p n k -> p (n k)"),
+                in_=a_flat[g].partition_broadcast(P),
+            )
+
+        load(0)
+        load(1)
+        load_a_bc(0)
+        load(2)
+        load(3)
+
+        b_rows = const.tile([P, P], BF16)
+        nc.vector.memset(b_rows[:], 0.0)
         one = const.tile([P, 1], F32)
         nc.vector.memset(one[:], 1.0)
+        nc.scalar.dma_start(out=b_rows[0:HC, :], in_=bq.rearrange("(b p) -> b p", p=P))
+        a_raw = const.tile([P, GROUPS, K_NGB], BF16)
+        nc.scalar.dma_start(out=a_raw[:], in_=alpha.rearrange("(g p) k o -> p g (k o)", p=P))
         one_s = const.tile([P, 1], F32)
         nc.scalar.sqrt(out=one_s[:], in_=one[:])
 
-        def words_to_mx(src_words, codes, scales):
-            grouped = grp.tile([P, 4 * P, 4], BF16, align_bytes=64, tag="grouped")
-            g_words = grouped[:].bitcast(F32)
-            for half in range(2):
-                xt = pxt.tile([P, 2, 2, P], F32, tag="xt")
-                for b in range(2):
-                    for u in range(2):
-                        nc.tensor.transpose(
-                            xt[:, b, u, :], src_words[:, 2 * half + b, u * P : (u + 1) * P], ident_f[:]
-                        )
-                nc.scalar.copy(
-                    out=g_words[:, 2 * half * P : (2 * half + 2) * P, :].rearrange(
-                        "p (b c) u -> p b c u", b=2
-                    ),
-                    in_=xt[:].rearrange("p b u c -> p b c u"),
-                )
+        ww_raw = const.tile([P, D_OUT // P, D_IN + D_HID], BF16)
+        hn_raw = const.tile([P, GROUPS, D_IN], BF16)
+        bw_bc = const.tile([P, D_OUT], BF16)
+
+        def late_loads(j):
+            if j == 0:
+                nc.sync.dma_start(out=ww_raw[:], in_=Ww.rearrange("(b p) c -> p b c", p=P))
+            elif j == 2:
+                nc.sync.dma_start(out=hn_raw[:], in_=h_node.rearrange("(g p) i -> p g i", p=P))
+                nc.sync.dma_start(out=bw_bc[:], in_=bw.partition_broadcast(P))
+            elif j in (4, 8, 12):
+                load_a_bc(j // 4)
+
+        def words_T(src_words, half, pool, tag):
+            xt = pool.tile([P, 2, 2, P], F32, tag=tag, name="xt")
+            for b in range(2):
+                for u in range(2):
+                    nc.tensor.transpose(
+                        xt[:, b, u, :], src_words[:, 2 * half + b, u * P : (u + 1) * P], ident_f[:]
+                    )
+            return xt
+
+        def words_copy(xt, grouped, half):
+            nc.scalar.copy(
+                out=grouped[:].bitcast(F32)[:, 2 * half * P : (2 * half + 2) * P, :].rearrange(
+                    "p (b c) u -> p b c u", b=2
+                ),
+                in_=xt[:].rearrange("p b u c -> p b c u"),
+            )
+
+        def quantise(grouped, codes, scales):
             nc.vector.quantize_mx(
-                out=codes.bitcast(FP8X4),
-                scales=scales,
-                in_=grouped[:].rearrange("p c t -> p (c t)"),
+                out=codes.bitcast(FP8X4), scales=scales, in_=grouped[:].rearrange("p c t -> p (c t)")
             )
 
         wq_c = const.tile([P, D_HID], U32, align_bytes=64)
         wq_s = const.tile([P, D_HID], U8, align_bytes=64)
-        words_to_mx(wq_raw[:].bitcast(F32), wq_c[:], wq_s[:])
+        wq_g = grp.tile([P, 4 * P, 4], BF16, align_bytes=64, tag="grouped", name="wq_g")
+        wq_words = wq_raw[:].bitcast(F32)
+        wt0 = words_T(wq_words, 0, pz, "z")
+        wt1 = words_T(wq_words, 1, pz, "z")
+        words_copy(wt0, wq_g, 0)
+        words_copy(wt1, wq_g, 1)
 
-        bT = pxt.tile([P, P], BF16, tag="xt")
+        bT = pe.tile([P, P], BF16, tag="eT", name="bT")
         nc.tensor.transpose(bT[:], b_rows[:], ident_b[:])
         b_col = const.tile([P, HC], F32)
         nc.vector.tensor_copy(out=b_col[:], in_=bT[:, 0:HC])
         b_low = const.tile([P, HC], F32)
         nc.vector.tensor_scalar(out=b_low[:], in0=b_col[:], scalar1=SLOPE, scalar2=None, op0=ALU.mult)
+        quantise(wq_g, wq_c[:], wq_s[:])
 
         a_f = const.tile([P, GROUPS, K_NGB], F32)
         nc.vector.tensor_copy(out=a_f[:], in_=a_raw[:])
@@ -120,10 +158,7 @@ def tile_pinsageconv_t_kernel(tc, h_node, h_ngbrs, alpha, Wq, bq, Ww, bw, out):
         nc.vector.reciprocal(out=a_rec[:], in_=a_den[:])
         a_n = const.tile([P, GROUPS, K_NGB], F32)
         nc.vector.tensor_tensor(
-            out=a_n[:],
-            in0=a_f[:],
-            in1=a_rec[:].unsqueeze(2).to_broadcast([P, GROUPS, K_NGB]),
-            op=ALU.mult,
+            out=a_n[:], in0=a_f[:], in1=a_rec[:].unsqueeze(2).to_broadcast([P, GROUPS, K_NGB]), op=ALU.mult
         )
 
         w0_c = const.tile([P, D_OUT], U32, align_bytes=64)
@@ -132,40 +167,198 @@ def tile_pinsageconv_t_kernel(tc, h_node, h_ngbrs, alpha, Wq, bq, Ww, bw, out):
         w1_s = const.tile([P, D_OUT], U8, align_bytes=64)
         hn_c = const.tile([P, N_NODES], U32, align_bytes=64)
         hn_s = const.tile([P, N_NODES], U8, align_bytes=64)
+        prep_g = {}
+        prep_ps = {}
 
-        def prepare_second_layer():
-            words_to_mx(ww_raw[:].bitcast(F32)[:, :, 0 : D_IN // 2], w0_c[:], w0_s[:])
-            words_to_mx(hn_raw[:].bitcast(F32), hn_c[:], hn_s[:])
-            grouped = grp.tile([P, 4 * P, 4], BF16, align_bytes=64, tag="grouped")
-            for ob in range(4):
-                wt = pxt.tile([P, 4, P], BF16, tag="xt")
+        def prep_T(i):
+            if i % 4 == 0 or i == 2:
+                prep_g[i] = const.tile([P, 4 * P, 4], BF16, align_bytes=64, name="prep_g%d" % i)
+            if i < 2:
+                prep_ps[i] = words_T(ww_raw[:].bitcast(F32)[:, :, 0 : D_IN // 2], i, pz, "z")
+            elif i < 4:
+                prep_ps[i] = words_T(hn_raw[:].bitcast(F32), i - 2, pz, "z")
+            else:
+                ob = i - 4
+                wt = pz.tile([P, 4, P], BF16, tag="z", name="wt")
                 for t in range(4):
                     nc.tensor.transpose(
                         wt[:, t, :], ww_raw[:, ob, D_IN + t * P : D_IN + (t + 1) * P], ident_b[:]
                     )
+                prep_ps[i] = wt
+
+        def prep_copy(i):
+            if i < 2:
+                words_copy(prep_ps[i], prep_g[0], i)
+            elif i < 4:
+                words_copy(prep_ps[i], prep_g[2], i - 2)
+            else:
+                ob = i - 4
                 nc.scalar.copy(
-                    out=grouped[:, ob * P : (ob + 1) * P, :], in_=wt[:].rearrange("p t c -> p c t")
+                    out=prep_g[4][:, ob * P : (ob + 1) * P, :], in_=prep_ps[i][:].rearrange("p t c -> p c t")
                 )
-            nc.vector.quantize_mx(
-                out=w1_c[:].bitcast(FP8X4), scales=w1_s[:], in_=grouped[:].rearrange("p c t -> p (c t)")
+
+        def prep_quant(i):
+            if i == 1:
+                quantise(prep_g[0], w0_c[:], w0_s[:])
+            elif i == 3:
+                quantise(prep_g[2], hn_c[:], hn_s[:])
+            elif i == 7:
+                quantise(prep_g[4], w1_c[:], w1_s[:])
+
+        grouped = {}
+        xt_ps = {}
+        x_c = {}
+        x_s = {}
+        z_ps = {}
+        y_sb = {}
+        e_sb = {}
+        ea_sb = {}
+        eT_ps = {}
+        acc = {}
+        accp = {}
+
+        def x_T(xh):
+            qd, half = divmod(xh, 2)
+            if half == 0:
+                grouped[qd] = grp.tile([P, 4 * P, 4], BF16, align_bytes=64, tag="grouped", name="grouped")
+            if xh < 2:
+                xt_ps[xh] = words_T(x_sb[qd][:].bitcast(F32), half, pe, "eT")
+            else:
+                xt_ps[xh] = words_T(x_sb[qd][:].bitcast(F32), half, pxt, "xt")
+
+        def x_copy(xh):
+            qd, half = divmod(xh, 2)
+            words_copy(xt_ps[xh], grouped[qd], half)
+
+        def x_quant(qd):
+            x_c[qd] = qnt.tile([P, KQ * P], U32, align_bytes=64, name="x_c")
+            x_s[qd] = qnt.tile([P, KQ * P], U8, align_bytes=64, name="x_s")
+            quantise(grouped[qd], x_c[qd][:], x_s[qd][:])
+
+        def mx(t):
+            qd, hc = divmod(t, HC)
+            cols = slice(hc * P, (hc + 1) * P)
+            z_ps[t] = pz.tile([P, KQ * P], F32, tag="z", name="z")
+            nc.tensor.matmul_mx(
+                out=z_ps[t][:], lhsT=wq_c[:, cols].bitcast(FP8X4), lhsT_scale=wq_s[:, cols],
+                rhs=x_c[qd][:].bitcast(FP8X4), rhs_scale=x_s[qd][:], start=True, stop=True,
             )
 
-        def second_layer(g, acc, accp):
-            hagg = tail.tile([P, D_HID], F32)
+        def ylow(t):
+            hc = t % HC
+            y_sb[t] = ypool.tile([P, KQ * P], F32, name="y")
+            nc.scalar.activation(
+                out=y_sb[t][:], in_=z_ps[t][:], func=ACT.Identity, bias=b_low[:, hc : hc + 1], scale=SLOPE
+            )
+
+        def emax(t):
+            hc = t % HC
+            e_sb[t] = epool.tile([P, KQ * P], F32, name="e")
             nc.vector.scalar_tensor_tensor(
-                out=hagg[:], in0=accp[:], scalar=a_rec[:, g : g + 1], in1=acc[:], op0=ALU.mult, op1=ALU.add
+                out=e_sb[t][:], in0=z_ps[t][:], scalar=b_col[:, hc : hc + 1], in1=y_sb[t][:],
+                op0=ALU.add, op1=ALU.max,
             )
-            hT = pxt.tile([P, 4, P], F32, tag="xt")
+
+        def gmul(t):
+            qd = t // HC
+            g, q = divmod(qd, QUADS)
+            kg = kg_of(qd)
+            if kg == 0:
+                return
+            ea_sb[t] = eapool.tile([P, kg * P], F32, tag="ea", name="ea")
+            nc.gpsimd.tensor_tensor(
+                out=ea_sb[t][:].rearrange("p (k n) -> p k n", k=kg),
+                in0=e_sb[t][:, 0 : kg * P].rearrange("p (k n) -> p k n", k=kg),
+                in1=a_bc[:, g * P : (g + 1) * P, q * KQ : q * KQ + kg].rearrange("p n k -> p k n"),
+                op=ALU.mult,
+            )
+
+        first_acc = {}
+        last_acc = {}
+        for g in range(GROUPS):
+            with_g = [qd for qd in range(g * QUADS, (g + 1) * QUADS) if kg_of(qd) > 0]
+            if with_g:
+                first_acc[g] = with_g[0] * HC
+                last_acc[g] = with_g[-1] * HC + HC - 1
+
+        def tacc(t):
+            qd, hc = divmod(t, HC)
+            g = qd // QUADS
+            kg = kg_of(qd)
+            if kg == 0:
+                return
+            if t == first_acc[g]:
+                accp[g] = pacc.tile([P, D_HID], F32, name="accp")
+            for kk in range(kg):
+                nc.tensor.matmul(
+                    out=accp[g][:, hc * P : (hc + 1) * P], lhsT=ea_sb[t][:, kk * P : (kk + 1) * P],
+                    rhs=ident_f[:], is_transpose=True,
+                    start=(t == first_acc[g] and kk == 0), stop=(t == last_acc[g] and kk == kg - 1),
+                )
+
+        def tk(qd):
+            for kk in range(kg_of(qd), KQ):
+                eT_ps[(qd, kk)] = pe.tile([P, D_HID], F32, tag="eT", name="eT")
+                for hc in range(HC):
+                    nc.tensor.transpose(
+                        eT_ps[(qd, kk)][:, hc * P : (hc + 1) * P],
+                        e_sb[qd * HC + hc][:, kk * P : (kk + 1) * P], ident_f[:],
+                    )
+
+        def fma(qd):
+            g, q = divmod(qd, QUADS)
+            for kk in range(kg_of(qd), KQ):
+                k = q * KQ + kk
+                if g not in acc:
+                    acc[g] = const.tile([P, D_HID], F32, name="acc%d" % g)
+                    nc.vector.tensor_scalar(
+                        out=acc[g][:], in0=eT_ps[(qd, kk)][:], scalar1=a_n[:, g, k : k + 1], scalar2=None,
+                        op0=ALU.mult,
+                    )
+                else:
+                    nc.vector.scalar_tensor_tensor(
+                        out=acc[g][:], in0=eT_ps[(qd, kk)][:], scalar=a_n[:, g, k : k + 1], in1=acc[g][:],
+                        op0=ALU.mult, op1=ALU.add,
+                    )
+
+        s2 = {}
+
+        def l2_hagg(g):
+            if g in accp and g in acc:
+                hagg = tail.tile([P, D_HID], F32, name="hagg")
+                nc.vector.scalar_tensor_tensor(
+                    out=hagg[:], in0=accp[g][:], scalar=a_rec[:, g : g + 1], in1=acc[g][:],
+                    op0=ALU.mult, op1=ALU.add,
+                )
+            elif g in accp:
+                hagg = tail.tile([P, D_HID], F32, name="hagg")
+                nc.vector.tensor_scalar(
+                    out=hagg[:], in0=accp[g][:], scalar1=a_rec[:, g : g + 1], scalar2=None, op0=ALU.mult
+                )
+            else:
+                hagg = acc[g]
+            s2[(g, "hagg")] = hagg
+
+        def l2_T(g):
+            hT = pz.tile([P, 4, P], F32, tag="z", name="hT")
             for t in range(4):
-                nc.tensor.transpose(hT[:, t, :], hagg[:, t * P : (t + 1) * P], ident_f[:])
-            hg = tail.tile([P, P, 4], BF16, align_bytes=64)
-            nc.scalar.copy(out=hg[:], in_=hT[:].rearrange("p t c -> p c t"))
-            ha_c = tail.tile([P, P], U32, align_bytes=64)
-            ha_s = tail.tile([P, P], U8, align_bytes=64)
-            nc.vector.quantize_mx(
-                out=ha_c[:].bitcast(FP8X4), scales=ha_s[:], in_=hg[:].rearrange("p c t -> p (c t)")
-            )
-            z2 = pz.tile([P, D_OUT], F32, tag="z")
+                nc.tensor.transpose(hT[:, t, :], s2[(g, "hagg")][:, t * P : (t + 1) * P], ident_f[:])
+            s2[(g, "hT")] = hT
+
+        def l2_copy(g):
+            hg = tail.tile([P, P, 4], BF16, align_bytes=64, name="hg")
+            nc.scalar.copy(out=hg[:], in_=s2[(g, "hT")][:].rearrange("p t c -> p c t"))
+            s2[(g, "hg")] = hg
+
+        def l2_quant(g):
+            ha_c = tail.tile([P, P], U32, align_bytes=64, name="ha_c")
+            ha_s = tail.tile([P, P], U8, align_bytes=64, name="ha_s")
+            quantise(s2[(g, "hg")], ha_c[:], ha_s[:])
+            s2[(g, "ha")] = (ha_c, ha_s)
+
+        def l2_mx(g):
+            ha_c, ha_s = s2[(g, "ha")]
+            z2 = pz.tile([P, D_OUT], F32, tag="z", name="z2")
             cols = slice(g * P, (g + 1) * P)
             nc.tensor.matmul_mx(
                 out=z2[:], lhsT=hn_c[:, cols].bitcast(FP8X4), lhsT_scale=hn_s[:, cols],
@@ -175,85 +368,120 @@ def tile_pinsageconv_t_kernel(tc, h_node, h_ngbrs, alpha, Wq, bq, Ww, bw, out):
                 out=z2[:], lhsT=ha_c[:].bitcast(FP8X4), lhsT_scale=ha_s[:],
                 rhs=w1_c[:].bitcast(FP8X4), rhs_scale=w1_s[:], start=False, stop=True,
             )
-            v2 = tail.tile([P, D_OUT], F32)
-            nc.vector.tensor_tensor(out=v2[:], in0=z2[:], in1=bw_bc[:], op=ALU.add)
-            h2 = tail.tile([P, D_OUT], F32)
+            s2[(g, "z2")] = z2
+
+        def l2_bias(g):
+            v2 = tail.tile([P, D_OUT], F32, name="v2")
+            nc.vector.tensor_tensor(out=v2[:], in0=s2[(g, "z2")][:], in1=bw_bc[:], op=ALU.add)
+            s2[(g, "v2")] = v2
+
+        def l2_lrelu(g):
+            h2 = tail.tile([P, D_OUT], F32, name="h2")
+            v2 = s2[(g, "v2")]
             nc.vector.scalar_tensor_tensor(
                 out=h2[:], in0=v2[:], scalar=SLOPE, in1=v2[:], op0=ALU.mult, op1=ALU.max
             )
-            sq = tail.tile([P, D_OUT], F32)
-            ss = tail.tile([P, 1], F32)
-            nc.scalar.activation(out=sq[:], in_=h2[:], func=ACT.Square, accum_out=ss[:])
-            nrm = tail.tile([P, 1], F32)
+            s2[(g, "h2")] = h2
+
+        def l2_norm_s(g):
+            sq = tail.tile([P, D_OUT], F32, name="sq")
+            ss = tail.tile([P, 1], F32, name="ss")
+            nc.scalar.activation(out=sq[:], in_=s2[(g, "h2")][:], func=ACT.Square, accum_out=ss[:])
+            nrm = tail.tile([P, 1], F32, name="nrm")
             nc.scalar.sqrt(out=nrm[:], in_=ss[:])
-            den = tail.tile([P, 1], F32)
+            s2[(g, "nrm")] = nrm
+
+        def l2_norm_v(g):
+            nrm = s2[(g, "nrm")]
+            den = tail.tile([P, 1], F32, name="den")
             nc.vector.scalar_tensor_tensor(
                 out=den[:], in0=nrm[:], scalar=0.0, in1=nrm[:], op0=ALU.is_equal, op1=ALU.add
             )
-            rec = tail.tile([P, 1], F32)
+            rec = tail.tile([P, 1], F32, name="rec")
             nc.vector.reciprocal(out=rec[:], in_=den[:])
-            res = tail.tile([P, D_OUT], F32)
-            nc.vector.tensor_scalar(out=res[:], in0=h2[:], scalar1=rec[:, 0:1], scalar2=None, op0=ALU.mult)
-            nc.sync.dma_start(out=out[g * P : (g + 1) * P, :], in_=res[:])
+            s2[(g, "rec")] = rec
 
-        for g in range(GROUPS):
-            acc = const.tile([P, D_HID], F32, name="acc%d" % g)
-            accp = pacc.tile([P, D_HID], F32)
-            for q in range(QUADS):
-                x_sb = xin.tile([P, KQ, D_IN], BF16)
-                nc.sync.dma_start(
-                    out=x_sb[:], in_=h_ngbrs[g * P : (g + 1) * P, q * KQ : (q + 1) * KQ, :]
+        def l2_res(g):
+            res = tail.tile([P, D_OUT], F32, name="res")
+            if RES_ON_SCALAR and g < GROUPS - 1:
+                nc.scalar.activation(
+                    out=res[:], in_=s2[(g, "h2")][:], func=ACT.Copy, scale=s2[(g, "rec")][:, 0:1]
                 )
-                x_c = qnt.tile([P, KQ * P], U32, align_bytes=64)
-                x_s = qnt.tile([P, KQ * P], U8, align_bytes=64)
-                words_to_mx(x_sb[:].bitcast(F32), x_c[:], x_s[:])
-                e_tiles = []
-                for hc in range(HC):
-                    cols = slice(hc * P, (hc + 1) * P)
-                    z = pz.tile([P, KQ * P], F32, tag="z")
-                    nc.tensor.matmul_mx(
-                        out=z[:], lhsT=wq_c[:, cols].bitcast(FP8X4), lhsT_scale=wq_s[:, cols],
-                        rhs=x_c[:].bitcast(FP8X4), rhs_scale=x_s[:], start=True, stop=True,
-                    )
-                    y = ypool.tile([P, KQ * P], F32)
-                    nc.scalar.activation(
-                        out=y[:], in_=z[:], func=ACT.Identity, bias=b_low[:, hc : hc + 1], scale=SLOPE
-                    )
-                    e = epool.tile([P, KQ * P], F32)
-                    nc.vector.scalar_tensor_tensor(
-                        out=e[:], in0=z[:], scalar=b_col[:, hc : hc + 1], in1=y[:], op0=ALU.add, op1=ALU.max
-                    )
-                    e_tiles.append(e)
-                    ea = eapool.tile([P, KG * P], F32)
-                    nc.gpsimd.tensor_tensor(
-                        out=ea[:].rearrange("p (k n) -> p k n", k=KG),
-                        in0=e[:, 0 : KG * P].rearrange("p (k n) -> p k n", k=KG),
-                        in1=a_bc[:, g * P : (g + 1) * P, q * KQ : q * KQ + KG].rearrange("p n k -> p k n"),
-                        op=ALU.mult,
-                    )
-                    for kk in range(KG):
-                        nc.tensor.matmul(
-                            out=accp[:, hc * P : (hc + 1) * P], lhsT=ea[:, kk * P : (kk + 1) * P], rhs=ident_f[:],
-                            is_transpose=True,
-                            start=(q == 0 and hc == 0 and kk == 0),
-                            stop=(q == QUADS - 1 and hc == HC - 1 and kk == KG - 1),
-                        )
-                for kk in range(KG, KQ):
-                    eT = pe.tile([P, D_HID], F32)
-                    for hc in range(HC):
-                        nc.tensor.transpose(
-                            eT[:, hc * P : (hc + 1) * P], e_tiles[hc][:, kk * P : (kk + 1) * P], ident_f[:]
-                        )
-                    k = q * KQ + kk
-                    if k == KG:
-                        nc.vector.tensor_scalar(
-                            out=acc[:], in0=eT[:], scalar1=a_n[:, g, k : k + 1], scalar2=None, op0=ALU.mult
-                        )
-                    else:
-                        nc.vector.scalar_tensor_tensor(
-                            out=acc[:], in0=eT[:], scalar=a_n[:, g, k : k + 1], in1=acc[:],
-                            op0=ALU.mult, op1=ALU.add,
-                        )
-                if g == 0 and q == 1:
-                    prepare_second_layer()
-            second_layer(g, acc, accp)
+            else:
+                nc.vector.tensor_scalar(
+                    out=res[:], in0=s2[(g, "h2")][:], scalar1=s2[(g, "rec")][:, 0:1], scalar2=None, op0=ALU.mult
+                )
+            s2[(g, "res")] = res
+
+        def l2_store(g):
+            nc.sync.dma_start(out=out[g * P : (g + 1) * P, :], in_=s2[(g, "res")][:])
+
+        def l2_due(j, lag):
+            g, r = divmod(j - lag, NSTEP // GROUPS)
+            if r == 0 and 1 <= g <= GROUPS:
+                return g - 1
+            return None
+
+        for j in range(-4, NSTEP + 12):
+            if j % 2 == 0 and 4 <= j // 2 + 6 < NQ:
+                load(j // 2 + 6)
+            late_loads(j)
+            g = l2_due(j, 11)
+            if g is not None:
+                l2_store(g)
+            if 0 <= j + 3 < 2 * NQ:
+                x_copy(j + 3)
+            if 0 <= j - PREP0 - 1 < 8:
+                prep_copy(j - PREP0 - 1)
+            g = l2_due(j, 4)
+            if g is not None:
+                l2_copy(g)
+            g = l2_due(j, 6)
+            if g is not None:
+                l2_mx(g)
+            if 0 <= j < NSTEP:
+                mx(2 * j)
+                mx(2 * j + 1)
+                ylow(2 * j)
+                ylow(2 * j + 1)
+                emax(2 * j)
+                gmul(2 * j)
+                emax(2 * j + 1)
+                gmul(2 * j + 1)
+            if 0 <= j - 2 < NSTEP:
+                tacc(2 * (j - 2))
+                tacc(2 * (j - 2) + 1)
+            if j % 2 == 0 and 0 <= (j - 2) // 2 < NQ:
+                tk((j - 2) // 2)
+            g = l2_due(j, 3)
+            if g is not None:
+                l2_T(g)
+            if 0 <= j - PREP0 < 8:
+                prep_T(j - PREP0)
+            if 0 <= j + 4 < 2 * NQ:
+                x_T(j + 4)
+            if j % 2 == 0 and 0 <= j // 2 + 1 < NQ:
+                x_quant(j // 2 + 1)
+            if j % 2 == 1 and 0 <= (j - 3) // 2 < NQ:
+                fma((j - 3) // 2)
+            if 0 <= j - PREP0 - 2 < 8:
+                prep_quant(j - PREP0 - 2)
+            g = l2_due(j, 2)
+            if g is not None:
+                l2_hagg(g)
+            g = l2_due(j, 5)
+            if g is not None:
+                l2_quant(g)
+            g = l2_due(j, 6)
+            if g is not None:
+                l2_bias(g)
+            g = l2_due(j, 7)
+            if g is not None:
+                l2_lrelu(g)
+            g = l2_due(j, 8)
+            if g is not None:
+                l2_norm_s(g)
+                l2_norm_v(g)
+            g = l2_due(j, 9)
+            if g is not None:
+                l2_res(g)

@@ -22,7 +22,7 @@ NQ = GROUPS * QUADS
 HC = D_HID // P
 NT = NQ * HC
 NSTEP = NT // 2
-KG_PATTERN = (3,)
+ROUTES = "FSFFSFSF"
 MANUAL = True
 RES_ON_SCALAR = True
 PREP0 = 6
@@ -30,8 +30,8 @@ PREP0 = 6
 FLOPS = 2 * N_NODES * K_NGB * D_IN * D_HID + 2 * N_NODES * (D_IN + D_HID) * D_OUT
 
 
-def kg_of(qd):
-    return KG_PATTERN[qd % len(KG_PATTERN)]
+def route_of(t):
+    return ROUTES[t % len(ROUTES)]
 
 
 def tile_pinsageconv_t_kernel(tc, h_node, h_ngbrs, alpha, Wq, bq, Ww, bw, out):
@@ -42,13 +42,12 @@ def tile_pinsageconv_t_kernel(tc, h_node, h_ngbrs, alpha, Wq, bq, Ww, bw, out):
         grp = ctx.enter_context(tc.tile_pool(name="grp", bufs=3))
         qnt = ctx.enter_context(tc.tile_pool(name="qnt", bufs=3))
         ypool = ctx.enter_context(tc.tile_pool(name="ypool", bufs=3))
-        epool = ctx.enter_context(tc.tile_pool(name="epool", bufs=10))
-        eapool = ctx.enter_context(tc.tile_pool(name="eapool", bufs=8))
+        epool = ctx.enter_context(tc.tile_pool(name="epool", bufs=12))
+        lpool = ctx.enter_context(tc.tile_pool(name="lpool", bufs=6))
         tail = ctx.enter_context(tc.tile_pool(name="tail", bufs=2))
         pxt = ctx.enter_context(tc.psum_pool(name="pxt", bufs=1))
         pz = ctx.enter_context(tc.psum_pool(name="pz", bufs=3))
-        pe = ctx.enter_context(tc.psum_pool(name="pe", bufs=2))
-        pacc = ctx.enter_context(tc.psum_pool(name="pacc", bufs=2))
+        pe = ctx.enter_context(tc.psum_pool(name="pe", bufs=4))
         if MANUAL:
             ctx.enter_context(tc.manual_schedule())
 
@@ -69,18 +68,8 @@ def tile_pinsageconv_t_kernel(tc, h_node, h_ngbrs, alpha, Wq, bq, Ww, bw, out):
                 out=x_sb[qd][:], in_=h_ngbrs[g * P : (g + 1) * P, q * KQ : (q + 1) * KQ, :]
             )
 
-        a_bc = const.tile([P, N_NODES, K_NGB], BF16)
-        a_flat = alpha.rearrange("(g n) k o -> g (n k o)", g=GROUPS)
-
-        def load_a_bc(g):
-            nc.sync.dma_start(
-                out=a_bc[:, g * P : (g + 1) * P, :].rearrange("p n k -> p (n k)"),
-                in_=a_flat[g].partition_broadcast(P),
-            )
-
         load(0)
         load(1)
-        load_a_bc(0)
         load(2)
         load(3)
 
@@ -104,8 +93,6 @@ def tile_pinsageconv_t_kernel(tc, h_node, h_ngbrs, alpha, Wq, bq, Ww, bw, out):
             elif j == 2:
                 nc.sync.dma_start(out=hn_raw[:], in_=h_node.rearrange("(g p) i -> p g i", p=P))
                 nc.sync.dma_start(out=bw_bc[:], in_=bw.partition_broadcast(P))
-            elif j in (4, 8, 12):
-                load_a_bc(j // 4)
 
         def words_T(src_words, half, pool, tag):
             xt = pool.tile([P, 2, 2, P], F32, tag=tag, name="xt")
@@ -144,6 +131,10 @@ def tile_pinsageconv_t_kernel(tc, h_node, h_ngbrs, alpha, Wq, bq, Ww, bw, out):
         nc.vector.tensor_copy(out=b_col[:], in_=bT[:, 0:HC])
         b_low = const.tile([P, HC], F32)
         nc.vector.tensor_scalar(out=b_low[:], in0=b_col[:], scalar1=SLOPE, scalar2=None, op0=ALU.mult)
+        b_high = const.tile([P, HC], F32)
+        nc.vector.tensor_scalar(
+            out=b_high[:], in0=b_col[:], scalar1=1.0 - SLOPE, scalar2=None, op0=ALU.mult
+        )
         quantise(wq_g, wq_c[:], wq_s[:])
 
         a_f = const.tile([P, GROUPS, K_NGB], F32)
@@ -212,10 +203,9 @@ def tile_pinsageconv_t_kernel(tc, h_node, h_ngbrs, alpha, Wq, bq, Ww, bw, out):
         z_ps = {}
         y_sb = {}
         e_sb = {}
-        ea_sb = {}
+        l_sb = {}
         eT_ps = {}
         acc = {}
-        accp = {}
 
         def x_T(xh):
             qd, half = divmod(xh, 2)
@@ -244,105 +234,67 @@ def tile_pinsageconv_t_kernel(tc, h_node, h_ngbrs, alpha, Wq, bq, Ww, bw, out):
                 rhs=x_c[qd][:].bitcast(FP8X4), rhs_scale=x_s[qd][:], start=True, stop=True,
             )
 
-        def ylow(t):
+        def scalar_part(t):
             hc = t % HC
-            y_sb[t] = ypool.tile([P, KQ * P], F32, name="y")
-            nc.scalar.activation(
-                out=y_sb[t][:], in_=z_ps[t][:], func=ACT.Identity, bias=b_low[:, hc : hc + 1], scale=SLOPE
-            )
-
-        def emax(t):
-            hc = t % HC
-            e_sb[t] = epool.tile([P, KQ * P], F32, name="e")
-            nc.vector.scalar_tensor_tensor(
-                out=e_sb[t][:], in0=z_ps[t][:], scalar=b_col[:, hc : hc + 1], in1=y_sb[t][:],
-                op0=ALU.add, op1=ALU.max,
-            )
-
-        def gmul(t):
-            qd = t // HC
-            g, q = divmod(qd, QUADS)
-            kg = kg_of(qd)
-            if kg == 0:
-                return
-            ea_sb[t] = eapool.tile([P, kg * P], F32, tag="ea", name="ea")
-            nc.gpsimd.tensor_tensor(
-                out=ea_sb[t][:].rearrange("p (k n) -> p k n", k=kg),
-                in0=e_sb[t][:, 0 : kg * P].rearrange("p (k n) -> p k n", k=kg),
-                in1=a_bc[:, g * P : (g + 1) * P, q * KQ : q * KQ + kg].rearrange("p n k -> p k n"),
-                op=ALU.mult,
-            )
-
-        first_acc = {}
-        last_acc = {}
-        for g in range(GROUPS):
-            with_g = [qd for qd in range(g * QUADS, (g + 1) * QUADS) if kg_of(qd) > 0]
-            if with_g:
-                first_acc[g] = with_g[0] * HC
-                last_acc[g] = with_g[-1] * HC + HC - 1
-
-        def tacc(t):
-            qd, hc = divmod(t, HC)
-            g = qd // QUADS
-            kg = kg_of(qd)
-            if kg == 0:
-                return
-            if t == first_acc[g]:
-                accp[g] = pacc.tile([P, D_HID], F32, name="accp")
-            for kk in range(kg):
-                nc.tensor.matmul(
-                    out=accp[g][:, hc * P : (hc + 1) * P], lhsT=ea_sb[t][:, kk * P : (kk + 1) * P],
-                    rhs=ident_f[:], is_transpose=True,
-                    start=(t == first_acc[g] and kk == 0), stop=(t == last_acc[g] and kk == kg - 1),
-                )
-
-        def tk(qd):
-            for kk in range(kg_of(qd), KQ):
-                eT_ps[(qd, kk)] = pe.tile([P, D_HID], F32, tag="eT", name="eT")
-                for hc in range(HC):
-                    nc.tensor.transpose(
-                        eT_ps[(qd, kk)][:, hc * P : (hc + 1) * P],
-                        e_sb[qd * HC + hc][:, kk * P : (kk + 1) * P], ident_f[:],
-                    )
-
-        def fma(qd):
-            g, q = divmod(qd, QUADS)
-            for kk in range(kg_of(qd), KQ):
-                k = q * KQ + kk
-                if g not in acc:
-                    acc[g] = const.tile([P, D_HID], F32, name="acc%d" % g)
-                    nc.vector.tensor_scalar(
-                        out=acc[g][:], in0=eT_ps[(qd, kk)][:], scalar1=a_n[:, g, k : k + 1], scalar2=None,
-                        op0=ALU.mult,
-                    )
-                else:
-                    nc.vector.scalar_tensor_tensor(
-                        out=acc[g][:], in0=eT_ps[(qd, kk)][:], scalar=a_n[:, g, k : k + 1], in1=acc[g][:],
-                        op0=ALU.mult, op1=ALU.add,
-                    )
-
-        s2 = {}
-
-        def l2_hagg(g):
-            if g in accp and g in acc:
-                hagg = tail.tile([P, D_HID], F32, name="hagg")
-                nc.vector.scalar_tensor_tensor(
-                    out=hagg[:], in0=accp[g][:], scalar=a_rec[:, g : g + 1], in1=acc[g][:],
-                    op0=ALU.mult, op1=ALU.add,
-                )
-            elif g in accp:
-                hagg = tail.tile([P, D_HID], F32, name="hagg")
-                nc.vector.tensor_scalar(
-                    out=hagg[:], in0=accp[g][:], scalar1=a_rec[:, g : g + 1], scalar2=None, op0=ALU.mult
+            if route_of(t) == "F":
+                y_sb[t] = ypool.tile([P, KQ * P], F32, name="y")
+                nc.scalar.activation(
+                    out=y_sb[t][:], in_=z_ps[t][:], func=ACT.Identity, bias=b_low[:, hc : hc + 1], scale=SLOPE
                 )
             else:
-                hagg = acc[g]
-            s2[(g, "hagg")] = hagg
+                e_sb[t] = epool.tile([P, KQ * P], F32, name="e")
+                nc.scalar.activation(
+                    out=e_sb[t][:], in_=z_ps[t][:], func=ACT.Relu, bias=b_high[:, hc : hc + 1], scale=1.0 - SLOPE
+                )
+                l_sb[t] = lpool.tile([P, KQ * P], F32, name="l")
+                nc.scalar.activation(
+                    out=l_sb[t][:], in_=z_ps[t][:], func=ACT.Identity, bias=b_low[:, hc : hc + 1], scale=SLOPE
+                )
+
+        def vector_part(t):
+            hc = t % HC
+            if route_of(t) == "F":
+                e_sb[t] = epool.tile([P, KQ * P], F32, name="e")
+                nc.vector.scalar_tensor_tensor(
+                    out=e_sb[t][:], in0=z_ps[t][:], scalar=b_col[:, hc : hc + 1], in1=y_sb[t][:],
+                    op0=ALU.add, op1=ALU.max,
+                )
+
+        def tk(qd, kk):
+            eT_ps[(qd, kk)] = pe.tile([P, D_HID], F32, tag="eT", name="eT")
+            parts = []
+            for hc in range(HC):
+                t = qd * HC + hc
+                parts.append((hc, e_sb[t]))
+                if route_of(t) == "S":
+                    parts.append((hc, l_sb[t]))
+            for i, (hc, src) in enumerate(parts):
+                nc.tensor.matmul(
+                    out=eT_ps[(qd, kk)][:, hc * P : (hc + 1) * P], lhsT=src[:, kk * P : (kk + 1) * P],
+                    rhs=ident_f[:], is_transpose=True, start=(i == 0), stop=(i == len(parts) - 1),
+                )
+
+        def fma(qd, kk):
+            g, q = divmod(qd, QUADS)
+            k = q * KQ + kk
+            if k == 0:
+                acc[g] = const.tile([P, D_HID], F32, name="acc%d" % g)
+                nc.vector.tensor_scalar(
+                    out=acc[g][:], in0=eT_ps[(qd, kk)][:], scalar1=a_n[:, g, k : k + 1], scalar2=None,
+                    op0=ALU.mult,
+                )
+            else:
+                nc.vector.scalar_tensor_tensor(
+                    out=acc[g][:], in0=eT_ps[(qd, kk)][:], scalar=a_n[:, g, k : k + 1], in1=acc[g][:],
+                    op0=ALU.mult, op1=ALU.add,
+                )
+
+        s2 = {}
 
         def l2_T(g):
             hT = pz.tile([P, 4, P], F32, tag="z", name="hT")
             for t in range(4):
-                nc.tensor.transpose(hT[:, t, :], s2[(g, "hagg")][:, t * P : (t + 1) * P], ident_f[:])
+                nc.tensor.transpose(hT[:, t, :], acc[g][:, t * P : (t + 1) * P], ident_f[:])
             s2[(g, "hT")] = hT
 
         def l2_copy(g):
@@ -442,17 +394,18 @@ def tile_pinsageconv_t_kernel(tc, h_node, h_ngbrs, alpha, Wq, bq, Ww, bw, out):
             if 0 <= j < NSTEP:
                 mx(2 * j)
                 mx(2 * j + 1)
-                ylow(2 * j)
-                ylow(2 * j + 1)
-                emax(2 * j)
-                gmul(2 * j)
-                emax(2 * j + 1)
-                gmul(2 * j + 1)
-            if 0 <= j - 2 < NSTEP:
-                tacc(2 * (j - 2))
-                tacc(2 * (j - 2) + 1)
-            if j % 2 == 0 and 0 <= (j - 2) // 2 < NQ:
-                tk((j - 2) // 2)
+                scalar_part(2 * j)
+                scalar_part(2 * j + 1)
+            qd_f, pair_f = divmod(j - 3, 2)
+            for i in range(2):
+                if 0 <= j < NSTEP:
+                    vector_part(2 * j + i)
+                if 0 <= qd_f < NQ:
+                    fma(qd_f, 2 * pair_f + i)
+            qd_t, pair_t = divmod(j - 2, 2)
+            if 0 <= qd_t < NQ:
+                tk(qd_t, 2 * pair_t)
+                tk(qd_t, 2 * pair_t + 1)
             g = l2_due(j, 3)
             if g is not None:
                 l2_T(g)
@@ -462,13 +415,8 @@ def tile_pinsageconv_t_kernel(tc, h_node, h_ngbrs, alpha, Wq, bq, Ww, bw, out):
                 x_T(j + 4)
             if j % 2 == 0 and 0 <= j // 2 + 1 < NQ:
                 x_quant(j // 2 + 1)
-            if j % 2 == 1 and 0 <= (j - 3) // 2 < NQ:
-                fma((j - 3) // 2)
             if 0 <= j - PREP0 - 2 < 8:
                 prep_quant(j - PREP0 - 2)
-            g = l2_due(j, 2)
-            if g is not None:
-                l2_hagg(g)
             g = l2_due(j, 5)
             if g is not None:
                 l2_quant(g)

@@ -26,6 +26,7 @@ ROUTES = "FSFFSFSF"
 MANUAL = True
 RES_ON_SCALAR = True
 PREP0 = 6
+LAG_T = 2
 
 FLOPS = 2 * N_NODES * K_NGB * D_IN * D_HID + 2 * N_NODES * (D_IN + D_HID) * D_OUT
 
@@ -378,17 +379,17 @@ def tile_pinsageconv_t_kernel(tc, h_node, h_ngbrs, alpha, Wq, bq, Ww, bw, out):
             if j % 2 == 0 and 4 <= j // 2 + 6 < NQ:
                 load(j // 2 + 6)
             late_loads(j)
-            g = l2_due(j, 11)
+            g = l2_due(j, LAG_T + 8)
             if g is not None:
                 l2_store(g)
             if 0 <= j + 3 < 2 * NQ:
                 x_copy(j + 3)
             if 0 <= j - PREP0 - 1 < 8:
                 prep_copy(j - PREP0 - 1)
-            g = l2_due(j, 4)
+            g = l2_due(j, LAG_T + 1)
             if g is not None:
                 l2_copy(g)
-            g = l2_due(j, 6)
+            g = l2_due(j, LAG_T + 3)
             if g is not None:
                 l2_mx(g)
             if 0 <= j < NSTEP:
@@ -396,40 +397,39 @@ def tile_pinsageconv_t_kernel(tc, h_node, h_ngbrs, alpha, Wq, bq, Ww, bw, out):
                 mx(2 * j + 1)
                 scalar_part(2 * j)
                 scalar_part(2 * j + 1)
-            qd_f, pair_f = divmod(j - 3, 2)
-            for i in range(2):
-                if 0 <= j < NSTEP:
-                    vector_part(2 * j + i)
-                if 0 <= qd_f < NQ:
-                    fma(qd_f, 2 * pair_f + i)
-            qd_t, pair_t = divmod(j - 2, 2)
+            qd_t, pair_t = divmod(j - LAG_T, 2)
             if 0 <= qd_t < NQ:
                 tk(qd_t, 2 * pair_t)
                 tk(qd_t, 2 * pair_t + 1)
-            g = l2_due(j, 3)
+            g = l2_due(j, LAG_T)
             if g is not None:
                 l2_T(g)
             if 0 <= j - PREP0 < 8:
                 prep_T(j - PREP0)
             if 0 <= j + 4 < 2 * NQ:
                 x_T(j + 4)
+            for i in range(2):
+                if 0 <= j < NSTEP:
+                    vector_part(2 * j + i)
+                if 0 <= qd_t < NQ:
+                    fma(qd_t, 2 * pair_t + i)
             if j % 2 == 0 and 0 <= j // 2 + 1 < NQ:
                 x_quant(j // 2 + 1)
             if 0 <= j - PREP0 - 2 < 8:
                 prep_quant(j - PREP0 - 2)
-            g = l2_due(j, 5)
+            g = l2_due(j, LAG_T + 2)
             if g is not None:
                 l2_quant(g)
-            g = l2_due(j, 6)
+            g = l2_due(j, LAG_T + 3)
             if g is not None:
                 l2_bias(g)
-            g = l2_due(j, 7)
+            g = l2_due(j, LAG_T + 4)
             if g is not None:
                 l2_lrelu(g)
-            g = l2_due(j, 8)
+            g = l2_due(j, LAG_T + 5)
             if g is not None:
                 l2_norm_s(g)
                 l2_norm_v(g)
-            g = l2_due(j, 9)
+            g = l2_due(j, LAG_T + 6)
             if g is not None:
                 l2_res(g)

@@ -26,7 +26,8 @@ ROUTES = "FSFFSFSF"
 MANUAL = True
 RES_ON_SCALAR = True
 PREP0 = 6
-LAG_T = 2
+L2_LAG = (5, 6, 7, 10, 11, 12, 13, 0, 15)
+LAG_T = 3
 
 FLOPS = 2 * N_NODES * K_NGB * D_IN * D_HID + 2 * N_NODES * (D_IN + D_HID) * D_OUT
 
@@ -43,8 +44,8 @@ def tile_pinsageconv_t_kernel(tc, h_node, h_ngbrs, alpha, Wq, bq, Ww, bw, out):
         grp = ctx.enter_context(tc.tile_pool(name="grp", bufs=3))
         qnt = ctx.enter_context(tc.tile_pool(name="qnt", bufs=3))
         ypool = ctx.enter_context(tc.tile_pool(name="ypool", bufs=3))
-        epool = ctx.enter_context(tc.tile_pool(name="epool", bufs=12))
-        lpool = ctx.enter_context(tc.tile_pool(name="lpool", bufs=6))
+        epool = ctx.enter_context(tc.tile_pool(name="epool", bufs=14))
+        lpool = ctx.enter_context(tc.tile_pool(name="lpool", bufs=3))
         tail = ctx.enter_context(tc.tile_pool(name="tail", bufs=2))
         pxt = ctx.enter_context(tc.psum_pool(name="pxt", bufs=1))
         pz = ctx.enter_context(tc.psum_pool(name="pz", bufs=3))
@@ -166,12 +167,12 @@ def tile_pinsageconv_t_kernel(tc, h_node, h_ngbrs, alpha, Wq, bq, Ww, bw, out):
             if i % 4 == 0 or i == 2:
                 prep_g[i] = const.tile([P, 4 * P, 4], BF16, align_bytes=64, name="prep_g%d" % i)
             if i < 2:
-                prep_ps[i] = words_T(ww_raw[:].bitcast(F32)[:, :, 0 : D_IN // 2], i, pz, "z")
+                prep_ps[i] = words_T(ww_raw[:].bitcast(F32)[:, :, 0 : D_IN // 2], i, pe, "eT")
             elif i < 4:
-                prep_ps[i] = words_T(hn_raw[:].bitcast(F32), i - 2, pz, "z")
+                prep_ps[i] = words_T(hn_raw[:].bitcast(F32), i - 2, pe, "eT")
             else:
                 ob = i - 4
-                wt = pz.tile([P, 4, P], BF16, tag="z", name="wt")
+                wt = pe.tile([P, 4, P], BF16, tag="eT", name="wt")
                 for t in range(4):
                     nc.tensor.transpose(
                         wt[:, t, :], ww_raw[:, ob, D_IN + t * P : D_IN + (t + 1) * P], ident_b[:]
@@ -204,7 +205,6 @@ def tile_pinsageconv_t_kernel(tc, h_node, h_ngbrs, alpha, Wq, bq, Ww, bw, out):
         z_ps = {}
         y_sb = {}
         e_sb = {}
-        l_sb = {}
         eT_ps = {}
         acc = {}
 
@@ -243,14 +243,16 @@ def tile_pinsageconv_t_kernel(tc, h_node, h_ngbrs, alpha, Wq, bq, Ww, bw, out):
                     out=y_sb[t][:], in_=z_ps[t][:], func=ACT.Identity, bias=b_low[:, hc : hc + 1], scale=SLOPE
                 )
             else:
+                r_sb = lpool.tile([P, KQ * P], F32, name="r")
+                nc.scalar.activation(
+                    out=r_sb[:], in_=z_ps[t][:], func=ACT.Relu, bias=b_high[:, hc : hc + 1], scale=1.0 - SLOPE
+                )
+                l_sb = lpool.tile([P, KQ * P], F32, name="l")
+                nc.scalar.activation(
+                    out=l_sb[:], in_=z_ps[t][:], func=ACT.Identity, bias=b_low[:, hc : hc + 1], scale=SLOPE
+                )
                 e_sb[t] = epool.tile([P, KQ * P], F32, name="e")
-                nc.scalar.activation(
-                    out=e_sb[t][:], in_=z_ps[t][:], func=ACT.Relu, bias=b_high[:, hc : hc + 1], scale=1.0 - SLOPE
-                )
-                l_sb[t] = lpool.tile([P, KQ * P], F32, name="l")
-                nc.scalar.activation(
-                    out=l_sb[t][:], in_=z_ps[t][:], func=ACT.Identity, bias=b_low[:, hc : hc + 1], scale=SLOPE
-                )
+                nc.gpsimd.tensor_tensor(out=e_sb[t][:], in0=r_sb[:], in1=l_sb[:], op=ALU.add)
 
         def vector_part(t):
             hc = t % HC
@@ -267,8 +269,6 @@ def tile_pinsageconv_t_kernel(tc, h_node, h_ngbrs, alpha, Wq, bq, Ww, bw, out):
             for hc in range(HC):
                 t = qd * HC + hc
                 parts.append((hc, e_sb[t]))
-                if route_of(t) == "S":
-                    parts.append((hc, l_sb[t]))
             for i, (hc, src) in enumerate(parts):
                 nc.tensor.matmul(
                     out=eT_ps[(qd, kk)][:, hc * P : (hc + 1) * P], lhsT=src[:, kk * P : (kk + 1) * P],
@@ -293,7 +293,7 @@ def tile_pinsageconv_t_kernel(tc, h_node, h_ngbrs, alpha, Wq, bq, Ww, bw, out):
         s2 = {}
 
         def l2_T(g):
-            hT = pz.tile([P, 4, P], F32, tag="z", name="hT")
+            hT = pe.tile([P, 4, P], F32, tag="eT", name="hT")
             for t in range(4):
                 nc.tensor.transpose(hT[:, t, :], acc[g][:, t * P : (t + 1) * P], ident_f[:])
             s2[(g, "hT")] = hT
@@ -375,21 +375,21 @@ def tile_pinsageconv_t_kernel(tc, h_node, h_ngbrs, alpha, Wq, bq, Ww, bw, out):
                 return g - 1
             return None
 
-        for j in range(-4, NSTEP + 12):
+        for j in range(-4, NSTEP + L2_LAG[8] + 1):
             if j % 2 == 0 and 4 <= j // 2 + 6 < NQ:
                 load(j // 2 + 6)
             late_loads(j)
-            g = l2_due(j, LAG_T + 8)
+            g = l2_due(j, L2_LAG[8])
             if g is not None:
                 l2_store(g)
             if 0 <= j + 3 < 2 * NQ:
                 x_copy(j + 3)
             if 0 <= j - PREP0 - 1 < 8:
                 prep_copy(j - PREP0 - 1)
-            g = l2_due(j, LAG_T + 1)
+            g = l2_due(j, L2_LAG[1])
             if g is not None:
                 l2_copy(g)
-            g = l2_due(j, LAG_T + 3)
+            g = l2_due(j, L2_LAG[3])
             if g is not None:
                 l2_mx(g)
             if 0 <= j < NSTEP:
@@ -401,7 +401,7 @@ def tile_pinsageconv_t_kernel(tc, h_node, h_ngbrs, alpha, Wq, bq, Ww, bw, out):
             if 0 <= qd_t < NQ:
                 tk(qd_t, 2 * pair_t)
                 tk(qd_t, 2 * pair_t + 1)
-            g = l2_due(j, LAG_T)
+            g = l2_due(j, L2_LAG[0])
             if g is not None:
                 l2_T(g)
             if 0 <= j - PREP0 < 8:
@@ -417,19 +417,19 @@ def tile_pinsageconv_t_kernel(tc, h_node, h_ngbrs, alpha, Wq, bq, Ww, bw, out):
                 x_quant(j // 2 + 1)
             if 0 <= j - PREP0 - 2 < 8:
                 prep_quant(j - PREP0 - 2)
-            g = l2_due(j, LAG_T + 2)
+            g = l2_due(j, L2_LAG[2])
             if g is not None:
                 l2_quant(g)
-            g = l2_due(j, LAG_T + 3)
+            g = l2_due(j, L2_LAG[3])
             if g is not None:
                 l2_bias(g)
-            g = l2_due(j, LAG_T + 4)
+            g = l2_due(j, L2_LAG[4])
             if g is not None:
                 l2_lrelu(g)
-            g = l2_due(j, LAG_T + 5)
+            g = l2_due(j, L2_LAG[5])
             if g is not None:
                 l2_norm_s(g)
                 l2_norm_v(g)
-            g = l2_due(j, LAG_T + 6)
+            g = l2_due(j, L2_LAG[6])
             if g is not None:
                 l2_res(g)

@@ -33,6 +33,8 @@ FLOPS = 2 * N_NODES * K_NGB * D_IN * D_HID + 2 * N_NODES * (D_IN + D_HID) * D_OU
 
 
 def route_of(t):
+    if t >= NT - 8:
+        return "F"
     return ROUTES[t % len(ROUTES)]
 
 
@@ -40,15 +42,14 @@ def tile_pinsageconv_t_kernel(tc, h_node, h_ngbrs, alpha, Wq, bq, Ww, bw, out):
     nc = tc.nc
     with ExitStack() as ctx:
         const = ctx.enter_context(tc.tile_pool(name="const", bufs=1))
-        xin = ctx.enter_context(tc.tile_pool(name="xin", bufs=6))
-        grp = ctx.enter_context(tc.tile_pool(name="grp", bufs=3))
-        qnt = ctx.enter_context(tc.tile_pool(name="qnt", bufs=3))
+        xin = ctx.enter_context(tc.tile_pool(name="xin", bufs=7))
+        grp = ctx.enter_context(tc.tile_pool(name="grp", bufs=4))
+        qnt = ctx.enter_context(tc.tile_pool(name="qnt", bufs=5))
         ypool = ctx.enter_context(tc.tile_pool(name="ypool", bufs=3))
         epool = ctx.enter_context(tc.tile_pool(name="epool", bufs=14))
         lpool = ctx.enter_context(tc.tile_pool(name="lpool", bufs=3))
         tail = ctx.enter_context(tc.tile_pool(name="tail", bufs=2))
-        pxt = ctx.enter_context(tc.psum_pool(name="pxt", bufs=1))
-        pz = ctx.enter_context(tc.psum_pool(name="pz", bufs=3))
+        pz = ctx.enter_context(tc.psum_pool(name="pz", bufs=4))
         pe = ctx.enter_context(tc.psum_pool(name="pe", bufs=4))
         if MANUAL:
             ctx.enter_context(tc.manual_schedule())
@@ -212,10 +213,7 @@ def tile_pinsageconv_t_kernel(tc, h_node, h_ngbrs, alpha, Wq, bq, Ww, bw, out):
             qd, half = divmod(xh, 2)
             if half == 0:
                 grouped[qd] = grp.tile([P, 4 * P, 4], BF16, align_bytes=64, tag="grouped", name="grouped")
-            if xh < 2:
-                xt_ps[xh] = words_T(x_sb[qd][:].bitcast(F32), half, pe, "eT")
-            else:
-                xt_ps[xh] = words_T(x_sb[qd][:].bitcast(F32), half, pxt, "xt")
+            xt_ps[xh] = words_T(x_sb[qd][:].bitcast(F32), half, pe, "eT")
 
         def x_copy(xh):
             qd, half = divmod(xh, 2)
@@ -300,7 +298,10 @@ def tile_pinsageconv_t_kernel(tc, h_node, h_ngbrs, alpha, Wq, bq, Ww, bw, out):
 
         def l2_copy(g):
             hg = tail.tile([P, P, 4], BF16, align_bytes=64, name="hg")
-            nc.scalar.copy(out=hg[:], in_=s2[(g, "hT")][:].rearrange("p t c -> p c t"))
+            if g == GROUPS - 1:
+                nc.vector.tensor_copy(out=hg[:], in_=s2[(g, "hT")][:].rearrange("p t c -> p c t"))
+            else:
+                nc.scalar.copy(out=hg[:], in_=s2[(g, "hT")][:].rearrange("p t c -> p c t"))
             s2[(g, "hg")] = hg
 
         def l2_quant(g):
@@ -309,19 +310,22 @@ def tile_pinsageconv_t_kernel(tc, h_node, h_ngbrs, alpha, Wq, bq, Ww, bw, out):
             quantise(s2[(g, "hg")], ha_c[:], ha_s[:])
             s2[(g, "ha")] = (ha_c, ha_s)
 
-        def l2_mx(g):
-            ha_c, ha_s = s2[(g, "ha")]
+        def l2_mx0(g):
             z2 = pz.tile([P, D_OUT], F32, tag="z", name="z2")
             cols = slice(g * P, (g + 1) * P)
+            s2[(g, "z2")] = z2
             nc.tensor.matmul_mx(
                 out=z2[:], lhsT=hn_c[:, cols].bitcast(FP8X4), lhsT_scale=hn_s[:, cols],
                 rhs=w0_c[:].bitcast(FP8X4), rhs_scale=w0_s[:], start=True, stop=False,
             )
+
+        def l2_mx1(g):
+            ha_c, ha_s = s2[(g, "ha")]
+            z2 = s2[(g, "z2")]
             nc.tensor.matmul_mx(
                 out=z2[:], lhsT=ha_c[:].bitcast(FP8X4), lhsT_scale=ha_s[:],
                 rhs=w1_c[:].bitcast(FP8X4), rhs_scale=w1_s[:], start=False, stop=True,
             )
-            s2[(g, "z2")] = z2
 
         def l2_bias(g):
             v2 = tail.tile([P, D_OUT], F32, name="v2")
@@ -375,6 +379,21 @@ def tile_pinsageconv_t_kernel(tc, h_node, h_ngbrs, alpha, Wq, bq, Ww, bw, out):
                 return g - 1
             return None
 
+        xt_at = {}
+        xc_at = {}
+        xq_at = {}
+        for xh in range(2 * NQ):
+            if xh < 4:
+                jx = xh - 4
+            elif xh < 8:
+                jx = (xh - 4) // 2
+            else:
+                jx = xh - 6
+            xt_at[jx] = xt_at.get(jx, []) + [xh]
+            xc_at[jx + 1] = xc_at.get(jx + 1, []) + [xh]
+            if xh % 2 == 1:
+                xq_at[jx + 1] = xh // 2
+
         for j in range(-4, NSTEP + L2_LAG[8] + 1):
             if j % 2 == 0 and 4 <= j // 2 + 6 < NQ:
                 load(j // 2 + 6)
@@ -382,8 +401,8 @@ def tile_pinsageconv_t_kernel(tc, h_node, h_ngbrs, alpha, Wq, bq, Ww, bw, out):
             g = l2_due(j, L2_LAG[8])
             if g is not None:
                 l2_store(g)
-            if 0 <= j + 3 < 2 * NQ:
-                x_copy(j + 3)
+            for xh in xc_at.get(j, []):
+                x_copy(xh)
             if 0 <= j - PREP0 - 1 < 8:
                 prep_copy(j - PREP0 - 1)
             g = l2_due(j, L2_LAG[1])
@@ -391,30 +410,34 @@ def tile_pinsageconv_t_kernel(tc, h_node, h_ngbrs, alpha, Wq, bq, Ww, bw, out):
                 l2_copy(g)
             g = l2_due(j, L2_LAG[3])
             if g is not None:
-                l2_mx(g)
+                if g < GROUPS - 1:
+                    l2_mx0(g)
+                l2_mx1(g)
             if 0 <= j < NSTEP:
                 mx(2 * j)
                 mx(2 * j + 1)
                 scalar_part(2 * j)
                 scalar_part(2 * j + 1)
+            for xh in xt_at.get(j, []):
+                x_T(xh)
             qd_t, pair_t = divmod(j - LAG_T, 2)
             if 0 <= qd_t < NQ:
                 tk(qd_t, 2 * pair_t)
                 tk(qd_t, 2 * pair_t + 1)
             g = l2_due(j, L2_LAG[0])
             if g is not None:
+                if g == GROUPS - 1:
+                    l2_mx0(g)
                 l2_T(g)
             if 0 <= j - PREP0 < 8:
                 prep_T(j - PREP0)
-            if 0 <= j + 4 < 2 * NQ:
-                x_T(j + 4)
             for i in range(2):
                 if 0 <= j < NSTEP:
                     vector_part(2 * j + i)
                 if 0 <= qd_t < NQ:
                     fma(qd_t, 2 * pair_t + i)
-            if j % 2 == 0 and 0 <= j // 2 + 1 < NQ:
-                x_quant(j // 2 + 1)
+            if j in xq_at:
+                x_quant(xq_at[j])
             if 0 <= j - PREP0 - 2 < 8:
                 prep_quant(j - PREP0 - 2)
             g = l2_due(j, L2_LAG[2])

@@ -22,7 +22,7 @@ NQ = GROUPS * QUADS
 HC = D_HID // P
 NT = NQ * HC
 NSTEP = NT // 2
-ROUTES = "FSFFSFSF"
+ROUTES = "FS"
 MANUAL = True
 RES_ON_SCALAR = True
 PREP0 = 6
@@ -33,7 +33,7 @@ FLOPS = 2 * N_NODES * K_NGB * D_IN * D_HID + 2 * N_NODES * (D_IN + D_HID) * D_OU
 
 
 def route_of(t):
-    if t >= NT - 8:
+    if t >= NT - 2:
         return "F"
     return ROUTES[t % len(ROUTES)]
 
@@ -276,15 +276,16 @@ def tile_pinsageconv_t_kernel(tc, h_node, h_ngbrs, alpha, Wq, bq, Ww, bw, out):
         def fma(qd, kk):
             g, q = divmod(qd, QUADS)
             k = q * KQ + kk
-            if k == 0:
-                acc[g] = const.tile([P, D_HID], F32, name="acc%d" % g)
+            half = (g, k % 2)
+            if k < 2:
+                acc[half] = const.tile([P, D_HID], F32, name="acc%d_%d" % half)
                 nc.vector.tensor_scalar(
-                    out=acc[g][:], in0=eT_ps[(qd, kk)][:], scalar1=a_n[:, g, k : k + 1], scalar2=None,
+                    out=acc[half][:], in0=eT_ps[(qd, kk)][:], scalar1=a_n[:, g, k : k + 1], scalar2=None,
                     op0=ALU.mult,
                 )
             else:
                 nc.vector.scalar_tensor_tensor(
-                    out=acc[g][:], in0=eT_ps[(qd, kk)][:], scalar=a_n[:, g, k : k + 1], in1=acc[g][:],
+                    out=acc[half][:], in0=eT_ps[(qd, kk)][:], scalar=a_n[:, g, k : k + 1], in1=acc[half][:],
                     op0=ALU.mult, op1=ALU.add,
                 )
 
@@ -292,16 +293,17 @@ def tile_pinsageconv_t_kernel(tc, h_node, h_ngbrs, alpha, Wq, bq, Ww, bw, out):
 
         def l2_T(g):
             hT = pe.tile([P, 4, P], F32, tag="eT", name="hT")
-            for t in range(4):
-                nc.tensor.transpose(hT[:, t, :], acc[g][:, t * P : (t + 1) * P], ident_f[:])
+            for i in range(8):
+                t, par = divmod(i, 2)
+                nc.tensor.matmul(
+                    out=hT[:, t, :], lhsT=acc[(g, par)][:, t * P : (t + 1) * P], rhs=ident_f[:],
+                    is_transpose=True, start=(i == 0), stop=(i == 7),
+                )
             s2[(g, "hT")] = hT
 
         def l2_copy(g):
             hg = tail.tile([P, P, 4], BF16, align_bytes=64, name="hg")
-            if g == GROUPS - 1:
-                nc.vector.tensor_copy(out=hg[:], in_=s2[(g, "hT")][:].rearrange("p t c -> p c t"))
-            else:
-                nc.scalar.copy(out=hg[:], in_=s2[(g, "hT")][:].rearrange("p t c -> p c t"))
+            nc.scalar.copy(out=hg[:], in_=s2[(g, "hT")][:].rearrange("p t c -> p c t"))
             s2[(g, "hg")] = hg
 
         def l2_quant(g):

@@ -60,16 +60,22 @@ def tile_pinsageconv_t_kernel(tc, h_node, h_ngbrs, alpha, Wq, bq, Ww, bw, out):
         make_identity(nc, ident_b[:])
 
         wq_raw = const.tile([P, HC, D_IN], BF16)
-        nc.sync.dma_start(out=wq_raw[:], in_=Wq.rearrange("(b p) i -> p b i", p=P))
+        wq_view = Wq.rearrange("(b p) i -> p b i", p=P)
+        nc.sync.dma_start(out=wq_raw[:, 0:2, :], in_=wq_view[:, 0:2, :])
+        nc.sync.dma_start(out=wq_raw[:, 2:4, :], in_=wq_view[:, 2:4, :])
 
         x_sb = {}
 
         def load(qd):
             g, q = divmod(qd, QUADS)
             x_sb[qd] = xin.tile([P, KQ, D_IN], BF16, name="x_sb")
-            nc.sync.dma_start(
-                out=x_sb[qd][:], in_=h_ngbrs[g * P : (g + 1) * P, q * KQ : (q + 1) * KQ, :]
-            )
+            pieces = 2 if qd == 0 else 1
+            step = KQ // pieces
+            for i in range(pieces):
+                nc.sync.dma_start(
+                    out=x_sb[qd][:, i * step : (i + 1) * step, :],
+                    in_=h_ngbrs[g * P : (g + 1) * P, q * KQ + i * step : q * KQ + (i + 1) * step, :],
+                )
 
         load(0)
         load(1)
@@ -363,8 +369,9 @@ def tile_pinsageconv_t_kernel(tc, h_node, h_ngbrs, alpha, Wq, bq, Ww, bw, out):
         def l2_res(g):
             res = tail.tile([P, D_OUT], F32, name="res")
             if RES_ON_SCALAR and g < GROUPS - 1:
-                nc.scalar.activation(
-                    out=res[:], in_=s2[(g, "h2")][:], func=ACT.Copy, scale=s2[(g, "rec")][:, 0:1]
+                nc.gpsimd.tensor_scalar(
+                    out=res[:], in0=s2[(g, "h2")][:], scalar1=s2[(g, "rec")][:, 0:1], scalar2=0.0,
+                    op0=ALU.mult, op1=ALU.add,
                 )
             else:
                 nc.vector.tensor_scalar(

@@ -22,20 +22,20 @@ NQ = GROUPS * QUADS
 HC = D_HID // P
 NT = NQ * HC
 NSTEP = NT // 2
-ROUTES = "FS"
-MANUAL = True
 RES_ON_SCALAR = True
+PARK = N_NODES - NQ
+G_SHARE = (3, 2)
 PREP0 = 6
-L2_LAG = (5, 6, 7, 10, 11, 12, 13, 0, 15)
+L2_LAG = (5, 6, 7, 10, 11, 12, 13, 3, 15)
 LAG_T = 3
 
 FLOPS = 2 * N_NODES * K_NGB * D_IN * D_HID + 2 * N_NODES * (D_IN + D_HID) * D_OUT
 
 
-def route_of(t):
-    if t >= NT - 2:
-        return "F"
-    return ROUTES[t % len(ROUTES)]
+def weighed(qd):
+    if qd == 0:
+        return 0
+    return G_SHARE[qd % 2]
 
 
 def tile_pinsageconv_t_kernel(tc, h_node, h_ngbrs, alpha, Wq, bq, Ww, bw, out):
@@ -47,12 +47,11 @@ def tile_pinsageconv_t_kernel(tc, h_node, h_ngbrs, alpha, Wq, bq, Ww, bw, out):
         qnt = ctx.enter_context(tc.tile_pool(name="qnt", bufs=5))
         ypool = ctx.enter_context(tc.tile_pool(name="ypool", bufs=3))
         epool = ctx.enter_context(tc.tile_pool(name="epool", bufs=14))
-        lpool = ctx.enter_context(tc.tile_pool(name="lpool", bufs=3))
         tail = ctx.enter_context(tc.tile_pool(name="tail", bufs=2))
         pz = ctx.enter_context(tc.psum_pool(name="pz", bufs=4))
-        pe = ctx.enter_context(tc.psum_pool(name="pe", bufs=4))
-        if MANUAL:
-            ctx.enter_context(tc.manual_schedule())
+        pe = ctx.enter_context(tc.psum_pool(name="pe", bufs=3))
+        pa = ctx.enter_context(tc.psum_pool(name="pa", bufs=1))
+        ctx.enter_context(tc.manual_schedule())
 
         ident_f = const.tile([P, P], F32)
         make_identity(nc, ident_f[:])
@@ -140,10 +139,6 @@ def tile_pinsageconv_t_kernel(tc, h_node, h_ngbrs, alpha, Wq, bq, Ww, bw, out):
         nc.vector.tensor_copy(out=b_col[:], in_=bT[:, 0:HC])
         b_low = const.tile([P, HC], F32)
         nc.vector.tensor_scalar(out=b_low[:], in0=b_col[:], scalar1=SLOPE, scalar2=None, op0=ALU.mult)
-        b_high = const.tile([P, HC], F32)
-        nc.vector.tensor_scalar(
-            out=b_high[:], in0=b_col[:], scalar1=1.0 - SLOPE, scalar2=None, op0=ALU.mult
-        )
         quantise(wq_g, wq_c[:], wq_s[:])
 
         a_f = const.tile([P, GROUPS, K_NGB], F32)
@@ -160,6 +155,27 @@ def tile_pinsageconv_t_kernel(tc, h_node, h_ngbrs, alpha, Wq, bq, Ww, bw, out):
         nc.vector.tensor_tensor(
             out=a_n[:], in0=a_f[:], in1=a_rec[:].unsqueeze(2).to_broadcast([P, GROUPS, K_NGB]), op=ALU.mult
         )
+
+        a_bc = const.tile([P, NQ, KQ * P], F32)
+        park = {}
+
+        def park_T():
+            park["ps"] = pe.tile([P, P], F32, tag="eT", name="aT")
+            nc.tensor.transpose(park["ps"][:], a_n[:].rearrange("p g k -> p (g k)"), ident_f[:])
+
+        def park_store():
+            aT_sb = const.tile([P, P], F32, name="aT_sb")
+            nc.scalar.copy(out=aT_sb[:], in_=park["ps"][:])
+            nc.gpsimd.dma_start(
+                out=out[PARK : PARK + NQ, :].rearrange("r (s n) -> (r s) n", n=P), in_=aT_sb[:]
+            )
+            for g in range(GROUPS):
+                nc.gpsimd.dma_start(
+                    out=a_bc[:, g * QUADS : (g + 1) * QUADS, :].rearrange("p q c -> p (q c)"),
+                    in_=out[PARK + g * QUADS : PARK + (g + 1) * QUADS, :]
+                    .rearrange("q c -> (q c)")
+                    .partition_broadcast(P),
+                )
 
         w0_c = const.tile([P, D_OUT], U32, align_bytes=64)
         w0_s = const.tile([P, D_OUT], U8, align_bytes=64)
@@ -213,6 +229,7 @@ def tile_pinsageconv_t_kernel(tc, h_node, h_ngbrs, alpha, Wq, bq, Ww, bw, out):
         y_sb = {}
         e_sb = {}
         eT_ps = {}
+        sum_ps = {}
         acc = {}
 
         def x_T(xh):
@@ -241,68 +258,80 @@ def tile_pinsageconv_t_kernel(tc, h_node, h_ngbrs, alpha, Wq, bq, Ww, bw, out):
 
         def scalar_part(t):
             hc = t % HC
-            if route_of(t) == "F":
-                y_sb[t] = ypool.tile([P, KQ * P], F32, name="y")
-                nc.scalar.activation(
-                    out=y_sb[t][:], in_=z_ps[t][:], func=ACT.Identity, bias=b_low[:, hc : hc + 1], scale=SLOPE
-                )
-            else:
-                r_sb = lpool.tile([P, KQ * P], F32, name="r")
-                nc.scalar.activation(
-                    out=r_sb[:], in_=z_ps[t][:], func=ACT.Relu, bias=b_high[:, hc : hc + 1], scale=1.0 - SLOPE
-                )
-                l_sb = lpool.tile([P, KQ * P], F32, name="l")
-                nc.scalar.activation(
-                    out=l_sb[:], in_=z_ps[t][:], func=ACT.Identity, bias=b_low[:, hc : hc + 1], scale=SLOPE
-                )
-                e_sb[t] = epool.tile([P, KQ * P], F32, name="e")
-                nc.gpsimd.tensor_tensor(out=e_sb[t][:], in0=r_sb[:], in1=l_sb[:], op=ALU.add)
+            y_sb[t] = ypool.tile([P, KQ * P], F32, name="y")
+            nc.scalar.activation(
+                out=y_sb[t][:], in_=z_ps[t][:], func=ACT.Identity, bias=b_low[:, hc : hc + 1], scale=SLOPE
+            )
 
         def vector_part(t):
             hc = t % HC
-            if route_of(t) == "F":
-                e_sb[t] = epool.tile([P, KQ * P], F32, name="e")
-                nc.vector.scalar_tensor_tensor(
-                    out=e_sb[t][:], in0=z_ps[t][:], scalar=b_col[:, hc : hc + 1], in1=y_sb[t][:],
-                    op0=ALU.add, op1=ALU.max,
+            e_sb[t] = epool.tile([P, KQ * P], F32, name="e")
+            nc.vector.scalar_tensor_tensor(
+                out=e_sb[t][:], in0=z_ps[t][:], scalar=b_col[:, hc : hc + 1], in1=y_sb[t][:],
+                op0=ALU.add, op1=ALU.max,
+            )
+
+        def weigh(t):
+            qd = t // HC
+            n = weighed(qd) * P
+            if n:
+                nc.gpsimd.tensor_tensor(
+                    out=e_sb[t][:, 0:n], in0=e_sb[t][:, 0:n], in1=a_bc[:, qd, 0:n], op=ALU.mult
+                )
+
+        def sum_T(t):
+            qd, hc = divmod(t, HC)
+            g, q = divmod(qd, QUADS)
+            n = weighed(qd)
+            if n and g not in sum_ps:
+                sum_ps[g] = pa.tile([P, D_HID], F32, tag="sum", name="sum")
+                first = True
+            else:
+                first = False
+            for kk in range(n):
+                nc.tensor.matmul(
+                    out=sum_ps[g][:, hc * P : (hc + 1) * P], lhsT=e_sb[t][:, kk * P : (kk + 1) * P],
+                    rhs=ident_f[:], is_transpose=True, start=(first and kk == 0),
+                    stop=(q == QUADS - 1 and hc == HC - 1 and kk == n - 1),
                 )
 
         def tk(qd, kk):
             eT_ps[(qd, kk)] = pe.tile([P, D_HID], F32, tag="eT", name="eT")
-            parts = []
             for hc in range(HC):
-                t = qd * HC + hc
-                parts.append((hc, e_sb[t]))
-            for i, (hc, src) in enumerate(parts):
                 nc.tensor.matmul(
-                    out=eT_ps[(qd, kk)][:, hc * P : (hc + 1) * P], lhsT=src[:, kk * P : (kk + 1) * P],
-                    rhs=ident_f[:], is_transpose=True, start=(i == 0), stop=(i == len(parts) - 1),
+                    out=eT_ps[(qd, kk)][:, hc * P : (hc + 1) * P],
+                    lhsT=e_sb[qd * HC + hc][:, kk * P : (kk + 1) * P],
+                    rhs=ident_f[:], is_transpose=True, start=(hc == 0), stop=(hc == HC - 1),
                 )
 
         def fma(qd, kk):
             g, q = divmod(qd, QUADS)
             k = q * KQ + kk
-            half = (g, k % 2)
-            if k < 2:
-                acc[half] = const.tile([P, D_HID], F32, name="acc%d_%d" % half)
+            if g not in acc:
+                acc[g] = const.tile([P, D_HID], F32, name="acc%d" % g)
                 nc.vector.tensor_scalar(
-                    out=acc[half][:], in0=eT_ps[(qd, kk)][:], scalar1=a_n[:, g, k : k + 1], scalar2=None,
+                    out=acc[g][:], in0=eT_ps[(qd, kk)][:], scalar1=a_n[:, g, k : k + 1], scalar2=None,
                     op0=ALU.mult,
                 )
             else:
                 nc.vector.scalar_tensor_tensor(
-                    out=acc[half][:], in0=eT_ps[(qd, kk)][:], scalar=a_n[:, g, k : k + 1], in1=acc[half][:],
+                    out=acc[g][:], in0=eT_ps[(qd, kk)][:], scalar=a_n[:, g, k : k + 1], in1=acc[g][:],
                     op0=ALU.mult, op1=ALU.add,
                 )
 
         s2 = {}
 
+        def l2_sum(g):
+            s2[(g, "sum")] = tail.tile([P, D_HID], F32, name="sum_sb")
+            nc.scalar.copy(out=s2[(g, "sum")][:], in_=sum_ps[g][:])
+
         def l2_T(g):
             hT = pe.tile([P, 4, P], F32, tag="eT", name="hT")
             for i in range(8):
                 t, par = divmod(i, 2)
+                part = (acc[g], s2[(g, "sum")])[par]
                 nc.tensor.matmul(
-                    out=hT[:, t, :], lhsT=acc[(g, par)][:, t * P : (t + 1) * P], rhs=ident_f[:],
+                    out=hT[:, t, :], lhsT=part[:, t * P : (t + 1) * P], rhs=ident_f[:],
                     is_transpose=True, start=(i == 0), stop=(i == 7),
                 )
             s2[(g, "hT")] = hT
@@ -410,6 +439,9 @@ def tile_pinsageconv_t_kernel(tc, h_node, h_ngbrs, alpha, Wq, bq, Ww, bw, out):
             g = l2_due(j, L2_LAG[8])
             if g is not None:
                 l2_store(g)
+            g = l2_due(j, L2_LAG[7])
+            if g is not None:
+                l2_sum(g)
             for xh in xc_at.get(j, []):
                 x_copy(xh)
             if 0 <= j - PREP0 - 1 < 8:
@@ -430,9 +462,19 @@ def tile_pinsageconv_t_kernel(tc, h_node, h_ngbrs, alpha, Wq, bq, Ww, bw, out):
             for xh in xt_at.get(j, []):
                 x_T(xh)
             qd_t, pair_t = divmod(j - LAG_T, 2)
+            own = []
             if 0 <= qd_t < NQ:
-                tk(qd_t, 2 * pair_t)
-                tk(qd_t, 2 * pair_t + 1)
+                rest = list(range(weighed(qd_t), KQ))
+                cut = (len(rest) + 1) // 2
+                own = rest[:cut] if pair_t == 0 else rest[cut:]
+                for kk in own:
+                    tk(qd_t, kk)
+                sum_T(qd_t * HC + 2 * pair_t)
+                sum_T(qd_t * HC + 2 * pair_t + 1)
+            if j == -2:
+                park_T()
+            if j == -1:
+                park_store()
             g = l2_due(j, L2_LAG[0])
             if g is not None:
                 if g == GROUPS - 1:
@@ -443,8 +485,9 @@ def tile_pinsageconv_t_kernel(tc, h_node, h_ngbrs, alpha, Wq, bq, Ww, bw, out):
             for i in range(2):
                 if 0 <= j < NSTEP:
                     vector_part(2 * j + i)
-                if 0 <= qd_t < NQ:
-                    fma(qd_t, 2 * pair_t + i)
+                    weigh(2 * j + i)
+                if i < len(own):
+                    fma(qd_t, own[i])
             if j in xq_at:
                 x_quant(xq_at[j])
             if 0 <= j - PREP0 - 2 < 8:

@@ -15,38 +15,52 @@ AX = mybir.AxisListType
 P = 128
 N_NODES, K_NGB, D_IN, D_HID, D_OUT = 512, 32, 512, 512, 512
 SLOPE = 0.01
+TINY = 1e-37
 GROUPS = N_NODES // P
 KQ = 4
 QUADS = K_NGB // KQ
 NQ = GROUPS * QUADS
 HC = D_HID // P
-NT = NQ * HC
-NSTEP = NT // 2
-RES_ON_SCALAR = True
 PARK = N_NODES - NQ
-G_SHARE = (3, 2)
-PREP0 = 6
-L2_LAG = (5, 6, 7, 10, 11, 12, 13, 3, 15)
-LAG_T = 3
+SHARE_EVEN = (2, 2)
+SHARE_ODD = (2, 2)
+SUM_LAG = 2
+LAGS = (1, 2, 3, 4, 5, 5, 6)
+QA = 2
+ORDER = "y0 e0 L l Q y1 e1 w0 y2 e2 y3 e3 w1 E c0 c1 p b n r".split(" ")
+AHEAD = QA + 1
+PREP0 = 2
+FIRST_LOADS = 5
+G_FIRST = 2
+WAHEAD = 3
 
 FLOPS = 2 * N_NODES * K_NGB * D_IN * D_HID + 2 * N_NODES * (D_IN + D_HID) * D_OUT
 
 
-def weighed(qd):
-    if qd == 0:
+def weighed(qd, pair):
+    if qd < G_FIRST:
         return 0
-    return G_SHARE[qd % 2]
+    return (SHARE_ODD if qd % 2 else SHARE_EVEN)[pair]
+
+
+def left(qd):
+    res = []
+    for kk in range(KQ - 1, -1, -1):
+        pairs = [pair for pair in range(2) if weighed(qd, pair) <= kk]
+        if pairs:
+            res.append((kk, 2 * pairs[0], 2 * pairs[-1] + 2))
+    return res
 
 
 def tile_pinsageconv_t_kernel(tc, h_node, h_ngbrs, alpha, Wq, bq, Ww, bw, out):
     nc = tc.nc
     with ExitStack() as ctx:
         const = ctx.enter_context(tc.tile_pool(name="const", bufs=1))
-        xin = ctx.enter_context(tc.tile_pool(name="xin", bufs=7))
+        xin = ctx.enter_context(tc.tile_pool(name="xin", bufs=6))
         grp = ctx.enter_context(tc.tile_pool(name="grp", bufs=4))
-        qnt = ctx.enter_context(tc.tile_pool(name="qnt", bufs=5))
-        ypool = ctx.enter_context(tc.tile_pool(name="ypool", bufs=3))
-        epool = ctx.enter_context(tc.tile_pool(name="epool", bufs=14))
+        qnt = ctx.enter_context(tc.tile_pool(name="qnt", bufs=4))
+        ypool = ctx.enter_context(tc.tile_pool(name="ypool", bufs=4))
+        epool = ctx.enter_context(tc.tile_pool(name="epool", bufs=8))
         tail = ctx.enter_context(tc.tile_pool(name="tail", bufs=2))
         pz = ctx.enter_context(tc.psum_pool(name="pz", bufs=4))
         pe = ctx.enter_context(tc.psum_pool(name="pe", bufs=3))
@@ -77,29 +91,32 @@ def tile_pinsageconv_t_kernel(tc, h_node, h_ngbrs, alpha, Wq, bq, Ww, bw, out):
                 )
 
         load(0)
-        load(1)
-        load(2)
-        load(3)
 
         b_rows = const.tile([P, P], BF16)
         nc.vector.memset(b_rows[:], 0.0)
         one = const.tile([P, 1], F32)
         nc.vector.memset(one[:], 1.0)
-        nc.scalar.dma_start(out=b_rows[0:HC, :], in_=bq.rearrange("(b p) -> b p", p=P))
+        tiny = const.tile([P, 1], F32)
+        nc.vector.tensor_scalar(out=tiny[:], in0=one[:], scalar1=TINY, scalar2=None, op0=ALU.mult)
         a_raw = const.tile([P, GROUPS, K_NGB], BF16)
         nc.scalar.dma_start(out=a_raw[:], in_=alpha.rearrange("(g p) k o -> p g (k o)", p=P))
+        nc.scalar.dma_start(out=b_rows[0:HC, :], in_=bq.rearrange("(b p) -> b p", p=P))
         one_s = const.tile([P, 1], F32)
-        nc.scalar.sqrt(out=one_s[:], in_=one[:])
+        nc.scalar.activation(out=one_s[:], in_=one[:], func=ACT.Abs_reciprocal_sqrt)
+
+        for qd in range(1, FIRST_LOADS):
+            load(qd)
 
         ww_raw = const.tile([P, D_OUT // P, D_IN + D_HID], BF16)
         hn_raw = const.tile([P, GROUPS, D_IN], BF16)
         bw_bc = const.tile([P, D_OUT], BF16)
 
-        def late_loads(j):
-            if j == 0:
+        def late_loads(i):
+            if i == 0:
                 nc.sync.dma_start(out=ww_raw[:], in_=Ww.rearrange("(b p) c -> p b c", p=P))
-            elif j == 2:
+            elif i == 1:
                 nc.sync.dma_start(out=hn_raw[:], in_=h_node.rearrange("(g p) i -> p g i", p=P))
+            elif i == 4:
                 nc.sync.dma_start(out=bw_bc[:], in_=bw.partition_broadcast(P))
 
         def words_T(src_words, half, pool, tag):
@@ -111,8 +128,8 @@ def tile_pinsageconv_t_kernel(tc, h_node, h_ngbrs, alpha, Wq, bq, Ww, bw, out):
                     )
             return xt
 
-        def words_copy(xt, grouped, half):
-            nc.scalar.copy(
+        def words_copy(xt, grouped, half, copy):
+            copy(
                 out=grouped[:].bitcast(F32)[:, 2 * half * P : (2 * half + 2) * P, :].rearrange(
                     "p (b c) u -> p b c u", b=2
                 ),
@@ -126,56 +143,6 @@ def tile_pinsageconv_t_kernel(tc, h_node, h_ngbrs, alpha, Wq, bq, Ww, bw, out):
 
         wq_c = const.tile([P, D_HID], U32, align_bytes=64)
         wq_s = const.tile([P, D_HID], U8, align_bytes=64)
-        wq_g = grp.tile([P, 4 * P, 4], BF16, align_bytes=64, tag="grouped", name="wq_g")
-        wq_words = wq_raw[:].bitcast(F32)
-        wt0 = words_T(wq_words, 0, pz, "z")
-        wt1 = words_T(wq_words, 1, pz, "z")
-        words_copy(wt0, wq_g, 0)
-        words_copy(wt1, wq_g, 1)
-
-        bT = pe.tile([P, P], BF16, tag="eT", name="bT")
-        nc.tensor.transpose(bT[:], b_rows[:], ident_b[:])
-        b_col = const.tile([P, HC], F32)
-        nc.vector.tensor_copy(out=b_col[:], in_=bT[:, 0:HC])
-        b_low = const.tile([P, HC], F32)
-        nc.vector.tensor_scalar(out=b_low[:], in0=b_col[:], scalar1=SLOPE, scalar2=None, op0=ALU.mult)
-        quantise(wq_g, wq_c[:], wq_s[:])
-
-        a_f = const.tile([P, GROUPS, K_NGB], F32)
-        nc.vector.tensor_copy(out=a_f[:], in_=a_raw[:])
-        a_sum = const.tile([P, GROUPS], F32)
-        nc.vector.tensor_reduce(out=a_sum[:], in_=a_f[:], axis=AX.X, op=ALU.add)
-        a_den = const.tile([P, GROUPS], F32)
-        nc.vector.scalar_tensor_tensor(
-            out=a_den[:], in0=a_sum[:], scalar=0.0, in1=a_sum[:], op0=ALU.is_equal, op1=ALU.add
-        )
-        a_rec = const.tile([P, GROUPS], F32)
-        nc.vector.reciprocal(out=a_rec[:], in_=a_den[:])
-        a_n = const.tile([P, GROUPS, K_NGB], F32)
-        nc.vector.tensor_tensor(
-            out=a_n[:], in0=a_f[:], in1=a_rec[:].unsqueeze(2).to_broadcast([P, GROUPS, K_NGB]), op=ALU.mult
-        )
-
-        a_bc = const.tile([P, NQ, KQ * P], F32)
-        park = {}
-
-        def park_T():
-            park["ps"] = pe.tile([P, P], F32, tag="eT", name="aT")
-            nc.tensor.transpose(park["ps"][:], a_n[:].rearrange("p g k -> p (g k)"), ident_f[:])
-
-        def park_store():
-            aT_sb = const.tile([P, P], F32, name="aT_sb")
-            nc.scalar.copy(out=aT_sb[:], in_=park["ps"][:])
-            nc.gpsimd.dma_start(
-                out=out[PARK : PARK + NQ, :].rearrange("r (s n) -> (r s) n", n=P), in_=aT_sb[:]
-            )
-            for g in range(GROUPS):
-                nc.gpsimd.dma_start(
-                    out=a_bc[:, g * QUADS : (g + 1) * QUADS, :].rearrange("p q c -> p (q c)"),
-                    in_=out[PARK + g * QUADS : PARK + (g + 1) * QUADS, :]
-                    .rearrange("q c -> (q c)")
-                    .partition_broadcast(P),
-                )
 
         w0_c = const.tile([P, D_OUT], U32, align_bytes=64)
         w0_s = const.tile([P, D_OUT], U8, align_bytes=64)
@@ -204,9 +171,9 @@ def tile_pinsageconv_t_kernel(tc, h_node, h_ngbrs, alpha, Wq, bq, Ww, bw, out):
 
         def prep_copy(i):
             if i < 2:
-                words_copy(prep_ps[i], prep_g[0], i)
+                words_copy(prep_ps[i], prep_g[0], i, nc.scalar.copy)
             elif i < 4:
-                words_copy(prep_ps[i], prep_g[2], i - 2)
+                words_copy(prep_ps[i], prep_g[2], i - 2, nc.scalar.copy)
             else:
                 ob = i - 4
                 nc.scalar.copy(
@@ -232,81 +199,78 @@ def tile_pinsageconv_t_kernel(tc, h_node, h_ngbrs, alpha, Wq, bq, Ww, bw, out):
         sum_ps = {}
         acc = {}
 
-        def x_T(xh):
-            qd, half = divmod(xh, 2)
+        def x_T(qd, half, pool=pe, tag="eT"):
             if half == 0:
                 grouped[qd] = grp.tile([P, 4 * P, 4], BF16, align_bytes=64, tag="grouped", name="grouped")
-            xt_ps[xh] = words_T(x_sb[qd][:].bitcast(F32), half, pe, "eT")
+            xt_ps[(qd, half)] = words_T(x_sb[qd][:].bitcast(F32), half, pool, tag)
 
-        def x_copy(xh):
-            qd, half = divmod(xh, 2)
-            words_copy(xt_ps[xh], grouped[qd], half)
+        def x_copy(qd, half, copy=nc.scalar.copy):
+            words_copy(xt_ps[(qd, half)], grouped[qd], half, copy)
 
         def x_quant(qd):
             x_c[qd] = qnt.tile([P, KQ * P], U32, align_bytes=64, name="x_c")
             x_s[qd] = qnt.tile([P, KQ * P], U8, align_bytes=64, name="x_s")
             quantise(grouped[qd], x_c[qd][:], x_s[qd][:])
 
-        def mx(t):
-            qd, hc = divmod(t, HC)
+        def mx(qd, hc):
             cols = slice(hc * P, (hc + 1) * P)
-            z_ps[t] = pz.tile([P, KQ * P], F32, tag="z", name="z")
+            z_ps[hc] = pz.tile([P, KQ * P], F32, tag="z", name="z")
             nc.tensor.matmul_mx(
-                out=z_ps[t][:], lhsT=wq_c[:, cols].bitcast(FP8X4), lhsT_scale=wq_s[:, cols],
+                out=z_ps[hc][:], lhsT=wq_c[:, cols].bitcast(FP8X4), lhsT_scale=wq_s[:, cols],
                 rhs=x_c[qd][:].bitcast(FP8X4), rhs_scale=x_s[qd][:], start=True, stop=True,
             )
 
-        def scalar_part(t):
-            hc = t % HC
-            y_sb[t] = ypool.tile([P, KQ * P], F32, name="y")
+        def low(hc):
+            y_sb[hc] = ypool.tile([P, KQ * P], F32, name="y")
             nc.scalar.activation(
-                out=y_sb[t][:], in_=z_ps[t][:], func=ACT.Identity, bias=b_low[:, hc : hc + 1], scale=SLOPE
+                out=y_sb[hc][:], in_=z_ps[hc][:], func=ACT.Identity, bias=b_low[:, hc : hc + 1], scale=SLOPE
             )
 
-        def vector_part(t):
-            hc = t % HC
-            e_sb[t] = epool.tile([P, KQ * P], F32, name="e")
+        def lrelu(qd, hc):
+            pair, i = divmod(hc, 2)
+            if i == 0:
+                e_sb[(qd, pair)] = epool.tile([P, 2, KQ * P], F32, name="e")
             nc.vector.scalar_tensor_tensor(
-                out=e_sb[t][:], in0=z_ps[t][:], scalar=b_col[:, hc : hc + 1], in1=y_sb[t][:],
+                out=e_sb[(qd, pair)][:, i, :], in0=z_ps[hc][:], scalar=b_col[:, hc : hc + 1], in1=y_sb[hc][:],
                 op0=ALU.add, op1=ALU.max,
             )
 
-        def weigh(t):
-            qd = t // HC
-            n = weighed(qd) * P
+        def weigh(qd, pair):
+            n = weighed(qd, pair) * P
             if n:
+                e = e_sb[(qd, pair)]
                 nc.gpsimd.tensor_tensor(
-                    out=e_sb[t][:, 0:n], in0=e_sb[t][:, 0:n], in1=a_bc[:, qd, 0:n], op=ALU.mult
+                    out=e[:, :, 0:n], in0=e[:, :, 0:n],
+                    in1=a_bc[:, qd, 0:n].unsqueeze(1).to_broadcast([P, 2, n]), op=ALU.mult,
                 )
 
-        def sum_T(t):
-            qd, hc = divmod(t, HC)
+        def sum_T(qd, hc):
             g, q = divmod(qd, QUADS)
-            n = weighed(qd)
-            if n and g not in sum_ps:
+            n = weighed(qd, hc // 2)
+            first = n > 0 and g not in sum_ps
+            if first:
                 sum_ps[g] = pa.tile([P, D_HID], F32, tag="sum", name="sum")
-                first = True
-            else:
-                first = False
             for kk in range(n):
                 nc.tensor.matmul(
-                    out=sum_ps[g][:, hc * P : (hc + 1) * P], lhsT=e_sb[t][:, kk * P : (kk + 1) * P],
+                    out=sum_ps[g][:, hc * P : (hc + 1) * P],
+                    lhsT=e_sb[(qd, hc // 2)][:, hc % 2, kk * P : (kk + 1) * P],
                     rhs=ident_f[:], is_transpose=True, start=(first and kk == 0),
                     stop=(q == QUADS - 1 and hc == HC - 1 and kk == n - 1),
                 )
 
-        def tk(qd, kk):
+        def tk(qd, kk, lo, hi):
             eT_ps[(qd, kk)] = pe.tile([P, D_HID], F32, tag="eT", name="eT")
-            for hc in range(HC):
+            for hc in range(lo, hi):
                 nc.tensor.matmul(
                     out=eT_ps[(qd, kk)][:, hc * P : (hc + 1) * P],
-                    lhsT=e_sb[qd * HC + hc][:, kk * P : (kk + 1) * P],
-                    rhs=ident_f[:], is_transpose=True, start=(hc == 0), stop=(hc == HC - 1),
+                    lhsT=e_sb[(qd, hc // 2)][:, hc % 2, kk * P : (kk + 1) * P],
+                    rhs=ident_f[:], is_transpose=True, start=(hc == lo), stop=(hc == hi - 1),
                 )
 
-        def fma(qd, kk):
+        def fma(qd, kk, lo, hi):
             g, q = divmod(qd, QUADS)
             k = q * KQ + kk
+            cols = slice(lo * P, hi * P)
             if g not in acc:
                 acc[g] = const.tile([P, D_HID], F32, name="acc%d" % g)
                 nc.vector.tensor_scalar(
@@ -315,8 +279,8 @@ def tile_pinsageconv_t_kernel(tc, h_node, h_ngbrs, alpha, Wq, bq, Ww, bw, out):
                 )
             else:
                 nc.vector.scalar_tensor_tensor(
-                    out=acc[g][:], in0=eT_ps[(qd, kk)][:], scalar=a_n[:, g, k : k + 1], in1=acc[g][:],
-                    op0=ALU.mult, op1=ALU.add,
+                    out=acc[g][:, cols], in0=eT_ps[(qd, kk)][:, cols], scalar=a_n[:, g, k : k + 1],
+                    in1=acc[g][:, cols], op0=ALU.mult, op1=ALU.add,
                 )
 
         s2 = {}
@@ -381,130 +345,158 @@ def tile_pinsageconv_t_kernel(tc, h_node, h_ngbrs, alpha, Wq, bq, Ww, bw, out):
             sq = tail.tile([P, D_OUT], F32, name="sq")
             ss = tail.tile([P, 1], F32, name="ss")
             nc.scalar.activation(out=sq[:], in_=s2[(g, "h2")][:], func=ACT.Square, accum_out=ss[:])
-            nrm = tail.tile([P, 1], F32, name="nrm")
-            nc.scalar.sqrt(out=nrm[:], in_=ss[:])
-            s2[(g, "nrm")] = nrm
-
-        def l2_norm_v(g):
-            nrm = s2[(g, "nrm")]
-            den = tail.tile([P, 1], F32, name="den")
-            nc.vector.scalar_tensor_tensor(
-                out=den[:], in0=nrm[:], scalar=0.0, in1=nrm[:], op0=ALU.is_equal, op1=ALU.add
-            )
-            rec = tail.tile([P, 1], F32, name="rec")
-            nc.vector.reciprocal(out=rec[:], in_=den[:])
-            s2[(g, "rec")] = rec
+            rs = tail.tile([P, 1], F32, name="rs")
+            nc.scalar.activation(out=rs[:], in_=ss[:], func=ACT.Abs_reciprocal_sqrt, bias=tiny[:, 0:1])
+            s2[(g, "rs")] = rs
 
         def l2_res(g):
             res = tail.tile([P, D_OUT], F32, name="res")
-            if RES_ON_SCALAR and g < GROUPS - 1:
-                nc.gpsimd.tensor_scalar(
-                    out=res[:], in0=s2[(g, "h2")][:], scalar1=s2[(g, "rec")][:, 0:1], scalar2=0.0,
-                    op0=ALU.mult, op1=ALU.add,
+            if g < GROUPS - 1:
+                nc.scalar.activation(
+                    out=res[:], in_=s2[(g, "h2")][:], func=ACT.Copy, scale=s2[(g, "rs")][:, 0:1]
                 )
             else:
                 nc.vector.tensor_scalar(
-                    out=res[:], in0=s2[(g, "h2")][:], scalar1=s2[(g, "rec")][:, 0:1], scalar2=None, op0=ALU.mult
+                    out=res[:], in0=s2[(g, "h2")][:], scalar1=s2[(g, "rs")][:, 0:1], scalar2=None, op0=ALU.mult
                 )
             s2[(g, "res")] = res
 
         def l2_store(g):
             nc.sync.dma_start(out=out[g * P : (g + 1) * P, :], in_=s2[(g, "res")][:])
 
-        def l2_due(j, lag):
-            g, r = divmod(j - lag, NSTEP // GROUPS)
+        b_col = const.tile([P, HC], F32)
+        b_low = const.tile([P, HC], F32)
+        a_f = const.tile([P, GROUPS, K_NGB], F32)
+        a_sum = const.tile([P, GROUPS], F32)
+        a_den = const.tile([P, GROUPS], F32)
+        a_rec = const.tile([P, GROUPS], F32)
+        a_n = const.tile([P, GROUPS, K_NGB], F32)
+        a_bc = const.tile([P, NQ, KQ * P], F32)
+        aT_sb = const.tile([P, P], F32, name="aT_sb")
+
+        wq_g = grp.tile([P, 4 * P, 4], BF16, align_bytes=64, tag="grouped", name="wq_g")
+        wq_words = wq_raw[:].bitcast(F32)
+        wt0 = words_T(wq_words, 0, pz, "z")
+        wt1 = words_T(wq_words, 1, pz, "z")
+        x_T(0, 0, pz, "z")
+        x_T(0, 1, pz, "z")
+        words_copy(wt0, wq_g, 0, nc.scalar.copy)
+        x_copy(0, 0, nc.scalar.copy)
+        nc.vector.tensor_copy(out=a_f[:], in_=a_raw[:])
+        words_copy(wt1, wq_g, 1, nc.vector.tensor_copy)
+        nc.vector.tensor_reduce(out=a_sum[:], in_=a_f[:], axis=AX.X, op=ALU.add)
+        quantise(wq_g, wq_c[:], wq_s[:])
+        nc.vector.scalar_tensor_tensor(
+            out=a_den[:], in0=a_sum[:], scalar=0.0, in1=a_sum[:], op0=ALU.is_equal, op1=ALU.add
+        )
+        x_copy(0, 1, nc.vector.tensor_copy)
+        nc.vector.reciprocal(out=a_rec[:], in_=a_den[:])
+        x_quant(0)
+        nc.vector.tensor_tensor(
+            out=a_n[:], in0=a_f[:], in1=a_rec[:].unsqueeze(2).to_broadcast([P, GROUPS, K_NGB]), op=ALU.mult
+        )
+        bT = pe.tile([P, P], BF16, tag="eT", name="bT")
+        nc.tensor.transpose(bT[:], b_rows[:], ident_b[:])
+        nc.vector.tensor_copy(out=b_col[:], in_=bT[:, 0:HC])
+        nc.vector.tensor_scalar(out=b_low[:], in0=b_col[:], scalar1=SLOPE, scalar2=None, op0=ALU.mult)
+        for qd in range(1, AHEAD):
+            for half in range(2):
+                x_T(qd, half)
+                x_copy(qd, half)
+
+        def park_weights():
+            aT = pe.tile([P, P], F32, tag="eT", name="aT")
+            nc.tensor.transpose(aT[:], a_n[:].rearrange("p g k -> p (g k)"), ident_f[:])
+            nc.scalar.copy(out=aT_sb[:], in_=aT[:])
+            nc.sync.dma_start(
+                out=out[PARK : PARK + NQ, :].rearrange("r (s n) -> (r s) n", n=P), in_=aT_sb[:]
+            )
+
+        def load_weights(qd):
+            nc.sync.dma_start(out=a_bc[:, qd, :], in_=out[PARK + qd, :].partition_broadcast(P))
+
+        def due(i, lag):
+            g, r = divmod(i - lag, QUADS)
             if r == 0 and 1 <= g <= GROUPS:
                 return g - 1
             return None
 
-        xt_at = {}
-        xc_at = {}
-        xq_at = {}
-        for xh in range(2 * NQ):
-            if xh < 4:
-                jx = xh - 4
-            elif xh < 8:
-                jx = (xh - 4) // 2
-            else:
-                jx = xh - 6
-            xt_at[jx] = xt_at.get(jx, []) + [xh]
-            xc_at[jx + 1] = xc_at.get(jx + 1, []) + [xh]
-            if xh % 2 == 1:
-                xq_at[jx + 1] = xh // 2
-
-        for j in range(-4, NSTEP + L2_LAG[8] + 1):
-            if j % 2 == 0 and 4 <= j // 2 + 6 < NQ:
-                load(j // 2 + 6)
-            late_loads(j)
-            g = l2_due(j, L2_LAG[8])
-            if g is not None:
-                l2_store(g)
-            g = l2_due(j, L2_LAG[7])
-            if g is not None:
-                l2_sum(g)
-            for xh in xc_at.get(j, []):
-                x_copy(xh)
-            if 0 <= j - PREP0 - 1 < 8:
-                prep_copy(j - PREP0 - 1)
-            g = l2_due(j, L2_LAG[1])
-            if g is not None:
-                l2_copy(g)
-            g = l2_due(j, L2_LAG[3])
-            if g is not None:
-                if g < GROUPS - 1:
-                    l2_mx0(g)
-                l2_mx1(g)
-            if 0 <= j < NSTEP:
-                mx(2 * j)
-                mx(2 * j + 1)
-                scalar_part(2 * j)
-                scalar_part(2 * j + 1)
-            for xh in xt_at.get(j, []):
-                x_T(xh)
-            qd_t, pair_t = divmod(j - LAG_T, 2)
-            own = []
-            if 0 <= qd_t < NQ:
-                rest = list(range(weighed(qd_t), KQ))
-                cut = (len(rest) + 1) // 2
-                own = rest[:cut] if pair_t == 0 else rest[cut:]
-                for kk in own:
-                    tk(qd_t, kk)
-                sum_T(qd_t * HC + 2 * pair_t)
-                sum_T(qd_t * HC + 2 * pair_t + 1)
-            if j == -2:
-                park_T()
-            if j == -1:
-                park_store()
-            g = l2_due(j, L2_LAG[0])
-            if g is not None:
-                if g == GROUPS - 1:
-                    l2_mx0(g)
-                l2_T(g)
-            if 0 <= j - PREP0 < 8:
-                prep_T(j - PREP0)
-            for i in range(2):
-                if 0 <= j < NSTEP:
-                    vector_part(2 * j + i)
-                    weigh(2 * j + i)
-                if i < len(own):
-                    fma(qd_t, own[i])
-            if j in xq_at:
-                x_quant(xq_at[j])
-            if 0 <= j - PREP0 - 2 < 8:
-                prep_quant(j - PREP0 - 2)
-            g = l2_due(j, L2_LAG[2])
-            if g is not None:
-                l2_quant(g)
-            g = l2_due(j, L2_LAG[3])
-            if g is not None:
-                l2_bias(g)
-            g = l2_due(j, L2_LAG[4])
-            if g is not None:
-                l2_lrelu(g)
-            g = l2_due(j, L2_LAG[5])
-            if g is not None:
-                l2_norm_s(g)
-                l2_norm_v(g)
-            g = l2_due(j, L2_LAG[6])
-            if g is not None:
-                l2_res(g)
+        late = []
+        for i in range(NQ + 6 + SUM_LAG):
+            run = i < NQ
+            old = i - 1
+            own = left(old) if 0 <= old < NQ else []
+            cut = (len(own) + 1) // 2
+            nxt = i + AHEAD if i + AHEAD < NQ else None
+            if i == 0:
+                park_weights()
+                for qd in range(G_FIRST, G_FIRST + WAHEAD):
+                    load_weights(qd)
+            elif i + G_FIRST + WAHEAD - 1 < NQ:
+                load_weights(i + G_FIRST + WAHEAD - 1)
+            if i + FIRST_LOADS < NQ:
+                load(i + FIRST_LOADS)
+            late_loads(i)
+            b = SUM_LAG - 1
+            g1, g2, g3, g4, g5, g6, g7 = (due(i, lag + b) for lag in LAGS)
+            if g1 is not None:
+                l2_sum(g1)
+            if g2 is not None:
+                l2_copy(g2)
+            if run:
+                for hc in range(HC):
+                    mx(i, hc)
+            if g3 is not None:
+                l2_mx0(g3)
+                l2_mx1(g3)
+            if nxt is not None:
+                x_T(nxt, 0)
+                x_T(nxt, 1)
+            for piece in own[:cut]:
+                tk(old, *piece)
+            if 0 <= i - SUM_LAG < NQ:
+                for hc in range(HC):
+                    sum_T(i - SUM_LAG, hc)
+            for piece in own[cut:]:
+                tk(old, *piece)
+            if g1 is not None:
+                l2_T(g1)
+            if 0 <= i - PREP0 < 8:
+                prep_T(i - PREP0)
+            for what in ORDER:
+                if what[0] == "y" and run:
+                    low(int(what[1]))
+                elif what[0] == "c" and nxt is not None:
+                    x_copy(nxt, int(what[1]))
+                elif what[0] == "e" and run:
+                    lrelu(i, int(what[1]))
+                elif what[0] == "w" and run:
+                    weigh(i, int(what[1]))
+                elif what == "L":
+                    for piece in late:
+                        fma(*piece)
+                elif what == "E":
+                    for piece in own[:cut]:
+                        fma(old, *piece)
+                elif what == "Q":
+                    if i == 0:
+                        for qd in range(1, QA):
+                            x_quant(qd)
+                    if i + QA < NQ:
+                        x_quant(i + QA)
+                    if g2 is not None:
+                        l2_quant(g2)
+                    if 0 <= i - PREP0 - 1 < 8:
+                        prep_quant(i - PREP0 - 1)
+                elif what == "l" and g4 is not None:
+                    l2_lrelu(g4)
+                elif what == "b" and g3 is not None:
+                    l2_bias(g3)
+                elif what == "p" and 0 <= i - PREP0 < 8:
+                    prep_copy(i - PREP0)
+                elif what == "n" and g5 is not None:
+                    l2_norm_s(g5)
+                elif what == "r" and g7 is not None:
+                    l2_res(g7)
+                    l2_store(g7)
+            late = [(old,) + piece for piece in own[cut:]]

@@ -22,25 +22,39 @@ QUADS = K_NGB // KQ
 NQ = GROUPS * QUADS
 HC = D_HID // P
 PARK = N_NODES - NQ
+ALONE = (0, 1)
 SHARE_EVEN = (2, 2)
-SHARE_ODD = (2, 2)
+SHARE_ODD = (3, 3)
 SUM_LAG = 2
-LAGS = (1, 2, 3, 4, 5, 5, 6)
-QA = 2
-ORDER = "y0 e0 L l Q y1 e1 w0 y2 e2 y3 e3 w1 E c0 c1 p b n r".split(" ")
-AHEAD = QA + 1
+LONE = 2
+QA = 1
+ORDER = "d y0 y1 c0 y2 y3 e0 w01 Q L e1 w12 e2 w23 e3 w34 E".split(" ")
+PORDER = "Z M02 j X0 S242 M24 X1 P T K S021".split(" ")
+AHEAD = QA + 2
 PREP0 = 2
 FIRST_LOADS = 5
-G_FIRST = 2
+G_FIRST = 0
 WAHEAD = 3
 
 FLOPS = 2 * N_NODES * K_NGB * D_IN * D_HID + 2 * N_NODES * (D_IN + D_HID) * D_OUT
 
 
 def weighed(qd, pair):
-    if qd < G_FIRST:
-        return 0
     return (SHARE_ODD if qd % 2 else SHARE_EVEN)[pair]
+
+
+def pair_of(qd):
+    if qd < LONE:
+        return qd, 1
+    return qd - (qd - LONE) % 2, 2
+
+
+def alone(qd, hc):
+    return hc == HC - 1 and qd % ALONE[1] < ALONE[0]
+
+
+def parts_of(qd, hc):
+    return (hc, HC) if alone(qd, hc) else (hc,)
 
 
 def left(qd):
@@ -56,12 +70,13 @@ def tile_pinsageconv_t_kernel(tc, h_node, h_ngbrs, alpha, Wq, bq, Ww, bw, out):
     nc = tc.nc
     with ExitStack() as ctx:
         const = ctx.enter_context(tc.tile_pool(name="const", bufs=1))
-        xin = ctx.enter_context(tc.tile_pool(name="xin", bufs=6))
-        grp = ctx.enter_context(tc.tile_pool(name="grp", bufs=4))
-        qnt = ctx.enter_context(tc.tile_pool(name="qnt", bufs=4))
-        ypool = ctx.enter_context(tc.tile_pool(name="ypool", bufs=4))
-        epool = ctx.enter_context(tc.tile_pool(name="epool", bufs=8))
-        tail = ctx.enter_context(tc.tile_pool(name="tail", bufs=2))
+        xin = ctx.enter_context(tc.tile_pool(name="xin", bufs=5))
+        grp = ctx.enter_context(tc.tile_pool(name="grp", bufs=3))
+        qnt = ctx.enter_context(tc.tile_pool(name="qnt", bufs=3))
+        ypool = ctx.enter_context(tc.tile_pool(name="ypool", bufs=3))
+        epool = ctx.enter_context(tc.tile_pool(name="epool", bufs=4))
+        prep = ctx.enter_context(tc.tile_pool(name="prep", bufs=2))
+        tail = ctx.enter_context(tc.tile_pool(name="tail", bufs=1))
         pz = ctx.enter_context(tc.psum_pool(name="pz", bufs=4))
         pe = ctx.enter_context(tc.psum_pool(name="pe", bufs=3))
         pa = ctx.enter_context(tc.psum_pool(name="pa", bufs=1))
@@ -128,9 +143,9 @@ def tile_pinsageconv_t_kernel(tc, h_node, h_ngbrs, alpha, Wq, bq, Ww, bw, out):
                     )
             return xt
 
-        def words_copy(xt, grouped, half, copy):
+        def words_copy(xt, grouped, half, copy, first=0):
             copy(
-                out=grouped[:].bitcast(F32)[:, 2 * half * P : (2 * half + 2) * P, :].rearrange(
+                out=grouped[:].bitcast(F32)[:, first + 2 * half * P : first + (2 * half + 2) * P, :].rearrange(
                     "p (b c) u -> p b c u", b=2
                 ),
                 in_=xt[:].rearrange("p b u c -> p b c u"),
@@ -155,7 +170,7 @@ def tile_pinsageconv_t_kernel(tc, h_node, h_ngbrs, alpha, Wq, bq, Ww, bw, out):
 
         def prep_T(i):
             if i % 4 == 0 or i == 2:
-                prep_g[i] = const.tile([P, 4 * P, 4], BF16, align_bytes=64, name="prep_g%d" % i)
+                prep_g[i] = prep.tile([P, 4 * P, 4], BF16, align_bytes=64, tag="prep_g", name="prep_g")
             if i < 2:
                 prep_ps[i] = words_T(ww_raw[:].bitcast(F32)[:, :, 0 : D_IN // 2], i, pe, "eT")
             elif i < 4:
@@ -200,48 +215,65 @@ def tile_pinsageconv_t_kernel(tc, h_node, h_ngbrs, alpha, Wq, bq, Ww, bw, out):
         acc = {}
 
         def x_T(qd, half, pool=pe, tag="eT"):
-            if half == 0:
-                grouped[qd] = grp.tile([P, 4 * P, 4], BF16, align_bytes=64, tag="grouped", name="grouped")
+            if half == 0 and pair_of(qd)[0] == qd:
+                n = pair_of(qd)[1]
+                grouped[qd] = grp.tile([P, n * KQ * P, 4], BF16, align_bytes=64, tag="grouped", name="grouped")
             xt_ps[(qd, half)] = words_T(x_sb[qd][:].bitcast(F32), half, pool, tag)
 
         def x_copy(qd, half, copy=nc.scalar.copy):
-            words_copy(xt_ps[(qd, half)], grouped[qd], half, copy)
+            lead = pair_of(qd)[0]
+            words_copy(xt_ps[(qd, half)], grouped[lead], half, copy, (qd - lead) * KQ * P)
 
         def x_quant(qd):
-            x_c[qd] = qnt.tile([P, KQ * P], U32, align_bytes=64, name="x_c")
-            x_s[qd] = qnt.tile([P, KQ * P], U8, align_bytes=64, name="x_s")
-            quantise(grouped[qd], x_c[qd][:], x_s[qd][:])
+            n = pair_of(qd)[1]
+            codes = qnt.tile([P, n * KQ * P], U32, align_bytes=64, name="x_c")
+            scales = qnt.tile([P, n * KQ * P], U8, align_bytes=64, name="x_s")
+            quantise(grouped[qd], codes[:], scales[:])
+            for j in range(n):
+                x_c[qd + j] = codes[:, j * KQ * P : (j + 1) * KQ * P]
+                x_s[qd + j] = scales[:, j * KQ * P : (j + 1) * KQ * P]
 
         def mx(qd, hc):
+            if hc == 0:
+                e_sb[qd] = epool.tile([P, HC + 1, KQ * P], F32, name="e")
             cols = slice(hc * P, (hc + 1) * P)
             z_ps[hc] = pz.tile([P, KQ * P], F32, tag="z", name="z")
             nc.tensor.matmul_mx(
                 out=z_ps[hc][:], lhsT=wq_c[:, cols].bitcast(FP8X4), lhsT_scale=wq_s[:, cols],
-                rhs=x_c[qd][:].bitcast(FP8X4), rhs_scale=x_s[qd][:], start=True, stop=True,
+                rhs=x_c[qd].bitcast(FP8X4), rhs_scale=x_s[qd], start=True, stop=True,
             )
 
-        def low(hc):
+        def low(qd, hc):
+            if alone(qd, hc):
+                nc.scalar.activation(
+                    out=e_sb[qd][:, hc, :], in_=z_ps[hc][:], func=ACT.Relu, bias=b_high[:, hc : hc + 1],
+                    scale=1.0 - SLOPE,
+                )
+                nc.scalar.activation(
+                    out=e_sb[qd][:, HC, :], in_=z_ps[hc][:], func=ACT.Identity, bias=b_low[:, hc : hc + 1],
+                    scale=SLOPE,
+                )
+                return
             y_sb[hc] = ypool.tile([P, KQ * P], F32, name="y")
             nc.scalar.activation(
                 out=y_sb[hc][:], in_=z_ps[hc][:], func=ACT.Identity, bias=b_low[:, hc : hc + 1], scale=SLOPE
             )
 
         def lrelu(qd, hc):
-            pair, i = divmod(hc, 2)
-            if i == 0:
-                e_sb[(qd, pair)] = epool.tile([P, 2, KQ * P], F32, name="e")
+            if alone(qd, hc):
+                return
             nc.vector.scalar_tensor_tensor(
-                out=e_sb[(qd, pair)][:, i, :], in0=z_ps[hc][:], scalar=b_col[:, hc : hc + 1], in1=y_sb[hc][:],
+                out=e_sb[qd][:, hc, :], in0=z_ps[hc][:], scalar=b_col[:, hc : hc + 1], in1=y_sb[hc][:],
                 op0=ALU.add, op1=ALU.max,
             )
 
-        def weigh(qd, pair):
-            n = weighed(qd, pair) * P
+        def weigh(qd, lo, hi):
+            n = weighed(qd, lo // 2) * P
+            hi += hi == HC and alone(qd, HC - 1)
             if n:
-                e = e_sb[(qd, pair)]
+                e = e_sb[qd][:, lo:hi, 0:n]
                 nc.gpsimd.tensor_tensor(
-                    out=e[:, :, 0:n], in0=e[:, :, 0:n],
-                    in1=a_bc[:, qd, 0:n].unsqueeze(1).to_broadcast([P, 2, n]), op=ALU.mult,
+                    out=e, in0=e, in1=a_bc[:, qd, 0:n].unsqueeze(1).to_broadcast([P, hi - lo, n]), op=ALU.mult
                 )
 
         def sum_T(qd, hc):
@@ -250,21 +282,23 @@ def tile_pinsageconv_t_kernel(tc, h_node, h_ngbrs, alpha, Wq, bq, Ww, bw, out):
             first = n > 0 and g not in sum_ps
             if first:
                 sum_ps[g] = pa.tile([P, D_HID], F32, tag="sum", name="sum")
-            for kk in range(n):
+            parts = [(part, kk) for part in parts_of(qd, hc) for kk in range(n)]
+            for i, (part, kk) in enumerate(parts):
                 nc.tensor.matmul(
                     out=sum_ps[g][:, hc * P : (hc + 1) * P],
-                    lhsT=e_sb[(qd, hc // 2)][:, hc % 2, kk * P : (kk + 1) * P],
-                    rhs=ident_f[:], is_transpose=True, start=(first and kk == 0),
-                    stop=(q == QUADS - 1 and hc == HC - 1 and kk == n - 1),
+                    lhsT=e_sb[qd][:, part, kk * P : (kk + 1) * P],
+                    rhs=ident_f[:], is_transpose=True, start=(first and i == 0),
+                    stop=(q == QUADS - 1 and hc == HC - 1 and i == len(parts) - 1),
                 )
 
         def tk(qd, kk, lo, hi):
             eT_ps[(qd, kk)] = pe.tile([P, D_HID], F32, tag="eT", name="eT")
-            for hc in range(lo, hi):
+            parts = [(part, hc) for hc in range(lo, hi) for part in parts_of(qd, hc)]
+            for i, (part, hc) in enumerate(parts):
                 nc.tensor.matmul(
                     out=eT_ps[(qd, kk)][:, hc * P : (hc + 1) * P],
-                    lhsT=e_sb[(qd, hc // 2)][:, hc % 2, kk * P : (kk + 1) * P],
-                    rhs=ident_f[:], is_transpose=True, start=(hc == lo), stop=(hc == hi - 1),
+                    lhsT=e_sb[qd][:, part, kk * P : (kk + 1) * P],
+                    rhs=ident_f[:], is_transpose=True, start=(i == 0), stop=(i == len(parts) - 1),
                 )
 
         def fma(qd, kk, lo, hi):
@@ -329,19 +363,22 @@ def tile_pinsageconv_t_kernel(tc, h_node, h_ngbrs, alpha, Wq, bq, Ww, bw, out):
             )
 
         def l2_bias(g):
+            zc = tail.tile([P, D_OUT], F32, name="zc")
+            nc.scalar.copy(out=zc[:], in_=s2[(g, "z2")][:])
             v2 = tail.tile([P, D_OUT], F32, name="v2")
-            nc.vector.tensor_tensor(out=v2[:], in0=s2[(g, "z2")][:], in1=bw_bc[:], op=ALU.add)
+            nc.gpsimd.tensor_tensor(out=v2[:], in0=zc[:], in1=bw_bc[:], op=ALU.add)
             s2[(g, "v2")] = v2
 
         def l2_lrelu(g):
-            h2 = tail.tile([P, D_OUT], F32, name="h2")
             v2 = s2[(g, "v2")]
-            nc.vector.scalar_tensor_tensor(
-                out=h2[:], in0=v2[:], scalar=SLOPE, in1=v2[:], op0=ALU.mult, op1=ALU.max
-            )
+            high = tail.tile([P, D_OUT], F32, name="high")
+            nc.scalar.activation(out=high[:], in_=v2[:], func=ACT.Relu, scale=1.0 - SLOPE)
+            nc.scalar.activation(out=v2[:], in_=v2[:], func=ACT.Copy, scale=SLOPE)
+            h2 = tail.tile([P, D_OUT], F32, name="h2")
+            nc.gpsimd.tensor_tensor(out=h2[:], in0=high[:], in1=v2[:], op=ALU.add)
             s2[(g, "h2")] = h2
 
-        def l2_norm_s(g):
+        def l2_norm(g):
             sq = tail.tile([P, D_OUT], F32, name="sq")
             ss = tail.tile([P, 1], F32, name="ss")
             nc.scalar.activation(out=sq[:], in_=s2[(g, "h2")][:], func=ACT.Square, accum_out=ss[:])
@@ -351,21 +388,43 @@ def tile_pinsageconv_t_kernel(tc, h_node, h_ngbrs, alpha, Wq, bq, Ww, bw, out):
 
         def l2_res(g):
             res = tail.tile([P, D_OUT], F32, name="res")
-            if g < GROUPS - 1:
-                nc.scalar.activation(
-                    out=res[:], in_=s2[(g, "h2")][:], func=ACT.Copy, scale=s2[(g, "rs")][:, 0:1]
-                )
-            else:
-                nc.vector.tensor_scalar(
-                    out=res[:], in0=s2[(g, "h2")][:], scalar1=s2[(g, "rs")][:, 0:1], scalar2=None, op0=ALU.mult
-                )
-            s2[(g, "res")] = res
+            nc.gpsimd.tensor_scalar(
+                out=res[:], in0=s2[(g, "h2")][:], scalar1=s2[(g, "rs")][:, 0:1], scalar2=0.0,
+                op0=ALU.mult, op1=ALU.add,
+            )
+            nc.sync.dma_start(out=out[g * P : (g + 1) * P, :], in_=res[:])
 
-        def l2_store(g):
-            nc.sync.dma_start(out=out[g * P : (g + 1) * P, :], in_=s2[(g, "res")][:])
+        def l2_end(g):
+            halves = [slice(0, D_OUT // 2), slice(D_OUT // 2, D_OUT)]
+            z2 = s2[(g, "z2")]
+            v2 = tail.tile([P, D_OUT], F32, name="v2")
+            h2 = tail.tile([P, D_OUT], F32, name="h2")
+            sq = tail.tile([P, D_OUT], F32, name="sq")
+            ss = [tail.tile([P, 1], F32, name="ss0"), tail.tile([P, 1], F32, name="ss1")]
+            for cols in halves:
+                nc.vector.tensor_tensor(out=v2[:, cols], in0=z2[:, cols], in1=bw_bc[:, cols], op=ALU.add)
+            for i, cols in enumerate(halves):
+                nc.vector.scalar_tensor_tensor(
+                    out=h2[:, cols], in0=v2[:, cols], scalar=SLOPE, in1=v2[:, cols], op0=ALU.mult, op1=ALU.max
+                )
+                nc.scalar.activation(out=sq[:, cols], in_=h2[:, cols], func=ACT.Square, accum_out=ss[i][:])
+            ssum = tail.tile([P, 1], F32, name="ssum")
+            nc.vector.tensor_scalar(
+                out=ssum[:], in0=ss[0][:], scalar1=ss[1][:, 0:1], scalar2=TINY, op0=ALU.add, op1=ALU.add
+            )
+            rs = tail.tile([P, 1], F32, name="rs")
+            nc.scalar.activation(out=rs[:], in_=ssum[:], func=ACT.Abs_reciprocal_sqrt)
+            res = [tail.tile([P, D_OUT // 2], F32, name="res0"), tail.tile([P, D_OUT // 2], F32, name="res1")]
+            nc.vector.tensor_scalar(
+                out=res[0][:], in0=h2[:, halves[0]], scalar1=rs[:, 0:1], scalar2=None, op0=ALU.mult
+            )
+            nc.sync.dma_start(out=out[g * P : (g + 1) * P, halves[0]], in_=res[0][:])
+            nc.scalar.activation(out=res[1][:], in_=h2[:, halves[1]], func=ACT.Copy, scale=rs[:, 0:1])
+            nc.scalar.dma_start(out=out[g * P : (g + 1) * P, halves[1]], in_=res[1][:])
 
         b_col = const.tile([P, HC], F32)
         b_low = const.tile([P, HC], F32)
+        b_high = const.tile([P, HC], F32)
         a_f = const.tile([P, GROUPS, K_NGB], F32)
         a_sum = const.tile([P, GROUPS], F32)
         a_den = const.tile([P, GROUPS], F32)
@@ -399,6 +458,7 @@ def tile_pinsageconv_t_kernel(tc, h_node, h_ngbrs, alpha, Wq, bq, Ww, bw, out):
         nc.tensor.transpose(bT[:], b_rows[:], ident_b[:])
         nc.vector.tensor_copy(out=b_col[:], in_=bT[:, 0:HC])
         nc.vector.tensor_scalar(out=b_low[:], in0=b_col[:], scalar1=SLOPE, scalar2=None, op0=ALU.mult)
+        nc.vector.tensor_scalar(out=b_high[:], in0=b_col[:], scalar1=1.0 - SLOPE, scalar2=None, op0=ALU.mult)
         for qd in range(1, AHEAD):
             for half in range(2):
                 x_T(qd, half)
@@ -422,10 +482,10 @@ def tile_pinsageconv_t_kernel(tc, h_node, h_ngbrs, alpha, Wq, bq, Ww, bw, out):
             return None
 
         late = []
-        for i in range(NQ + 6 + SUM_LAG):
-            run = i < NQ
+        summed = set()
+        for i in range(NQ):
             old = i - 1
-            own = left(old) if 0 <= old < NQ else []
+            own = left(old) if old >= 0 else []
             cut = (len(own) + 1) // 2
             nxt = i + AHEAD if i + AHEAD < NQ else None
             if i == 0:
@@ -437,41 +497,49 @@ def tile_pinsageconv_t_kernel(tc, h_node, h_ngbrs, alpha, Wq, bq, Ww, bw, out):
             if i + FIRST_LOADS < NQ:
                 load(i + FIRST_LOADS)
             late_loads(i)
-            b = SUM_LAG - 1
-            g1, g2, g3, g4, g5, g6, g7 = (due(i, lag + b) for lag in LAGS)
+            g1, g2, g3, g4, g5 = (due(i, lag + SUM_LAG) for lag in (0, 1, 2, 4, 5))
             if g1 is not None:
                 l2_sum(g1)
             if g2 is not None:
                 l2_copy(g2)
-            if run:
-                for hc in range(HC):
-                    mx(i, hc)
-            if g3 is not None:
-                l2_mx0(g3)
-                l2_mx1(g3)
-            if nxt is not None:
-                x_T(nxt, 0)
-                x_T(nxt, 1)
-            for piece in own[:cut]:
-                tk(old, *piece)
-            if 0 <= i - SUM_LAG < NQ:
-                for hc in range(HC):
-                    sum_T(i - SUM_LAG, hc)
-            for piece in own[cut:]:
-                tk(old, *piece)
-            if g1 is not None:
-                l2_T(g1)
-            if 0 <= i - PREP0 < 8:
-                prep_T(i - PREP0)
+            for what in PORDER:
+                if what[0] == "M":
+                    for hc in range(int(what[1]), int(what[2])):
+                        mx(i, hc)
+                elif what == "Z" and g3 is not None:
+                    l2_mx0(g3)
+                    l2_mx1(g3)
+                elif what[0] == "X" and nxt is not None:
+                    x_T(nxt, int(what[1]))
+                elif what == "K":
+                    for piece in own[:cut]:
+                        tk(old, *piece)
+                elif what == "k":
+                    for piece in own[cut:]:
+                        tk(old, *piece)
+                elif what == "j":
+                    for piece in late:
+                        tk(*piece)
+                elif what[0] == "S" and i >= int(what[3]):
+                    for hc in range(int(what[1]), int(what[2])):
+                        sum_T(i - int(what[3]), hc)
+                        summed.add((i - int(what[3]), hc))
+                elif what == "T" and g1 is not None:
+                    l2_T(g1)
+                elif what == "P" and 0 <= i - PREP0 < 8:
+                    prep_T(i - PREP0)
             for what in ORDER:
-                if what[0] == "y" and run:
-                    low(int(what[1]))
+                if what[0] == "y":
+                    low(i, int(what[1]))
+                elif what == "d":
+                    if (i + AHEAD - 1, 1) in xt_ps and i > 0:
+                        x_copy(i + AHEAD - 1, 1)
                 elif what[0] == "c" and nxt is not None:
                     x_copy(nxt, int(what[1]))
-                elif what[0] == "e" and run:
+                elif what[0] == "e":
                     lrelu(i, int(what[1]))
-                elif what[0] == "w" and run:
-                    weigh(i, int(what[1]))
+                elif what[0] == "w":
+                    weigh(i, int(what[1]), int(what[2]))
                 elif what == "L":
                     for piece in late:
                         fma(*piece)
@@ -481,22 +549,46 @@ def tile_pinsageconv_t_kernel(tc, h_node, h_ngbrs, alpha, Wq, bq, Ww, bw, out):
                 elif what == "Q":
                     if i == 0:
                         for qd in range(1, QA):
-                            x_quant(qd)
-                    if i + QA < NQ:
+                            if pair_of(qd)[0] == qd:
+                                x_quant(qd)
+                    if i + QA < NQ and pair_of(i + QA)[0] == i + QA:
                         x_quant(i + QA)
                     if g2 is not None:
                         l2_quant(g2)
                     if 0 <= i - PREP0 - 1 < 8:
                         prep_quant(i - PREP0 - 1)
-                elif what == "l" and g4 is not None:
-                    l2_lrelu(g4)
-                elif what == "b" and g3 is not None:
-                    l2_bias(g3)
-                elif what == "p" and 0 <= i - PREP0 < 8:
-                    prep_copy(i - PREP0)
-                elif what == "n" and g5 is not None:
-                    l2_norm_s(g5)
-                elif what == "r" and g7 is not None:
-                    l2_res(g7)
-                    l2_store(g7)
+            if g3 is not None:
+                l2_bias(g3)
+            if g4 is not None:
+                l2_lrelu(g4)
+            if g5 is not None:
+                l2_norm(g5)
+                l2_res(g5)
+            if 0 <= i - PREP0 < 8:
+                prep_copy(i - PREP0)
             late = [(old,) + piece for piece in own[cut:]]
+
+        g = GROUPS - 1
+        for qd in range(NQ - 4, NQ - 1):
+            for hc in range(HC):
+                if (qd, hc) not in summed:
+                    sum_T(qd, hc)
+        if "j" in PORDER:
+            for piece in late:
+                tk(*piece)
+        own = left(NQ - 1)
+        for piece in own:
+            tk(NQ - 1, *piece)
+        for hc in range(HC):
+            sum_T(NQ - 1, hc)
+        l2_mx0(g)
+        for piece in late:
+            fma(*piece)
+        for piece in own:
+            fma(NQ - 1, *piece)
+        l2_sum(g)
+        l2_T(g)
+        l2_copy(g)
+        l2_quant(g)
+        l2_mx1(g)
+        l2_end(g)

@@ -24,12 +24,12 @@ HC = D_HID // P
 PARK = N_NODES - NQ
 ALONE = (0, 1)
 SHARE_EVEN = (2, 2)
-SHARE_ODD = (3, 3)
-SUM_LAG = 2
+SHARE_ODD = (2, 2)
+SUM_LAG = 3
 LONE = 2
 QA = 1
-ORDER = "d y0 y1 c0 y2 y3 e0 w01 Q L e1 w12 e2 w23 e3 w34 E".split(" ")
-PORDER = "Z M02 j X0 S242 M24 X1 P T K S021".split(" ")
+ORDER = "d y0 y1 c0 y2 y3 Q e0 w01 e1 w12 L e2 w23 e3 w34 E".split(" ")
+PORDER = "M02 S023 X0 j M24 T X1 P Z S243 K".split(" ")
 AHEAD = QA + 2
 PREP0 = 2
 FIRST_LOADS = 5
@@ -70,12 +70,13 @@ def tile_pinsageconv_t_kernel(tc, h_node, h_ngbrs, alpha, Wq, bq, Ww, bw, out):
     nc = tc.nc
     with ExitStack() as ctx:
         const = ctx.enter_context(tc.tile_pool(name="const", bufs=1))
-        xin = ctx.enter_context(tc.tile_pool(name="xin", bufs=5))
+        xin = ctx.enter_context(tc.tile_pool(name="xin", bufs=6))
         grp = ctx.enter_context(tc.tile_pool(name="grp", bufs=3))
         qnt = ctx.enter_context(tc.tile_pool(name="qnt", bufs=3))
-        ypool = ctx.enter_context(tc.tile_pool(name="ypool", bufs=3))
-        epool = ctx.enter_context(tc.tile_pool(name="epool", bufs=4))
+        ypool = ctx.enter_context(tc.tile_pool(name="ypool", bufs=4))
+        epool = ctx.enter_context(tc.tile_pool(name="epool", bufs=6))
         prep = ctx.enter_context(tc.tile_pool(name="prep", bufs=2))
+        wgt = ctx.enter_context(tc.tile_pool(name="wgt", bufs=8))
         tail = ctx.enter_context(tc.tile_pool(name="tail", bufs=1))
         pz = ctx.enter_context(tc.psum_pool(name="pz", bufs=4))
         pe = ctx.enter_context(tc.psum_pool(name="pe", bufs=3))
@@ -235,7 +236,7 @@ def tile_pinsageconv_t_kernel(tc, h_node, h_ngbrs, alpha, Wq, bq, Ww, bw, out):
 
         def mx(qd, hc):
             if hc == 0:
-                e_sb[qd] = epool.tile([P, HC + 1, KQ * P], F32, name="e")
+                e_sb[qd] = epool.tile([P, HC + (ALONE[0] > 0), KQ * P], F32, name="e")
             cols = slice(hc * P, (hc + 1) * P)
             z_ps[hc] = pz.tile([P, KQ * P], F32, tag="z", name="z")
             nc.tensor.matmul_mx(
@@ -273,7 +274,7 @@ def tile_pinsageconv_t_kernel(tc, h_node, h_ngbrs, alpha, Wq, bq, Ww, bw, out):
             if n:
                 e = e_sb[qd][:, lo:hi, 0:n]
                 nc.gpsimd.tensor_tensor(
-                    out=e, in0=e, in1=a_bc[:, qd, 0:n].unsqueeze(1).to_broadcast([P, hi - lo, n]), op=ALU.mult
+                    out=e, in0=e, in1=a_bc[qd][:, 0:n].unsqueeze(1).to_broadcast([P, hi - lo, n]), op=ALU.mult
                 )
 
         def sum_T(qd, hc):
@@ -430,7 +431,7 @@ def tile_pinsageconv_t_kernel(tc, h_node, h_ngbrs, alpha, Wq, bq, Ww, bw, out):
         a_den = const.tile([P, GROUPS], F32)
         a_rec = const.tile([P, GROUPS], F32)
         a_n = const.tile([P, GROUPS, K_NGB], F32)
-        a_bc = const.tile([P, NQ, KQ * P], F32)
+        a_bc = {}
         aT_sb = const.tile([P, P], F32, name="aT_sb")
 
         wq_g = grp.tile([P, 4 * P, 4], BF16, align_bytes=64, tag="grouped", name="wq_g")
@@ -473,7 +474,8 @@ def tile_pinsageconv_t_kernel(tc, h_node, h_ngbrs, alpha, Wq, bq, Ww, bw, out):
             )
 
         def load_weights(qd):
-            nc.sync.dma_start(out=a_bc[:, qd, :], in_=out[PARK + qd, :].partition_broadcast(P))
+            a_bc[qd] = wgt.tile([P, KQ * P], F32, name="a_bc")
+            nc.sync.dma_start(out=a_bc[qd][:], in_=out[PARK + qd, :].partition_broadcast(P))
 
         def due(i, lag):
             g, r = divmod(i - lag, QUADS)
@@ -497,7 +499,7 @@ def tile_pinsageconv_t_kernel(tc, h_node, h_ngbrs, alpha, Wq, bq, Ww, bw, out):
             if i + FIRST_LOADS < NQ:
                 load(i + FIRST_LOADS)
             late_loads(i)
-            g1, g2, g3, g4, g5 = (due(i, lag + SUM_LAG) for lag in (0, 1, 2, 4, 5))
+            g1, g2, g3, g4, g5 = (due(i, lag + SUM_LAG) for lag in (0, 1, 2, 3, 4))
             if g1 is not None:
                 l2_sum(g1)
             if g2 is not None:
@@ -569,7 +571,7 @@ def tile_pinsageconv_t_kernel(tc, h_node, h_ngbrs, alpha, Wq, bq, Ww, bw, out):
             late = [(old,) + piece for piece in own[cut:]]
 
         g = GROUPS - 1
-        for qd in range(NQ - 4, NQ - 1):
+        for qd in range(NQ - 5, NQ - 1):
             for hc in range(HC):
                 if (qd, hc) not in summed:
                     sum_T(qd, hc)

@@ -24,22 +24,25 @@ HC = D_HID // P
 PARK = N_NODES - NQ
 ALONE = (0, 1)
 SHARE_EVEN = (2, 2)
-SHARE_ODD = (2, 2)
+SHARE_ODD = (3, 2)
 SUM_LAG = 3
+L2V = 0
 LONE = 2
 QA = 1
-ORDER = "d y0 y1 c0 y2 y3 Q e0 w01 e1 w12 L e2 w23 e3 w34 E".split(" ")
-PORDER = "M02 S023 X0 j M24 T X1 P Z S243 K".split(" ")
+ORDER = "d y0 y1 c0 y2 y3 e0 e1 w02 Q L e2 e3 w24 E".split(" ")
+PORDER = "M02 X0 M24 j T P S023 Z S243 X1 K".split(" ")
 AHEAD = QA + 2
 PREP0 = 2
-FIRST_LOADS = 5
-G_FIRST = 0
+FIRST_LOADS = 6
+G_FIRST = 1
 WAHEAD = 3
 
 FLOPS = 2 * N_NODES * K_NGB * D_IN * D_HID + 2 * N_NODES * (D_IN + D_HID) * D_OUT
 
 
 def weighed(qd, pair):
+    if qd < G_FIRST:
+        return 0
     return (SHARE_ODD if qd % 2 else SHARE_EVEN)[pair]
 
 
@@ -70,9 +73,9 @@ def tile_pinsageconv_t_kernel(tc, h_node, h_ngbrs, alpha, Wq, bq, Ww, bw, out):
     nc = tc.nc
     with ExitStack() as ctx:
         const = ctx.enter_context(tc.tile_pool(name="const", bufs=1))
-        xin = ctx.enter_context(tc.tile_pool(name="xin", bufs=6))
-        grp = ctx.enter_context(tc.tile_pool(name="grp", bufs=3))
-        qnt = ctx.enter_context(tc.tile_pool(name="qnt", bufs=3))
+        xin = ctx.enter_context(tc.tile_pool(name="xin", bufs=7))
+        grp = ctx.enter_context(tc.tile_pool(name="grp", bufs=4))
+        qnt = ctx.enter_context(tc.tile_pool(name="qnt", bufs=4))
         ypool = ctx.enter_context(tc.tile_pool(name="ypool", bufs=4))
         epool = ctx.enter_context(tc.tile_pool(name="epool", bufs=6))
         prep = ctx.enter_context(tc.tile_pool(name="prep", bufs=2))
@@ -364,6 +367,11 @@ def tile_pinsageconv_t_kernel(tc, h_node, h_ngbrs, alpha, Wq, bq, Ww, bw, out):
             )
 
         def l2_bias(g):
+            if L2V:
+                v2 = tail.tile([P, D_OUT], F32, name="v2")
+                nc.vector.tensor_tensor(out=v2[:], in0=s2[(g, "z2")][:], in1=bw_bc[:], op=ALU.add)
+                s2[(g, "v2")] = v2
+                return
             zc = tail.tile([P, D_OUT], F32, name="zc")
             nc.scalar.copy(out=zc[:], in_=s2[(g, "z2")][:])
             v2 = tail.tile([P, D_OUT], F32, name="v2")
@@ -372,6 +380,13 @@ def tile_pinsageconv_t_kernel(tc, h_node, h_ngbrs, alpha, Wq, bq, Ww, bw, out):
 
         def l2_lrelu(g):
             v2 = s2[(g, "v2")]
+            if L2V == 2:
+                h2 = tail.tile([P, D_OUT], F32, name="h2")
+                nc.vector.scalar_tensor_tensor(
+                    out=h2[:], in0=v2[:], scalar=SLOPE, in1=v2[:], op0=ALU.mult, op1=ALU.max
+                )
+                s2[(g, "h2")] = h2
+                return
             high = tail.tile([P, D_OUT], F32, name="high")
             nc.scalar.activation(out=high[:], in_=v2[:], func=ACT.Relu, scale=1.0 - SLOPE)
             nc.scalar.activation(out=v2[:], in_=v2[:], func=ACT.Copy, scale=SLOPE)
@@ -389,6 +404,12 @@ def tile_pinsageconv_t_kernel(tc, h_node, h_ngbrs, alpha, Wq, bq, Ww, bw, out):
 
         def l2_res(g):
             res = tail.tile([P, D_OUT], F32, name="res")
+            if L2V:
+                nc.scalar.activation(
+                    out=res[:], in_=s2[(g, "h2")][:], func=ACT.Copy, scale=s2[(g, "rs")][:, 0:1]
+                )
+                nc.sync.dma_start(out=out[g * P : (g + 1) * P, :], in_=res[:])
+                return
             nc.gpsimd.tensor_scalar(
                 out=res[:], in0=s2[(g, "h2")][:], scalar1=s2[(g, "rs")][:, 0:1], scalar2=0.0,
                 op0=ALU.mult, op1=ALU.add,
@@ -463,7 +484,7 @@ def tile_pinsageconv_t_kernel(tc, h_node, h_ngbrs, alpha, Wq, bq, Ww, bw, out):
         for qd in range(1, AHEAD):
             for half in range(2):
                 x_T(qd, half)
-                x_copy(qd, half)
+                x_copy(qd, half, nc.vector.tensor_copy if qd == 1 else nc.scalar.copy)
 
         def park_weights():
             aT = pe.tile([P, P], F32, tag="eT", name="aT")
@@ -490,15 +511,8 @@ def tile_pinsageconv_t_kernel(tc, h_node, h_ngbrs, alpha, Wq, bq, Ww, bw, out):
             own = left(old) if old >= 0 else []
             cut = (len(own) + 1) // 2
             nxt = i + AHEAD if i + AHEAD < NQ else None
-            if i == 0:
-                park_weights()
-                for qd in range(G_FIRST, G_FIRST + WAHEAD):
-                    load_weights(qd)
-            elif i + G_FIRST + WAHEAD - 1 < NQ:
-                load_weights(i + G_FIRST + WAHEAD - 1)
             if i + FIRST_LOADS < NQ:
                 load(i + FIRST_LOADS)
-            late_loads(i)
             g1, g2, g3, g4, g5 = (due(i, lag + SUM_LAG) for lag in (0, 1, 2, 3, 4))
             if g1 is not None:
                 l2_sum(g1)
@@ -508,6 +522,8 @@ def tile_pinsageconv_t_kernel(tc, h_node, h_ngbrs, alpha, Wq, bq, Ww, bw, out):
                 if what[0] == "M":
                     for hc in range(int(what[1]), int(what[2])):
                         mx(i, hc)
+                    if i == 0 and what == "M02":
+                        park_weights()
                 elif what == "Z" and g3 is not None:
                     l2_mx0(g3)
                     l2_mx1(g3)
@@ -530,6 +546,12 @@ def tile_pinsageconv_t_kernel(tc, h_node, h_ngbrs, alpha, Wq, bq, Ww, bw, out):
                     l2_T(g1)
                 elif what == "P" and 0 <= i - PREP0 < 8:
                     prep_T(i - PREP0)
+            if i == 0:
+                for qd in range(G_FIRST, G_FIRST + WAHEAD):
+                    load_weights(qd)
+            elif i + G_FIRST + WAHEAD - 1 < NQ:
+                load_weights(i + G_FIRST + WAHEAD - 1)
+            late_loads(i)
             for what in ORDER:
                 if what[0] == "y":
                     low(i, int(what[1]))

@@ -15,35 +15,26 @@ AX = mybir.AxisListType
 P = 128
 N_NODES, K_NGB, D_IN, D_HID, D_OUT = 512, 32, 512, 512, 512
 SLOPE = 0.01
-TINY = 1e-37
+TINY = 1e-19
 GROUPS = N_NODES // P
 KQ = 4
 QUADS = K_NGB // KQ
 NQ = GROUPS * QUADS
 HC = D_HID // P
-PARK = N_NODES - NQ
-ALONE = (0, 1)
-SHARE_EVEN = (2, 2)
-SHARE_ODD = (3, 2)
-SUM_LAG = 3
+KINDS = ("VVRA",)
+SUM_LAG = 2
 L2V = 0
+L2G = 0
+LAST_S = (0, 2, 3)
 LONE = 2
 QA = 1
-ORDER = "d y0 y1 c0 y2 y3 e0 e1 w02 Q L e2 e3 w24 E".split(" ")
-PORDER = "M02 X0 M24 j T P S023 Z S243 X1 K".split(" ")
+ORDER = "d y0 y1 c0 y2 y3 F2 Q e02 F3 e24 r F0 F1".split(" ")
+PORDER = "M02 j2 X0 X1 M24 Z K3 T K0 P K1".split(" ")
 AHEAD = QA + 2
 PREP0 = 2
 FIRST_LOADS = 6
-G_FIRST = 1
-WAHEAD = 3
 
 FLOPS = 2 * N_NODES * K_NGB * D_IN * D_HID + 2 * N_NODES * (D_IN + D_HID) * D_OUT
-
-
-def weighed(qd, pair):
-    if qd < G_FIRST:
-        return 0
-    return (SHARE_ODD if qd % 2 else SHARE_EVEN)[pair]
 
 
 def pair_of(qd):
@@ -52,21 +43,17 @@ def pair_of(qd):
     return qd - (qd - LONE) % 2, 2
 
 
-def alone(qd, hc):
-    return hc == HC - 1 and qd % ALONE[1] < ALONE[0]
+def kind(qd, hc):
+    return KINDS[qd % len(KINDS)][hc]
+
+
+def span(qd, what):
+    mine = [hc for hc in range(HC) if kind(qd, hc) == what]
+    return (mine[0], mine[-1] + 1) if mine else (0, 0)
 
 
 def parts_of(qd, hc):
-    return (hc, HC) if alone(qd, hc) else (hc,)
-
-
-def left(qd):
-    res = []
-    for kk in range(KQ - 1, -1, -1):
-        pairs = [pair for pair in range(2) if weighed(qd, pair) <= kk]
-        if pairs:
-            res.append((kk, 2 * pairs[0], 2 * pairs[-1] + 2))
-    return res
+    return (hc,) if kind(qd, hc) == "V" else (hc, hc + 2)
 
 
 def tile_pinsageconv_t_kernel(tc, h_node, h_ngbrs, alpha, Wq, bq, Ww, bw, out):
@@ -76,14 +63,11 @@ def tile_pinsageconv_t_kernel(tc, h_node, h_ngbrs, alpha, Wq, bq, Ww, bw, out):
         xin = ctx.enter_context(tc.tile_pool(name="xin", bufs=7))
         grp = ctx.enter_context(tc.tile_pool(name="grp", bufs=4))
         qnt = ctx.enter_context(tc.tile_pool(name="qnt", bufs=4))
-        ypool = ctx.enter_context(tc.tile_pool(name="ypool", bufs=4))
-        epool = ctx.enter_context(tc.tile_pool(name="epool", bufs=6))
+        epool = ctx.enter_context(tc.tile_pool(name="epool", bufs=4))
         prep = ctx.enter_context(tc.tile_pool(name="prep", bufs=2))
-        wgt = ctx.enter_context(tc.tile_pool(name="wgt", bufs=8))
         tail = ctx.enter_context(tc.tile_pool(name="tail", bufs=1))
-        pz = ctx.enter_context(tc.psum_pool(name="pz", bufs=4))
-        pe = ctx.enter_context(tc.psum_pool(name="pe", bufs=3))
-        pa = ctx.enter_context(tc.psum_pool(name="pa", bufs=1))
+        pz = ctx.enter_context(tc.psum_pool(name="pz", bufs=3))
+        pe = ctx.enter_context(tc.psum_pool(name="pe", bufs=5))
         ctx.enter_context(tc.manual_schedule())
 
         ident_f = const.tile([P, P], F32)
@@ -212,10 +196,8 @@ def tile_pinsageconv_t_kernel(tc, h_node, h_ngbrs, alpha, Wq, bq, Ww, bw, out):
         x_c = {}
         x_s = {}
         z_ps = {}
-        y_sb = {}
         e_sb = {}
         eT_ps = {}
-        sum_ps = {}
         acc = {}
 
         def x_T(qd, half, pool=pe, tag="eT"):
@@ -239,7 +221,7 @@ def tile_pinsageconv_t_kernel(tc, h_node, h_ngbrs, alpha, Wq, bq, Ww, bw, out):
 
         def mx(qd, hc):
             if hc == 0:
-                e_sb[qd] = epool.tile([P, HC + (ALONE[0] > 0), KQ * P], F32, name="e")
+                e_sb[qd] = epool.tile([P, HC + 2, KQ * P], F32, name="e")
             cols = slice(hc * P, (hc + 1) * P)
             z_ps[hc] = pz.tile([P, KQ * P], F32, tag="z", name="z")
             nc.tensor.matmul_mx(
@@ -248,56 +230,35 @@ def tile_pinsageconv_t_kernel(tc, h_node, h_ngbrs, alpha, Wq, bq, Ww, bw, out):
             )
 
         def low(qd, hc):
-            if alone(qd, hc):
+            nc.scalar.activation(
+                out=e_sb[qd][:, parts_of(qd, hc)[-1], :], in_=z_ps[hc][:], func=ACT.Identity,
+                bias=b_low[:, hc : hc + 1], scale=SLOPE,
+            )
+            if kind(qd, hc) == "A":
                 nc.scalar.activation(
                     out=e_sb[qd][:, hc, :], in_=z_ps[hc][:], func=ACT.Relu, bias=b_high[:, hc : hc + 1],
                     scale=1.0 - SLOPE,
                 )
-                nc.scalar.activation(
-                    out=e_sb[qd][:, HC, :], in_=z_ps[hc][:], func=ACT.Identity, bias=b_low[:, hc : hc + 1],
-                    scale=SLOPE,
-                )
-                return
-            y_sb[hc] = ypool.tile([P, KQ * P], F32, name="y")
-            nc.scalar.activation(
-                out=y_sb[hc][:], in_=z_ps[hc][:], func=ACT.Identity, bias=b_low[:, hc : hc + 1], scale=SLOPE
-            )
 
-        def lrelu(qd, hc):
-            if alone(qd, hc):
-                return
-            nc.vector.scalar_tensor_tensor(
-                out=e_sb[qd][:, hc, :], in0=z_ps[hc][:], scalar=b_col[:, hc : hc + 1], in1=y_sb[hc][:],
-                op0=ALU.add, op1=ALU.max,
-            )
-
-        def weigh(qd, lo, hi):
-            n = weighed(qd, lo // 2) * P
-            hi += hi == HC and alone(qd, HC - 1)
-            if n:
-                e = e_sb[qd][:, lo:hi, 0:n]
-                nc.gpsimd.tensor_tensor(
-                    out=e, in0=e, in1=a_bc[qd][:, 0:n].unsqueeze(1).to_broadcast([P, hi - lo, n]), op=ALU.mult
+        def lrelu(qd, lo, hi):
+            hi = min(hi, span(qd, "V")[1])
+            if lo < hi:
+                e = e_sb[qd][:, lo:hi, :]
+                nc.vector.scalar_tensor_tensor(
+                    out=e, in0=e, scalar=1.0 / SLOPE, in1=e, op0=ALU.mult, op1=ALU.max
                 )
 
-        def sum_T(qd, hc):
-            g, q = divmod(qd, QUADS)
-            n = weighed(qd, hc // 2)
-            first = n > 0 and g not in sum_ps
-            if first:
-                sum_ps[g] = pa.tile([P, D_HID], F32, tag="sum", name="sum")
-            parts = [(part, kk) for part in parts_of(qd, hc) for kk in range(n)]
-            for i, (part, kk) in enumerate(parts):
-                nc.tensor.matmul(
-                    out=sum_ps[g][:, hc * P : (hc + 1) * P],
-                    lhsT=e_sb[qd][:, part, kk * P : (kk + 1) * P],
-                    rhs=ident_f[:], is_transpose=True, start=(first and i == 0),
-                    stop=(q == QUADS - 1 and hc == HC - 1 and i == len(parts) - 1),
+        def upper(qd):
+            lo, hi = span(qd, "R")
+            if lo < hi:
+                nc.vector.tensor_scalar(
+                    out=e_sb[qd][:, lo:hi, :], in0=e_sb[qd][:, lo + 2 : hi + 2, :],
+                    scalar1=(1.0 - SLOPE) / SLOPE, scalar2=0.0, op0=ALU.mult, op1=ALU.max,
                 )
 
-        def tk(qd, kk, lo, hi):
+        def tk(qd, kk):
             eT_ps[(qd, kk)] = pe.tile([P, D_HID], F32, tag="eT", name="eT")
-            parts = [(part, hc) for hc in range(lo, hi) for part in parts_of(qd, hc)]
+            parts = [(part, hc) for hc in range(HC) for part in parts_of(qd, hc)]
             for i, (part, hc) in enumerate(parts):
                 nc.tensor.matmul(
                     out=eT_ps[(qd, kk)][:, hc * P : (hc + 1) * P],
@@ -305,37 +266,43 @@ def tile_pinsageconv_t_kernel(tc, h_node, h_ngbrs, alpha, Wq, bq, Ww, bw, out):
                     rhs=ident_f[:], is_transpose=True, start=(i == 0), stop=(i == len(parts) - 1),
                 )
 
-        def fma(qd, kk, lo, hi):
+        def fma(qd, kk):
             g, q = divmod(qd, QUADS)
             k = q * KQ + kk
-            cols = slice(lo * P, hi * P)
-            if g not in acc:
-                acc[g] = const.tile([P, D_HID], F32, name="acc%d" % g)
+            half = (g, k % 2)
+            if half not in acc:
+                acc[half] = const.tile([P, D_HID], F32, name="acc%d_%d" % half)
                 nc.vector.tensor_scalar(
-                    out=acc[g][:], in0=eT_ps[(qd, kk)][:], scalar1=a_n[:, g, k : k + 1], scalar2=None,
+                    out=acc[half][:], in0=eT_ps[(qd, kk)][:], scalar1=a_n[:, g, k : k + 1], scalar2=None,
                     op0=ALU.mult,
                 )
             else:
                 nc.vector.scalar_tensor_tensor(
-                    out=acc[g][:, cols], in0=eT_ps[(qd, kk)][:, cols], scalar=a_n[:, g, k : k + 1],
-                    in1=acc[g][:, cols], op0=ALU.mult, op1=ALU.add,
+                    out=acc[half][:], in0=eT_ps[(qd, kk)][:], scalar=a_n[:, g, k : k + 1], in1=acc[half][:],
+                    op0=ALU.mult, op1=ALU.add,
                 )
+
+        def scaled(qd, kk):
+            g, q = divmod(qd, QUADS)
+            k = q * KQ + kk
+            part = const.tile([P, D_HID], F32, name="part%d" % kk)
+            nc.scalar.activation(
+                out=part[:], in_=eT_ps[(qd, kk)][:], func=ACT.Copy, scale=a_n[:, g, k : k + 1]
+            )
+            return part
 
         s2 = {}
 
-        def l2_sum(g):
-            s2[(g, "sum")] = tail.tile([P, D_HID], F32, name="sum_sb")
-            nc.scalar.copy(out=s2[(g, "sum")][:], in_=sum_ps[g][:])
-
-        def l2_T(g):
-            hT = pe.tile([P, 4, P], F32, tag="eT", name="hT")
-            for i in range(8):
-                t, par = divmod(i, 2)
-                part = (acc[g], s2[(g, "sum")])[par]
-                nc.tensor.matmul(
-                    out=hT[:, t, :], lhsT=part[:, t * P : (t + 1) * P], rhs=ident_f[:],
-                    is_transpose=True, start=(i == 0), stop=(i == 7),
-                )
+        def l2_T(g, more=()):
+            hT = pe.tile([P, HC, P], F32, tag="eT", name="hT")
+            parts = [acc[(g, 0)], acc[(g, 1)], *more]
+            for j, part in enumerate(parts):
+                for hc in range(HC):
+                    nc.tensor.matmul(
+                        out=hT[:, hc, :], lhsT=part[:, hc * P : (hc + 1) * P], rhs=ident_f[:],
+                        is_transpose=True, start=(j == 0 and hc == 0),
+                        stop=(j == len(parts) - 1 and hc == HC - 1),
+                    )
             s2[(g, "hT")] = hT
 
         def l2_copy(g):
@@ -387,19 +354,29 @@ def tile_pinsageconv_t_kernel(tc, h_node, h_ngbrs, alpha, Wq, bq, Ww, bw, out):
                 )
                 s2[(g, "h2")] = h2
                 return
-            high = tail.tile([P, D_OUT], F32, name="high")
-            nc.scalar.activation(out=high[:], in_=v2[:], func=ACT.Relu, scale=1.0 - SLOPE)
-            nc.scalar.activation(out=v2[:], in_=v2[:], func=ACT.Copy, scale=SLOPE)
+            up = tail.tile([P, D_OUT], F32, name="up")
+            if L2G:
+                nc.gpsimd.tensor_scalar(
+                    out=up[:], in0=v2[:], scalar1=1.0 - SLOPE, scalar2=0.0, op0=ALU.mult, op1=ALU.max
+                )
+                nc.gpsimd.tensor_scalar(
+                    out=v2[:], in0=v2[:], scalar1=SLOPE, scalar2=0.0, op0=ALU.mult, op1=ALU.add
+                )
+            else:
+                nc.scalar.activation(out=up[:], in_=v2[:], func=ACT.Relu, scale=1.0 - SLOPE)
+                nc.scalar.activation(out=v2[:], in_=v2[:], func=ACT.Copy, scale=SLOPE)
             h2 = tail.tile([P, D_OUT], F32, name="h2")
-            nc.gpsimd.tensor_tensor(out=h2[:], in0=high[:], in1=v2[:], op=ALU.add)
+            nc.gpsimd.tensor_tensor(out=h2[:], in0=up[:], in1=v2[:], op=ALU.add)
             s2[(g, "h2")] = h2
 
         def l2_norm(g):
             sq = tail.tile([P, D_OUT], F32, name="sq")
             ss = tail.tile([P, 1], F32, name="ss")
-            nc.scalar.activation(out=sq[:], in_=s2[(g, "h2")][:], func=ACT.Square, accum_out=ss[:])
+            nc.scalar.activation(
+                out=sq[:], in_=s2[(g, "h2")][:], func=ACT.Square, bias=tiny[:, 0:1], accum_out=ss[:]
+            )
             rs = tail.tile([P, 1], F32, name="rs")
-            nc.scalar.activation(out=rs[:], in_=ss[:], func=ACT.Abs_reciprocal_sqrt, bias=tiny[:, 0:1])
+            nc.scalar.activation(out=rs[:], in_=ss[:], func=ACT.Abs_reciprocal_sqrt)
             s2[(g, "rs")] = rs
 
         def l2_res(g):
@@ -429,13 +406,11 @@ def tile_pinsageconv_t_kernel(tc, h_node, h_ngbrs, alpha, Wq, bq, Ww, bw, out):
                 nc.vector.scalar_tensor_tensor(
                     out=h2[:, cols], in0=v2[:, cols], scalar=SLOPE, in1=v2[:, cols], op0=ALU.mult, op1=ALU.max
                 )
-                nc.scalar.activation(out=sq[:, cols], in_=h2[:, cols], func=ACT.Square, accum_out=ss[i][:])
-            ssum = tail.tile([P, 1], F32, name="ssum")
-            nc.vector.tensor_scalar(
-                out=ssum[:], in0=ss[0][:], scalar1=ss[1][:, 0:1], scalar2=TINY, op0=ALU.add, op1=ALU.add
-            )
+                nc.scalar.activation(
+                    out=sq[:, cols], in_=h2[:, cols], func=ACT.Square, bias=tiny[:, 0:1], accum_out=ss[i][:]
+                )
             rs = tail.tile([P, 1], F32, name="rs")
-            nc.scalar.activation(out=rs[:], in_=ssum[:], func=ACT.Abs_reciprocal_sqrt)
+            nc.scalar.activation(out=rs[:], in_=ss[0][:], func=ACT.Abs_reciprocal_sqrt, bias=ss[1][:, 0:1])
             res = [tail.tile([P, D_OUT // 2], F32, name="res0"), tail.tile([P, D_OUT // 2], F32, name="res1")]
             nc.vector.tensor_scalar(
                 out=res[0][:], in0=h2[:, halves[0]], scalar1=rs[:, 0:1], scalar2=None, op0=ALU.mult
@@ -444,7 +419,6 @@ def tile_pinsageconv_t_kernel(tc, h_node, h_ngbrs, alpha, Wq, bq, Ww, bw, out):
             nc.scalar.activation(out=res[1][:], in_=h2[:, halves[1]], func=ACT.Copy, scale=rs[:, 0:1])
             nc.scalar.dma_start(out=out[g * P : (g + 1) * P, halves[1]], in_=res[1][:])
 
-        b_col = const.tile([P, HC], F32)
         b_low = const.tile([P, HC], F32)
         b_high = const.tile([P, HC], F32)
         a_f = const.tile([P, GROUPS, K_NGB], F32)
@@ -452,51 +426,40 @@ def tile_pinsageconv_t_kernel(tc, h_node, h_ngbrs, alpha, Wq, bq, Ww, bw, out):
         a_den = const.tile([P, GROUPS], F32)
         a_rec = const.tile([P, GROUPS], F32)
         a_n = const.tile([P, GROUPS, K_NGB], F32)
-        a_bc = {}
-        aT_sb = const.tile([P, P], F32, name="aT_sb")
 
         wq_g = grp.tile([P, 4 * P, 4], BF16, align_bytes=64, tag="grouped", name="wq_g")
         wq_words = wq_raw[:].bitcast(F32)
         wt0 = words_T(wq_words, 0, pz, "z")
         wt1 = words_T(wq_words, 1, pz, "z")
-        x_T(0, 0, pz, "z")
-        x_T(0, 1, pz, "z")
-        words_copy(wt0, wq_g, 0, nc.scalar.copy)
-        x_copy(0, 0, nc.scalar.copy)
-        nc.vector.tensor_copy(out=a_f[:], in_=a_raw[:])
-        words_copy(wt1, wq_g, 1, nc.vector.tensor_copy)
-        nc.vector.tensor_reduce(out=a_sum[:], in_=a_f[:], axis=AX.X, op=ALU.add)
-        quantise(wq_g, wq_c[:], wq_s[:])
-        nc.vector.scalar_tensor_tensor(
-            out=a_den[:], in0=a_sum[:], scalar=0.0, in1=a_sum[:], op0=ALU.is_equal, op1=ALU.add
-        )
-        x_copy(0, 1, nc.vector.tensor_copy)
-        nc.vector.reciprocal(out=a_rec[:], in_=a_den[:])
-        x_quant(0)
-        nc.vector.tensor_tensor(
-            out=a_n[:], in0=a_f[:], in1=a_rec[:].unsqueeze(2).to_broadcast([P, GROUPS, K_NGB]), op=ALU.mult
-        )
-        bT = pe.tile([P, P], BF16, tag="eT", name="bT")
+        x_T(0, 0)
+        x_T(0, 1)
+        bT = pz.tile([P, P], BF16, tag="z", name="bT")
         nc.tensor.transpose(bT[:], b_rows[:], ident_b[:])
-        nc.vector.tensor_copy(out=b_col[:], in_=bT[:, 0:HC])
-        nc.vector.tensor_scalar(out=b_low[:], in0=b_col[:], scalar1=SLOPE, scalar2=None, op0=ALU.mult)
-        nc.vector.tensor_scalar(out=b_high[:], in0=b_col[:], scalar1=1.0 - SLOPE, scalar2=None, op0=ALU.mult)
-        for qd in range(1, AHEAD):
-            for half in range(2):
-                x_T(qd, half)
-                x_copy(qd, half, nc.vector.tensor_copy if qd == 1 else nc.scalar.copy)
+        words_copy(wt0, wq_g, 0, nc.scalar.copy)
+        words_copy(wt1, wq_g, 1, nc.vector.tensor_copy)
+        quantise(wq_g, wq_c[:], wq_s[:])
+        x_copy(0, 0)
+        x_copy(0, 1)
+        nc.vector.tensor_scalar(out=b_low[:], in0=bT[:, 0:HC], scalar1=SLOPE, scalar2=None, op0=ALU.mult)
+        nc.vector.tensor_scalar(
+            out=b_high[:], in0=bT[:, 0:HC], scalar1=1.0 - SLOPE, scalar2=None, op0=ALU.mult
+        )
+        x_quant(0)
+        x_T(1, 0)
+        x_T(1, 1)
+        x_copy(1, 0, nc.vector.tensor_copy)
+        x_copy(1, 1, nc.vector.tensor_copy)
 
-        def park_weights():
-            aT = pe.tile([P, P], F32, tag="eT", name="aT")
-            nc.tensor.transpose(aT[:], a_n[:].rearrange("p g k -> p (g k)"), ident_f[:])
-            nc.scalar.copy(out=aT_sb[:], in_=aT[:])
-            nc.sync.dma_start(
-                out=out[PARK : PARK + NQ, :].rearrange("r (s n) -> (r s) n", n=P), in_=aT_sb[:]
+        def norm_weights():
+            nc.vector.tensor_copy(out=a_f[:], in_=a_raw[:])
+            nc.vector.tensor_reduce(out=a_sum[:], in_=a_f[:], axis=AX.X, op=ALU.add)
+            nc.vector.scalar_tensor_tensor(
+                out=a_den[:], in0=a_sum[:], scalar=0.0, in1=a_sum[:], op0=ALU.is_equal, op1=ALU.add
             )
-
-        def load_weights(qd):
-            a_bc[qd] = wgt.tile([P, KQ * P], F32, name="a_bc")
-            nc.sync.dma_start(out=a_bc[qd][:], in_=out[PARK + qd, :].partition_broadcast(P))
+            nc.vector.reciprocal(out=a_rec[:], in_=a_den[:])
+            nc.vector.tensor_tensor(
+                out=a_n[:], in0=a_f[:], in1=a_rec[:].unsqueeze(2).to_broadcast([P, GROUPS, K_NGB]), op=ALU.mult
+            )
 
         def due(i, lag):
             g, r = divmod(i - lag, QUADS)
@@ -504,72 +467,58 @@ def tile_pinsageconv_t_kernel(tc, h_node, h_ngbrs, alpha, Wq, bq, Ww, bw, out):
                 return g - 1
             return None
 
-        late = []
-        summed = set()
         for i in range(NQ):
-            old = i - 1
-            own = left(old) if old >= 0 else []
-            cut = (len(own) + 1) // 2
             nxt = i + AHEAD if i + AHEAD < NQ else None
             if i + FIRST_LOADS < NQ:
                 load(i + FIRST_LOADS)
+            late_loads(i)
             g1, g2, g3, g4, g5 = (due(i, lag + SUM_LAG) for lag in (0, 1, 2, 3, 4))
-            if g1 is not None:
-                l2_sum(g1)
             if g2 is not None:
                 l2_copy(g2)
             for what in PORDER:
+                n = int(what[1]) if len(what) > 1 else 0
                 if what[0] == "M":
-                    for hc in range(int(what[1]), int(what[2])):
+                    for hc in range(n, int(what[2])):
                         mx(i, hc)
-                    if i == 0 and what == "M02":
-                        park_weights()
                 elif what == "Z" and g3 is not None:
                     l2_mx0(g3)
                     l2_mx1(g3)
                 elif what[0] == "X" and nxt is not None:
-                    x_T(nxt, int(what[1]))
-                elif what == "K":
-                    for piece in own[:cut]:
-                        tk(old, *piece)
-                elif what == "k":
-                    for piece in own[cut:]:
-                        tk(old, *piece)
-                elif what == "j":
-                    for piece in late:
-                        tk(*piece)
-                elif what[0] == "S" and i >= int(what[3]):
-                    for hc in range(int(what[1]), int(what[2])):
-                        sum_T(i - int(what[3]), hc)
-                        summed.add((i - int(what[3]), hc))
+                    x_T(nxt, n)
+                    if i == 0 and n == 1:
+                        early = [(qd, half) for qd in range(2, AHEAD) for half in range(2)]
+                        for qd, half in early:
+                            x_T(qd, half)
+                            if half == 1:
+                                x_copy(qd, 0)
+                                x_copy(qd, 1)
+                elif what[0] == "K" and i >= 1:
+                    tk(i - 1, n)
+                elif what[0] == "j" and i >= 2:
+                    tk(i - 2, n)
                 elif what == "T" and g1 is not None:
                     l2_T(g1)
                 elif what == "P" and 0 <= i - PREP0 < 8:
                     prep_T(i - PREP0)
             if i == 0:
-                for qd in range(G_FIRST, G_FIRST + WAHEAD):
-                    load_weights(qd)
-            elif i + G_FIRST + WAHEAD - 1 < NQ:
-                load_weights(i + G_FIRST + WAHEAD - 1)
-            late_loads(i)
+                norm_weights()
             for what in ORDER:
+                n = int(what[1]) if len(what) > 1 else 0
                 if what[0] == "y":
-                    low(i, int(what[1]))
+                    low(i, n)
                 elif what == "d":
                     if (i + AHEAD - 1, 1) in xt_ps and i > 0:
                         x_copy(i + AHEAD - 1, 1)
                 elif what[0] == "c" and nxt is not None:
-                    x_copy(nxt, int(what[1]))
+                    x_copy(nxt, n)
+                elif what == "r":
+                    upper(i)
                 elif what[0] == "e":
-                    lrelu(i, int(what[1]))
-                elif what[0] == "w":
-                    weigh(i, int(what[1]), int(what[2]))
-                elif what == "L":
-                    for piece in late:
-                        fma(*piece)
-                elif what == "E":
-                    for piece in own[:cut]:
-                        fma(old, *piece)
+                    lrelu(i, n, int(what[2]))
+                elif what[0] == "F":
+                    qd = i - 1 if "K%d" % n in PORDER else i - 2
+                    if qd >= 0:
+                        fma(qd, n)
                 elif what == "Q":
                     if i == 0:
                         for qd in range(1, QA):
@@ -590,28 +539,21 @@ def tile_pinsageconv_t_kernel(tc, h_node, h_ngbrs, alpha, Wq, bq, Ww, bw, out):
                 l2_res(g5)
             if 0 <= i - PREP0 < 8:
                 prep_copy(i - PREP0)
-            late = [(old,) + piece for piece in own[cut:]]
 
         g = GROUPS - 1
-        for qd in range(NQ - 5, NQ - 1):
-            for hc in range(HC):
-                if (qd, hc) not in summed:
-                    sum_T(qd, hc)
-        if "j" in PORDER:
-            for piece in late:
-                tk(*piece)
-        own = left(NQ - 1)
-        for piece in own:
-            tk(NQ - 1, *piece)
-        for hc in range(HC):
-            sum_T(NQ - 1, hc)
+        for kk in range(KQ):
+            if "j%d" % kk in PORDER:
+                tk(NQ - 2, kk)
+                fma(NQ - 2, kk)
+        more = []
+        for kk in range(KQ):
+            tk(NQ - 1, kk)
+            if kk in LAST_S:
+                more.append(scaled(NQ - 1, kk))
+            else:
+                fma(NQ - 1, kk)
         l2_mx0(g)
-        for piece in late:
-            fma(*piece)
-        for piece in own:
-            fma(NQ - 1, *piece)
-        l2_sum(g)
-        l2_T(g)
+        l2_T(g, more)
         l2_copy(g)
         l2_quant(g)
         l2_mx1(g)

@@ -21,15 +21,16 @@ KQ = 4
 QUADS = K_NGB // KQ
 NQ = GROUPS * QUADS
 HC = D_HID // P
-KINDS = ("VVRA",)
+KINDS = ("VVRA", "VVVA")
 SUM_LAG = 2
 L2V = 0
 L2G = 0
+WARM = {'K2': 256, 'K3': 128}
 LAST_S = (0, 2, 3)
 LONE = 2
 QA = 1
-ORDER = "d y0 y1 c0 y2 y3 F2 Q e02 F3 e24 r F0 F1".split(" ")
-PORDER = "M02 j2 X0 X1 M24 Z K3 T K0 P K1".split(" ")
+ORDER = "d y0 y1 c0 y2 y3 F2 Q e02 r F3 e24 F0 F1".split(" ")
+PORDER = "M02 j2 X0 X1 M24 T K3 K1 P K0 Z".split(" ")
 AHEAD = QA + 2
 PREP0 = 2
 FIRST_LOADS = 6
@@ -122,8 +123,15 @@ def tile_pinsageconv_t_kernel(tc, h_node, h_ngbrs, alpha, Wq, bq, Ww, bw, out):
             elif i == 4:
                 nc.sync.dma_start(out=bw_bc[:], in_=bw.partition_broadcast(P))
 
-        def words_T(src_words, half, pool, tag):
+        def warm(bank, n):
+            if n:
+                nc.tensor.matmul(
+                    out=bank[:, 0:n], lhsT=ident_b[:], rhs=wq_raw[:, 0, 0:n], start=True, stop=True
+                )
+
+        def words_T(src_words, half, pool, tag, busy=0):
             xt = pool.tile([P, 2, 2, P], F32, tag=tag, name="xt")
+            warm(xt[:].rearrange("p b u c -> p (b u c)"), busy)
             for b in range(2):
                 for u in range(2):
                     nc.tensor.transpose(
@@ -204,7 +212,7 @@ def tile_pinsageconv_t_kernel(tc, h_node, h_ngbrs, alpha, Wq, bq, Ww, bw, out):
             if half == 0 and pair_of(qd)[0] == qd:
                 n = pair_of(qd)[1]
                 grouped[qd] = grp.tile([P, n * KQ * P, 4], BF16, align_bytes=64, tag="grouped", name="grouped")
-            xt_ps[(qd, half)] = words_T(x_sb[qd][:].bitcast(F32), half, pool, tag)
+            xt_ps[(qd, half)] = words_T(x_sb[qd][:].bitcast(F32), half, pool, tag, WARM.get("X%d" % half, 0))
 
         def x_copy(qd, half, copy=nc.scalar.copy):
             lead = pair_of(qd)[0]
@@ -258,6 +266,7 @@ def tile_pinsageconv_t_kernel(tc, h_node, h_ngbrs, alpha, Wq, bq, Ww, bw, out):
 
         def tk(qd, kk):
             eT_ps[(qd, kk)] = pe.tile([P, D_HID], F32, tag="eT", name="eT")
+            warm(eT_ps[(qd, kk)][:], WARM.get("K%d" % kk, 0))
             parts = [(part, hc) for hc in range(HC) for part in parts_of(qd, hc)]
             for i, (part, hc) in enumerate(parts):
                 nc.tensor.matmul(

@@ -21,47 +21,37 @@ KQ = 4
 QUADS = K_NGB // KQ
 NQ = GROUPS * QUADS
 HC = D_HID // P
-KINDS = ("VVRA", "VVVA")
-SUM_LAG = 2
-L2V = 0
-L2G = 0
-WARM = {'K2': 256, 'K3': 128}
-LAST_S = (0, 2, 3)
-LONE = 2
-QA = 1
-ORDER = "d y0 y1 c0 y2 y3 F2 Q e02 r F3 e24 F0 F1".split(" ")
-PORDER = "M02 j2 X0 X1 M24 T K3 K1 P K0 Z".split(" ")
-AHEAD = QA + 2
-PREP0 = 2
-FIRST_LOADS = 6
+COLS = KQ * P
+ONE_BY_ONE = 2
+AHEAD = 3
+LOADS = 6
+PREP_FIRST, PREP_JOBS = 2, 8
+WARM_COLS = 128
+
+WHOLE = 2
+PART_V, PART_S = 2, 3
+SLOTS = HC + 2
 
 FLOPS = 2 * N_NODES * K_NGB * D_IN * D_HID + 2 * N_NODES * (D_IN + D_HID) * D_OUT
 
 
-def pair_of(qd):
-    if qd < LONE:
-        return qd, 1
-    return qd - (qd - LONE) % 2, 2
+def parts_of(hc):
+    return (hc,) if hc < WHOLE else (hc, hc + HC - WHOLE)
 
 
-def kind(qd, hc):
-    return KINDS[qd % len(KINDS)][hc]
+def lead_of(qd):
+    return qd if qd < ONE_BY_ONE else qd - (qd - ONE_BY_ONE) % 2
 
 
-def span(qd, what):
-    mine = [hc for hc in range(HC) if kind(qd, hc) == what]
-    return (mine[0], mine[-1] + 1) if mine else (0, 0)
-
-
-def parts_of(qd, hc):
-    return (hc,) if kind(qd, hc) == "V" else (hc, hc + 2)
+def count_of(lead):
+    return 1 if lead < ONE_BY_ONE else 2
 
 
 def tile_pinsageconv_t_kernel(tc, h_node, h_ngbrs, alpha, Wq, bq, Ww, bw, out):
     nc = tc.nc
     with ExitStack() as ctx:
         const = ctx.enter_context(tc.tile_pool(name="const", bufs=1))
-        xin = ctx.enter_context(tc.tile_pool(name="xin", bufs=7))
+        xin = ctx.enter_context(tc.tile_pool(name="xin", bufs=LOADS + 1))
         grp = ctx.enter_context(tc.tile_pool(name="grp", bufs=4))
         qnt = ctx.enter_context(tc.tile_pool(name="qnt", bufs=4))
         epool = ctx.enter_context(tc.tile_pool(name="epool", bufs=4))
@@ -79,22 +69,21 @@ def tile_pinsageconv_t_kernel(tc, h_node, h_ngbrs, alpha, Wq, bq, Ww, bw, out):
         wq_raw = const.tile([P, HC, D_IN], BF16)
         wq_view = Wq.rearrange("(b p) i -> p b i", p=P)
         nc.sync.dma_start(out=wq_raw[:, 0:2, :], in_=wq_view[:, 0:2, :])
-        nc.sync.dma_start(out=wq_raw[:, 2:4, :], in_=wq_view[:, 2:4, :])
 
         x_sb = {}
 
         def load(qd):
             g, q = divmod(qd, QUADS)
             x_sb[qd] = xin.tile([P, KQ, D_IN], BF16, name="x_sb")
-            pieces = 2 if qd == 0 else 1
-            step = KQ // pieces
-            for i in range(pieces):
+            step = KQ // 2 if qd == 0 else KQ
+            for kk in range(0, KQ, step):
+                k = q * KQ + kk
                 nc.sync.dma_start(
-                    out=x_sb[qd][:, i * step : (i + 1) * step, :],
-                    in_=h_ngbrs[g * P : (g + 1) * P, q * KQ + i * step : q * KQ + (i + 1) * step, :],
+                    out=x_sb[qd][:, kk : kk + step, :], in_=h_ngbrs[g * P : (g + 1) * P, k : k + step, :]
                 )
 
         load(0)
+        nc.sync.dma_start(out=wq_raw[:, 2:4, :], in_=wq_view[:, 2:4, :])
 
         b_rows = const.tile([P, P], BF16)
         nc.vector.memset(b_rows[:], 0.0)
@@ -105,51 +94,41 @@ def tile_pinsageconv_t_kernel(tc, h_node, h_ngbrs, alpha, Wq, bq, Ww, bw, out):
         a_raw = const.tile([P, GROUPS, K_NGB], BF16)
         nc.scalar.dma_start(out=a_raw[:], in_=alpha.rearrange("(g p) k o -> p g (k o)", p=P))
         nc.scalar.dma_start(out=b_rows[0:HC, :], in_=bq.rearrange("(b p) -> b p", p=P))
-        one_s = const.tile([P, 1], F32)
-        nc.scalar.activation(out=one_s[:], in_=one[:], func=ACT.Abs_reciprocal_sqrt)
+        root = const.tile([P, 1], F32)
+        nc.scalar.activation(out=root[:], in_=one[:], func=ACT.Abs_reciprocal_sqrt)
 
-        for qd in range(1, FIRST_LOADS):
+        for qd in range(1, LOADS):
             load(qd)
 
         ww_raw = const.tile([P, D_OUT // P, D_IN + D_HID], BF16)
         hn_raw = const.tile([P, GROUPS, D_IN], BF16)
-        bw_bc = const.tile([P, D_OUT], BF16)
+        bw_all = const.tile([P, D_OUT], BF16)
 
-        def late_loads(i):
+        def load_second_layer(i):
             if i == 0:
                 nc.sync.dma_start(out=ww_raw[:], in_=Ww.rearrange("(b p) c -> p b c", p=P))
             elif i == 1:
                 nc.sync.dma_start(out=hn_raw[:], in_=h_node.rearrange("(g p) i -> p g i", p=P))
             elif i == 4:
-                nc.sync.dma_start(out=bw_bc[:], in_=bw.partition_broadcast(P))
+                nc.sync.dma_start(out=bw_all[:], in_=bw.partition_broadcast(P))
 
-        def warm(bank, n):
-            if n:
-                nc.tensor.matmul(
-                    out=bank[:, 0:n], lhsT=ident_b[:], rhs=wq_raw[:, 0, 0:n], start=True, stop=True
-                )
-
-        def words_T(src_words, half, pool, tag, busy=0):
-            xt = pool.tile([P, 2, 2, P], F32, tag=tag, name="xt")
-            warm(xt[:].rearrange("p b u c -> p (b u c)"), busy)
+        def words_T(words, half, pool, tag):
+            bank = pool.tile([P, 2, 2, P], F32, tag=tag, name="bank")
             for b in range(2):
                 for u in range(2):
-                    nc.tensor.transpose(
-                        xt[:, b, u, :], src_words[:, 2 * half + b, u * P : (u + 1) * P], ident_f[:]
-                    )
-            return xt
+                    nc.tensor.transpose(bank[:, b, u, :], words[:, 2 * half + b, u * P : (u + 1) * P], ident_f[:])
+            return bank
 
-        def words_copy(xt, grouped, half, copy, first=0):
+        def words_copy(bank, grouped, half, copy, first=0):
+            rows = slice(first + 2 * half * P, first + (2 * half + 2) * P)
             copy(
-                out=grouped[:].bitcast(F32)[:, first + 2 * half * P : first + (2 * half + 2) * P, :].rearrange(
-                    "p (b c) u -> p b c u", b=2
-                ),
-                in_=xt[:].rearrange("p b u c -> p b c u"),
+                out=grouped[:].bitcast(F32)[:, rows, :].rearrange("p (b c) u -> p b c u", b=2),
+                in_=bank[:].rearrange("p b u c -> p b c u"),
             )
 
         def quantise(grouped, codes, scales):
             nc.vector.quantize_mx(
-                out=codes.bitcast(FP8X4), scales=scales, in_=grouped[:].rearrange("p c t -> p (c t)")
+                out=codes.bitcast(FP8X4), scales=scales, in_=grouped.rearrange("p c t -> p (c t)")
             )
 
         wq_c = const.tile([P, D_HID], U32, align_bytes=64)
@@ -162,155 +141,138 @@ def tile_pinsageconv_t_kernel(tc, h_node, h_ngbrs, alpha, Wq, bq, Ww, bw, out):
         hn_c = const.tile([P, N_NODES], U32, align_bytes=64)
         hn_s = const.tile([P, N_NODES], U8, align_bytes=64)
         prep_g = {}
-        prep_ps = {}
+        prep_bank = {}
 
-        def prep_T(i):
-            if i % 4 == 0 or i == 2:
-                prep_g[i] = prep.tile([P, 4 * P, 4], BF16, align_bytes=64, tag="prep_g", name="prep_g")
-            if i < 2:
-                prep_ps[i] = words_T(ww_raw[:].bitcast(F32)[:, :, 0 : D_IN // 2], i, pe, "eT")
-            elif i < 4:
-                prep_ps[i] = words_T(hn_raw[:].bitcast(F32), i - 2, pe, "eT")
+        def prep_T(job):
+            if job in (0, 2, 4):
+                prep_g[job] = prep.tile([P, 4 * P, 4], BF16, align_bytes=64, tag="prep_g", name="prep_g")
+            if job < 2:
+                prep_bank[job] = words_T(ww_raw[:].bitcast(F32)[:, :, 0 : D_IN // 2], job, pe, "eT")
+            elif job < 4:
+                prep_bank[job] = words_T(hn_raw[:].bitcast(F32), job - 2, pe, "eT")
             else:
-                ob = i - 4
-                wt = pe.tile([P, 4, P], BF16, tag="eT", name="wt")
+                bank = pe.tile([P, 4, P], BF16, tag="eT", name="wt")
                 for t in range(4):
-                    nc.tensor.transpose(
-                        wt[:, t, :], ww_raw[:, ob, D_IN + t * P : D_IN + (t + 1) * P], ident_b[:]
-                    )
-                prep_ps[i] = wt
+                    cols = slice(D_IN + t * P, D_IN + (t + 1) * P)
+                    nc.tensor.transpose(bank[:, t, :], ww_raw[:, job - 4, cols], ident_b[:])
+                prep_bank[job] = bank
 
-        def prep_copy(i):
-            if i < 2:
-                words_copy(prep_ps[i], prep_g[0], i, nc.scalar.copy)
-            elif i < 4:
-                words_copy(prep_ps[i], prep_g[2], i - 2, nc.scalar.copy)
+        def prep_copy(job):
+            if job < 4:
+                words_copy(prep_bank[job], prep_g[job - job % 2], job % 2, nc.scalar.copy)
             else:
-                ob = i - 4
-                nc.scalar.copy(
-                    out=prep_g[4][:, ob * P : (ob + 1) * P, :], in_=prep_ps[i][:].rearrange("p t c -> p c t")
-                )
+                rows = slice((job - 4) * P, (job - 3) * P)
+                nc.scalar.copy(out=prep_g[4][:, rows, :], in_=prep_bank[job][:].rearrange("p t c -> p c t"))
 
-        def prep_quant(i):
-            if i == 1:
-                quantise(prep_g[0], w0_c[:], w0_s[:])
-            elif i == 3:
-                quantise(prep_g[2], hn_c[:], hn_s[:])
-            elif i == 7:
-                quantise(prep_g[4], w1_c[:], w1_s[:])
+        def prep_quant(job):
+            if job == 1:
+                quantise(prep_g[0][:], w0_c[:], w0_s[:])
+            elif job == 3:
+                quantise(prep_g[2][:], hn_c[:], hn_s[:])
+            elif job == 7:
+                quantise(prep_g[4][:], w1_c[:], w1_s[:])
 
         grouped = {}
-        xt_ps = {}
-        x_c = {}
-        x_s = {}
-        z_ps = {}
+        x_bank = {}
+        x_codes = {}
+        z_bank = {}
         e_sb = {}
-        eT_ps = {}
+        eT_bank = {}
         acc = {}
 
-        def x_T(qd, half, pool=pe, tag="eT"):
-            if half == 0 and pair_of(qd)[0] == qd:
-                n = pair_of(qd)[1]
-                grouped[qd] = grp.tile([P, n * KQ * P, 4], BF16, align_bytes=64, tag="grouped", name="grouped")
-            xt_ps[(qd, half)] = words_T(x_sb[qd][:].bitcast(F32), half, pool, tag, WARM.get("X%d" % half, 0))
+        def x_T(qd, half):
+            lead = lead_of(qd)
+            if half == 0 and lead == qd:
+                grouped[lead] = grp.tile(
+                    [P, count_of(lead) * COLS, 4], BF16, align_bytes=64, tag="grouped", name="grouped"
+                )
+            x_bank[(qd, half)] = words_T(x_sb[qd][:].bitcast(F32), half, pe, "eT")
 
         def x_copy(qd, half, copy=nc.scalar.copy):
-            lead = pair_of(qd)[0]
-            words_copy(xt_ps[(qd, half)], grouped[lead], half, copy, (qd - lead) * KQ * P)
+            lead = lead_of(qd)
+            words_copy(x_bank[(qd, half)], grouped[lead], half, copy, (qd - lead) * COLS)
 
-        def x_quant(qd):
-            n = pair_of(qd)[1]
-            codes = qnt.tile([P, n * KQ * P], U32, align_bytes=64, name="x_c")
-            scales = qnt.tile([P, n * KQ * P], U8, align_bytes=64, name="x_s")
-            quantise(grouped[qd], codes[:], scales[:])
+        def x_quant(lead):
+            n = count_of(lead)
+            codes = qnt.tile([P, n * COLS], U32, align_bytes=64, name="codes")
+            scales = qnt.tile([P, n * COLS], U8, align_bytes=64, name="scales")
+            quantise(grouped[lead][:], codes[:], scales[:])
             for j in range(n):
-                x_c[qd + j] = codes[:, j * KQ * P : (j + 1) * KQ * P]
-                x_s[qd + j] = scales[:, j * KQ * P : (j + 1) * KQ * P]
+                cols = slice(j * COLS, (j + 1) * COLS)
+                x_codes[lead + j] = (codes[:, cols], scales[:, cols])
 
         def mx(qd, hc):
             if hc == 0:
-                e_sb[qd] = epool.tile([P, HC + 2, KQ * P], F32, name="e")
+                e_sb[qd] = epool.tile([P, SLOTS, COLS], F32, name="e")
             cols = slice(hc * P, (hc + 1) * P)
-            z_ps[hc] = pz.tile([P, KQ * P], F32, tag="z", name="z")
+            codes, scales = x_codes[qd]
+            z_bank[hc] = pz.tile([P, COLS], F32, tag="z", name="z")
             nc.tensor.matmul_mx(
-                out=z_ps[hc][:], lhsT=wq_c[:, cols].bitcast(FP8X4), lhsT_scale=wq_s[:, cols],
-                rhs=x_c[qd].bitcast(FP8X4), rhs_scale=x_s[qd], start=True, stop=True,
+                out=z_bank[hc][:], lhsT=wq_c[:, cols].bitcast(FP8X4), lhsT_scale=wq_s[:, cols],
+                rhs=codes.bitcast(FP8X4), rhs_scale=scales, start=True, stop=True,
             )
 
-        def low(qd, hc):
+        def scalar_part(qd, hc):
             nc.scalar.activation(
-                out=e_sb[qd][:, parts_of(qd, hc)[-1], :], in_=z_ps[hc][:], func=ACT.Identity,
+                out=e_sb[qd][:, parts_of(hc)[-1], :], in_=z_bank[hc][:], func=ACT.Identity,
                 bias=b_low[:, hc : hc + 1], scale=SLOPE,
             )
-            if kind(qd, hc) == "A":
+            if hc == PART_S:
                 nc.scalar.activation(
-                    out=e_sb[qd][:, hc, :], in_=z_ps[hc][:], func=ACT.Relu, bias=b_high[:, hc : hc + 1],
+                    out=e_sb[qd][:, hc, :], in_=z_bank[hc][:], func=ACT.Relu, bias=b_high[:, hc : hc + 1],
                     scale=1.0 - SLOPE,
                 )
 
-        def lrelu(qd, lo, hi):
-            hi = min(hi, span(qd, "V")[1])
-            if lo < hi:
-                e = e_sb[qd][:, lo:hi, :]
-                nc.vector.scalar_tensor_tensor(
-                    out=e, in0=e, scalar=1.0 / SLOPE, in1=e, op0=ALU.mult, op1=ALU.max
-                )
+        def vector_whole(qd):
+            e = e_sb[qd][:, 0:WHOLE, :]
+            nc.vector.scalar_tensor_tensor(out=e, in0=e, scalar=1.0 / SLOPE, in1=e, op0=ALU.mult, op1=ALU.max)
 
-        def upper(qd):
-            lo, hi = span(qd, "R")
-            if lo < hi:
-                nc.vector.tensor_scalar(
-                    out=e_sb[qd][:, lo:hi, :], in0=e_sb[qd][:, lo + 2 : hi + 2, :],
-                    scalar1=(1.0 - SLOPE) / SLOPE, scalar2=0.0, op0=ALU.mult, op1=ALU.max,
-                )
+        def vector_part(qd):
+            upper, u = parts_of(PART_V)
+            nc.vector.tensor_scalar(
+                out=e_sb[qd][:, upper : upper + 1, :], in0=e_sb[qd][:, u : u + 1, :],
+                scalar1=(1.0 - SLOPE) / SLOPE, scalar2=0.0, op0=ALU.mult, op1=ALU.max,
+            )
 
-        def tk(qd, kk):
-            eT_ps[(qd, kk)] = pe.tile([P, D_HID], F32, tag="eT", name="eT")
-            warm(eT_ps[(qd, kk)][:], WARM.get("K%d" % kk, 0))
-            parts = [(part, hc) for hc in range(HC) for part in parts_of(qd, hc)]
-            for i, (part, hc) in enumerate(parts):
+        def neighbour_T(qd, kk, warm=False):
+            bank = pe.tile([P, D_HID], F32, tag="eT", name="eT")
+            eT_bank[(qd, kk)] = bank
+            if warm:
                 nc.tensor.matmul(
-                    out=eT_ps[(qd, kk)][:, hc * P : (hc + 1) * P],
-                    lhsT=e_sb[qd][:, part, kk * P : (kk + 1) * P],
-                    rhs=ident_f[:], is_transpose=True, start=(i == 0), stop=(i == len(parts) - 1),
+                    out=bank[:, 0:WARM_COLS], lhsT=ident_b[:], rhs=wq_raw[:, 0, 0:WARM_COLS], start=True, stop=True
+                )
+            parts = [(slot, hc) for hc in range(HC) for slot in parts_of(hc)]
+            for j, (slot, hc) in enumerate(parts):
+                nc.tensor.matmul(
+                    out=bank[:, hc * P : (hc + 1) * P], lhsT=e_sb[qd][:, slot, kk * P : (kk + 1) * P],
+                    rhs=ident_f[:], is_transpose=True, start=(j == 0), stop=(j == len(parts) - 1),
                 )
 
-        def fma(qd, kk):
+        def weigh(qd, kk):
             g, q = divmod(qd, QUADS)
             k = q * KQ + kk
-            half = (g, k % 2)
-            if half not in acc:
-                acc[half] = const.tile([P, D_HID], F32, name="acc%d_%d" % half)
+            key = (g, k % 2)
+            weight = a_n[:, g, k : k + 1]
+            bank = eT_bank[(qd, kk)]
+            if key not in acc:
+                acc[key] = const.tile([P, D_HID], F32, name="acc%d_%d" % key)
                 nc.vector.tensor_scalar(
-                    out=acc[half][:], in0=eT_ps[(qd, kk)][:], scalar1=a_n[:, g, k : k + 1], scalar2=None,
-                    op0=ALU.mult,
+                    out=acc[key][:], in0=bank[:], scalar1=weight, scalar2=None, op0=ALU.mult
                 )
             else:
                 nc.vector.scalar_tensor_tensor(
-                    out=acc[half][:], in0=eT_ps[(qd, kk)][:], scalar=a_n[:, g, k : k + 1], in1=acc[half][:],
-                    op0=ALU.mult, op1=ALU.add,
+                    out=acc[key][:], in0=bank[:], scalar=weight, in1=acc[key][:], op0=ALU.mult, op1=ALU.add
                 )
-
-        def scaled(qd, kk):
-            g, q = divmod(qd, QUADS)
-            k = q * KQ + kk
-            part = const.tile([P, D_HID], F32, name="part%d" % kk)
-            nc.scalar.activation(
-                out=part[:], in_=eT_ps[(qd, kk)][:], func=ACT.Copy, scale=a_n[:, g, k : k + 1]
-            )
-            return part
 
         s2 = {}
 
-        def l2_T(g, more=()):
+        def l2_T(g):
             hT = pe.tile([P, HC, P], F32, tag="eT", name="hT")
-            parts = [acc[(g, 0)], acc[(g, 1)], *more]
-            for j, part in enumerate(parts):
+            for j in range(2):
                 for hc in range(HC):
                     nc.tensor.matmul(
-                        out=hT[:, hc, :], lhsT=part[:, hc * P : (hc + 1) * P], rhs=ident_f[:],
-                        is_transpose=True, start=(j == 0 and hc == 0),
-                        stop=(j == len(parts) - 1 and hc == HC - 1),
+                        out=hT[:, hc, :], lhsT=acc[(g, j)][:, hc * P : (hc + 1) * P], rhs=ident_f[:],
+                        is_transpose=True, start=(j == 0 and hc == 0), stop=(j == 1 and hc == HC - 1),
                     )
             s2[(g, "hT")] = hT
 
@@ -322,10 +284,10 @@ def tile_pinsageconv_t_kernel(tc, h_node, h_ngbrs, alpha, Wq, bq, Ww, bw, out):
         def l2_quant(g):
             ha_c = tail.tile([P, P], U32, align_bytes=64, name="ha_c")
             ha_s = tail.tile([P, P], U8, align_bytes=64, name="ha_s")
-            quantise(s2[(g, "hg")], ha_c[:], ha_s[:])
+            quantise(s2[(g, "hg")][:], ha_c[:], ha_s[:])
             s2[(g, "ha")] = (ha_c, ha_s)
 
-        def l2_mx0(g):
+        def l2_mx_node(g):
             z2 = pz.tile([P, D_OUT], F32, tag="z", name="z2")
             cols = slice(g * P, (g + 1) * P)
             s2[(g, "z2")] = z2
@@ -334,75 +296,43 @@ def tile_pinsageconv_t_kernel(tc, h_node, h_ngbrs, alpha, Wq, bq, Ww, bw, out):
                 rhs=w0_c[:].bitcast(FP8X4), rhs_scale=w0_s[:], start=True, stop=False,
             )
 
-        def l2_mx1(g):
+        def l2_mx_agg(g):
             ha_c, ha_s = s2[(g, "ha")]
-            z2 = s2[(g, "z2")]
             nc.tensor.matmul_mx(
-                out=z2[:], lhsT=ha_c[:].bitcast(FP8X4), lhsT_scale=ha_s[:],
+                out=s2[(g, "z2")][:], lhsT=ha_c[:].bitcast(FP8X4), lhsT_scale=ha_s[:],
                 rhs=w1_c[:].bitcast(FP8X4), rhs_scale=w1_s[:], start=False, stop=True,
             )
 
         def l2_bias(g):
-            if L2V:
-                v2 = tail.tile([P, D_OUT], F32, name="v2")
-                nc.vector.tensor_tensor(out=v2[:], in0=s2[(g, "z2")][:], in1=bw_bc[:], op=ALU.add)
-                s2[(g, "v2")] = v2
-                return
             zc = tail.tile([P, D_OUT], F32, name="zc")
             nc.scalar.copy(out=zc[:], in_=s2[(g, "z2")][:])
             v2 = tail.tile([P, D_OUT], F32, name="v2")
-            nc.gpsimd.tensor_tensor(out=v2[:], in0=zc[:], in1=bw_bc[:], op=ALU.add)
+            nc.gpsimd.tensor_tensor(out=v2[:], in0=zc[:], in1=bw_all[:], op=ALU.add)
             s2[(g, "v2")] = v2
 
         def l2_lrelu(g):
             v2 = s2[(g, "v2")]
-            if L2V == 2:
-                h2 = tail.tile([P, D_OUT], F32, name="h2")
-                nc.vector.scalar_tensor_tensor(
-                    out=h2[:], in0=v2[:], scalar=SLOPE, in1=v2[:], op0=ALU.mult, op1=ALU.max
-                )
-                s2[(g, "h2")] = h2
-                return
             up = tail.tile([P, D_OUT], F32, name="up")
-            if L2G:
-                nc.gpsimd.tensor_scalar(
-                    out=up[:], in0=v2[:], scalar1=1.0 - SLOPE, scalar2=0.0, op0=ALU.mult, op1=ALU.max
-                )
-                nc.gpsimd.tensor_scalar(
-                    out=v2[:], in0=v2[:], scalar1=SLOPE, scalar2=0.0, op0=ALU.mult, op1=ALU.add
-                )
-            else:
-                nc.scalar.activation(out=up[:], in_=v2[:], func=ACT.Relu, scale=1.0 - SLOPE)
-                nc.scalar.activation(out=v2[:], in_=v2[:], func=ACT.Copy, scale=SLOPE)
+            nc.scalar.activation(out=up[:], in_=v2[:], func=ACT.Relu, scale=1.0 - SLOPE)
+            nc.scalar.activation(out=v2[:], in_=v2[:], func=ACT.Copy, scale=SLOPE)
             h2 = tail.tile([P, D_OUT], F32, name="h2")
             nc.gpsimd.tensor_tensor(out=h2[:], in0=up[:], in1=v2[:], op=ALU.add)
             s2[(g, "h2")] = h2
 
-        def l2_norm(g):
+        def l2_store(g):
+            h2 = s2[(g, "h2")]
             sq = tail.tile([P, D_OUT], F32, name="sq")
             ss = tail.tile([P, 1], F32, name="ss")
-            nc.scalar.activation(
-                out=sq[:], in_=s2[(g, "h2")][:], func=ACT.Square, bias=tiny[:, 0:1], accum_out=ss[:]
-            )
+            nc.scalar.activation(out=sq[:], in_=h2[:], func=ACT.Square, bias=tiny[:, 0:1], accum_out=ss[:])
             rs = tail.tile([P, 1], F32, name="rs")
             nc.scalar.activation(out=rs[:], in_=ss[:], func=ACT.Abs_reciprocal_sqrt)
-            s2[(g, "rs")] = rs
-
-        def l2_res(g):
             res = tail.tile([P, D_OUT], F32, name="res")
-            if L2V:
-                nc.scalar.activation(
-                    out=res[:], in_=s2[(g, "h2")][:], func=ACT.Copy, scale=s2[(g, "rs")][:, 0:1]
-                )
-                nc.sync.dma_start(out=out[g * P : (g + 1) * P, :], in_=res[:])
-                return
             nc.gpsimd.tensor_scalar(
-                out=res[:], in0=s2[(g, "h2")][:], scalar1=s2[(g, "rs")][:, 0:1], scalar2=0.0,
-                op0=ALU.mult, op1=ALU.add,
+                out=res[:], in0=h2[:], scalar1=rs[:, 0:1], scalar2=0.0, op0=ALU.mult, op1=ALU.add
             )
             nc.sync.dma_start(out=out[g * P : (g + 1) * P, :], in_=res[:])
 
-        def l2_end(g):
+        def l2_last(g):
             halves = [slice(0, D_OUT // 2), slice(D_OUT // 2, D_OUT)]
             z2 = s2[(g, "z2")]
             v2 = tail.tile([P, D_OUT], F32, name="v2")
@@ -410,61 +340,66 @@ def tile_pinsageconv_t_kernel(tc, h_node, h_ngbrs, alpha, Wq, bq, Ww, bw, out):
             sq = tail.tile([P, D_OUT], F32, name="sq")
             ss = [tail.tile([P, 1], F32, name="ss0"), tail.tile([P, 1], F32, name="ss1")]
             for cols in halves:
-                nc.vector.tensor_tensor(out=v2[:, cols], in0=z2[:, cols], in1=bw_bc[:, cols], op=ALU.add)
-            for i, cols in enumerate(halves):
+                nc.vector.tensor_tensor(out=v2[:, cols], in0=z2[:, cols], in1=bw_all[:, cols], op=ALU.add)
+            for j, cols in enumerate(halves):
                 nc.vector.scalar_tensor_tensor(
                     out=h2[:, cols], in0=v2[:, cols], scalar=SLOPE, in1=v2[:, cols], op0=ALU.mult, op1=ALU.max
                 )
                 nc.scalar.activation(
-                    out=sq[:, cols], in_=h2[:, cols], func=ACT.Square, bias=tiny[:, 0:1], accum_out=ss[i][:]
+                    out=sq[:, cols], in_=h2[:, cols], func=ACT.Square, bias=tiny[:, 0:1], accum_out=ss[j][:]
                 )
             rs = tail.tile([P, 1], F32, name="rs")
             nc.scalar.activation(out=rs[:], in_=ss[0][:], func=ACT.Abs_reciprocal_sqrt, bias=ss[1][:, 0:1])
             res = [tail.tile([P, D_OUT // 2], F32, name="res0"), tail.tile([P, D_OUT // 2], F32, name="res1")]
+            rows = slice(g * P, (g + 1) * P)
             nc.vector.tensor_scalar(
                 out=res[0][:], in0=h2[:, halves[0]], scalar1=rs[:, 0:1], scalar2=None, op0=ALU.mult
             )
-            nc.sync.dma_start(out=out[g * P : (g + 1) * P, halves[0]], in_=res[0][:])
+            nc.sync.dma_start(out=out[rows, halves[0]], in_=res[0][:])
             nc.scalar.activation(out=res[1][:], in_=h2[:, halves[1]], func=ACT.Copy, scale=rs[:, 0:1])
-            nc.scalar.dma_start(out=out[g * P : (g + 1) * P, halves[1]], in_=res[1][:])
+            nc.scalar.dma_start(out=out[rows, halves[1]], in_=res[1][:])
 
         b_low = const.tile([P, HC], F32)
         b_high = const.tile([P, HC], F32)
-        a_f = const.tile([P, GROUPS, K_NGB], F32)
-        a_sum = const.tile([P, GROUPS], F32)
-        a_den = const.tile([P, GROUPS], F32)
-        a_rec = const.tile([P, GROUPS], F32)
-        a_n = const.tile([P, GROUPS, K_NGB], F32)
-
         wq_g = grp.tile([P, 4 * P, 4], BF16, align_bytes=64, tag="grouped", name="wq_g")
         wq_words = wq_raw[:].bitcast(F32)
-        wt0 = words_T(wq_words, 0, pz, "z")
-        wt1 = words_T(wq_words, 1, pz, "z")
+
+        def wq_quant(half):
+            cols = slice(2 * half * P, (2 * half + 2) * P)
+            quantise(wq_g[:, cols, :], wq_c[:, cols], wq_s[:, cols])
+
+        wq_bank0 = words_T(wq_words, 0, pz, "z")
         x_T(0, 0)
         x_T(0, 1)
+        wq_bank1 = words_T(wq_words, 1, pz, "z")
         bT = pz.tile([P, P], BF16, tag="z", name="bT")
         nc.tensor.transpose(bT[:], b_rows[:], ident_b[:])
-        words_copy(wt0, wq_g, 0, nc.scalar.copy)
-        words_copy(wt1, wq_g, 1, nc.vector.tensor_copy)
-        quantise(wq_g, wq_c[:], wq_s[:])
+        words_copy(wq_bank0, wq_g, 0, nc.scalar.copy)
+        wq_quant(0)
         x_copy(0, 0)
-        x_copy(0, 1)
+        x_copy(0, 1, nc.vector.tensor_copy)
         nc.vector.tensor_scalar(out=b_low[:], in0=bT[:, 0:HC], scalar1=SLOPE, scalar2=None, op0=ALU.mult)
-        nc.vector.tensor_scalar(
-            out=b_high[:], in0=bT[:, 0:HC], scalar1=1.0 - SLOPE, scalar2=None, op0=ALU.mult
-        )
+        nc.vector.tensor_scalar(out=b_high[:], in0=bT[:, 0:HC], scalar1=1.0 - SLOPE, scalar2=None, op0=ALU.mult)
         x_quant(0)
+        words_copy(wq_bank1, wq_g, 1, nc.scalar.copy)
+        wq_quant(1)
         x_T(1, 0)
         x_T(1, 1)
         x_copy(1, 0, nc.vector.tensor_copy)
         x_copy(1, 1, nc.vector.tensor_copy)
 
-        def norm_weights():
+        a_n = const.tile([P, GROUPS, K_NGB], F32)
+
+        def normalise_weights():
+            a_f = const.tile([P, GROUPS, K_NGB], F32)
             nc.vector.tensor_copy(out=a_f[:], in_=a_raw[:])
+            a_sum = const.tile([P, GROUPS], F32)
             nc.vector.tensor_reduce(out=a_sum[:], in_=a_f[:], axis=AX.X, op=ALU.add)
+            a_den = const.tile([P, GROUPS], F32)
             nc.vector.scalar_tensor_tensor(
                 out=a_den[:], in0=a_sum[:], scalar=0.0, in1=a_sum[:], op0=ALU.is_equal, op1=ALU.add
             )
+            a_rec = const.tile([P, GROUPS], F32)
             nc.vector.reciprocal(out=a_rec[:], in_=a_den[:])
             nc.vector.tensor_tensor(
                 out=a_n[:], in0=a_f[:], in1=a_rec[:].unsqueeze(2).to_broadcast([P, GROUPS, K_NGB]), op=ALU.mult
@@ -472,98 +407,93 @@ def tile_pinsageconv_t_kernel(tc, h_node, h_ngbrs, alpha, Wq, bq, Ww, bw, out):
 
         def due(i, lag):
             g, r = divmod(i - lag, QUADS)
-            if r == 0 and 1 <= g <= GROUPS:
-                return g - 1
-            return None
+            return g - 1 if r == 0 and g >= 1 else None
 
         for i in range(NQ):
-            nxt = i + AHEAD if i + AHEAD < NQ else None
-            if i + FIRST_LOADS < NQ:
-                load(i + FIRST_LOADS)
-            late_loads(i)
-            g1, g2, g3, g4, g5 = (due(i, lag + SUM_LAG) for lag in (0, 1, 2, 3, 4))
-            if g2 is not None:
-                l2_copy(g2)
-            for what in PORDER:
-                n = int(what[1]) if len(what) > 1 else 0
-                if what[0] == "M":
-                    for hc in range(n, int(what[2])):
-                        mx(i, hc)
-                elif what == "Z" and g3 is not None:
-                    l2_mx0(g3)
-                    l2_mx1(g3)
-                elif what[0] == "X" and nxt is not None:
-                    x_T(nxt, n)
-                    if i == 0 and n == 1:
-                        early = [(qd, half) for qd in range(2, AHEAD) for half in range(2)]
-                        for qd, half in early:
-                            x_T(qd, half)
-                            if half == 1:
-                                x_copy(qd, 0)
-                                x_copy(qd, 1)
-                elif what[0] == "K" and i >= 1:
-                    tk(i - 1, n)
-                elif what[0] == "j" and i >= 2:
-                    tk(i - 2, n)
-                elif what == "T" and g1 is not None:
-                    l2_T(g1)
-                elif what == "P" and 0 <= i - PREP0 < 8:
-                    prep_T(i - PREP0)
-            if i == 0:
-                norm_weights()
-            for what in ORDER:
-                n = int(what[1]) if len(what) > 1 else 0
-                if what[0] == "y":
-                    low(i, n)
-                elif what == "d":
-                    if (i + AHEAD - 1, 1) in xt_ps and i > 0:
-                        x_copy(i + AHEAD - 1, 1)
-                elif what[0] == "c" and nxt is not None:
-                    x_copy(nxt, n)
-                elif what == "r":
-                    upper(i)
-                elif what[0] == "e":
-                    lrelu(i, n, int(what[2]))
-                elif what[0] == "F":
-                    qd = i - 1 if "K%d" % n in PORDER else i - 2
-                    if qd >= 0:
-                        fma(qd, n)
-                elif what == "Q":
-                    if i == 0:
-                        for qd in range(1, QA):
-                            if pair_of(qd)[0] == qd:
-                                x_quant(qd)
-                    if i + QA < NQ and pair_of(i + QA)[0] == i + QA:
-                        x_quant(i + QA)
-                    if g2 is not None:
-                        l2_quant(g2)
-                    if 0 <= i - PREP0 - 1 < 8:
-                        prep_quant(i - PREP0 - 1)
-            if g3 is not None:
-                l2_bias(g3)
-            if g4 is not None:
-                l2_lrelu(g4)
-            if g5 is not None:
-                l2_norm(g5)
-                l2_res(g5)
-            if 0 <= i - PREP0 < 8:
-                prep_copy(i - PREP0)
+            old = i - 1
+            new = i + AHEAD
+            job = i - PREP_FIRST
+            if i + LOADS < NQ:
+                load(i + LOADS)
+            load_second_layer(i)
+            g_T, g_quant, g_mx, g_lrelu, g_store = (due(i, lag) for lag in (2, 3, 4, 5, 6))
+            if g_quant is not None:
+                l2_copy(g_quant)
 
-        g = GROUPS - 1
-        for kk in range(KQ):
-            if "j%d" % kk in PORDER:
-                tk(NQ - 2, kk)
-                fma(NQ - 2, kk)
-        more = []
-        for kk in range(KQ):
-            tk(NQ - 1, kk)
-            if kk in LAST_S:
-                more.append(scaled(NQ - 1, kk))
+            mx(i, 0)
+            mx(i, 1)
+            if i > 0:
+                neighbour_T(old, 2, warm=True)
+                if new < NQ:
+                    x_T(new, 0)
+                    x_T(new, 1)
+            mx(i, 2)
+            mx(i, 3)
+            if i > 0:
+                neighbour_T(old, 3, warm=True)
+                if g_mx is not None:
+                    l2_mx_node(g_mx)
+                    l2_mx_agg(g_mx)
+                neighbour_T(old, 0)
+                if 0 <= job < PREP_JOBS:
+                    prep_T(job)
+                if g_T is not None:
+                    l2_T(g_T)
+                neighbour_T(old, 1)
+
+            if i > 0 and new - 1 < NQ:
+                x_copy(new - 1, 1)
+            scalar_part(i, 0)
+            scalar_part(i, 1)
+            if i > 0 and new < NQ:
+                x_copy(new, 0)
+            scalar_part(i, 2)
+            scalar_part(i, 3)
+
+            if i + 1 < NQ and lead_of(i + 1) == i + 1:
+                x_quant(i + 1)
+            if g_quant is not None:
+                l2_quant(g_quant)
+            if 0 <= job - 1 < PREP_JOBS:
+                prep_quant(job - 1)
+            if i == 0 or i == NQ - 1:
+                vector_whole(i)
+                vector_part(i)
+                if i > 0:
+                    weigh(old, 2)
             else:
-                fma(NQ - 1, kk)
-        l2_mx0(g)
-        l2_T(g, more)
+                weigh(old, 2)
+                vector_whole(i)
+                vector_part(i)
+            if i > 0:
+                weigh(old, 3)
+                weigh(old, 0)
+                weigh(old, 1)
+            else:
+                normalise_weights()
+                for qd in range(2, AHEAD + 1):
+                    x_T(qd, 0)
+                    x_T(qd, 1)
+                    x_copy(qd, 0)
+                    if qd < AHEAD:
+                        x_copy(qd, 1)
+
+            if g_mx is not None:
+                l2_bias(g_mx)
+            if g_lrelu is not None:
+                l2_lrelu(g_lrelu)
+            if g_store is not None:
+                l2_store(g_store)
+            if 0 <= job < PREP_JOBS:
+                prep_copy(job)
+
+        for kk in range(KQ):
+            neighbour_T(NQ - 1, kk, warm=kk >= 2)
+            weigh(NQ - 1, kk)
+        g = GROUPS - 1
+        l2_mx_node(g)
+        l2_T(g)
         l2_copy(g)
         l2_quant(g)
-        l2_mx1(g)
-        l2_end(g)
+        l2_mx_agg(g)
+        l2_last(g)

from contextlib import ExitStack

import concourse.mybir as mybir
from concourse.masks import make_identity

F32 = mybir.dt.float32
BF16 = mybir.dt.bfloat16
U32 = mybir.dt.uint32
U8 = mybir.dt.uint8
FP8X4 = mybir.dt.float8_e4m3fn_x4
ALU = mybir.AluOpType
ACT = mybir.ActivationFunctionType
AX = mybir.AxisListType

P = 128
N_NODES, K_NGB, D_IN, D_HID, D_OUT = 512, 32, 512, 512, 512
SLOPE = 0.01
TINY = 1e-19
GROUPS = N_NODES // P
KQ = 4
QUADS = K_NGB // KQ
NQ = GROUPS * QUADS
HC = D_HID // P
COLS = KQ * P
ONE_BY_ONE = 2
AHEAD = 3
LOADS = 6
PREP_FIRST, PREP_JOBS = 2, 8
WARM_COLS = 128

WHOLE = 2
PART_V, PART_S = 2, 3
SLOTS = HC + 2

FLOPS = 2 * N_NODES * K_NGB * D_IN * D_HID + 2 * N_NODES * (D_IN + D_HID) * D_OUT


def parts_of(hc):
    return (hc,) if hc < WHOLE else (hc, hc + HC - WHOLE)


def lead_of(qd):
    return qd if qd < ONE_BY_ONE else qd - (qd - ONE_BY_ONE) % 2


def count_of(lead):
    return 1 if lead < ONE_BY_ONE else 2


def tile_pinsageconv_t_kernel(tc, h_node, h_ngbrs, alpha, Wq, bq, Ww, bw, out):
    nc = tc.nc
    with ExitStack() as ctx:
        const = ctx.enter_context(tc.tile_pool(name="const", bufs=1))
        xin = ctx.enter_context(tc.tile_pool(name="xin", bufs=LOADS + 1))
        grp = ctx.enter_context(tc.tile_pool(name="grp", bufs=4))
        qnt = ctx.enter_context(tc.tile_pool(name="qnt", bufs=4))
        epool = ctx.enter_context(tc.tile_pool(name="epool", bufs=4))
        prep = ctx.enter_context(tc.tile_pool(name="prep", bufs=2))
        tail = ctx.enter_context(tc.tile_pool(name="tail", bufs=1))
        pz = ctx.enter_context(tc.psum_pool(name="pz", bufs=3))
        pe = ctx.enter_context(tc.psum_pool(name="pe", bufs=5))
        ctx.enter_context(tc.manual_schedule())

        ident_f = const.tile([P, P], F32)
        make_identity(nc, ident_f[:])
        ident_b = const.tile([P, P], BF16)
        make_identity(nc, ident_b[:])

        wq_raw = const.tile([P, HC, D_IN], BF16)
        wq_view = Wq.rearrange("(b p) i -> p b i", p=P)
        nc.sync.dma_start(out=wq_raw[:, 0:2, :], in_=wq_view[:, 0:2, :])

        x_sb = {}

        def load(qd):
            g, q = divmod(qd, QUADS)
            x_sb[qd] = xin.tile([P, KQ, D_IN], BF16, name="x_sb")
            step = KQ // 2 if qd == 0 else KQ
            for kk in range(0, KQ, step):
                k = q * KQ + kk
                nc.sync.dma_start(
                    out=x_sb[qd][:, kk : kk + step, :], in_=h_ngbrs[g * P : (g + 1) * P, k : k + step, :]
                )

        load(0)
        nc.sync.dma_start(out=wq_raw[:, 2:4, :], in_=wq_view[:, 2:4, :])

        b_rows = const.tile([P, P], BF16)
        nc.vector.memset(b_rows[:], 0.0)
        one = const.tile([P, 1], F32)
        nc.vector.memset(one[:], 1.0)
        tiny = const.tile([P, 1], F32)
        nc.vector.tensor_scalar(out=tiny[:], in0=one[:], scalar1=TINY, scalar2=None, op0=ALU.mult)
        a_raw = const.tile([P, GROUPS, K_NGB], BF16)
        nc.scalar.dma_start(out=a_raw[:], in_=alpha.rearrange("(g p) k o -> p g (k o)", p=P))
        nc.scalar.dma_start(out=b_rows[0:HC, :], in_=bq.rearrange("(b p) -> b p", p=P))
        root = const.tile([P, 1], F32)
        nc.scalar.activation(out=root[:], in_=one[:], func=ACT.Abs_reciprocal_sqrt)

        for qd in range(1, LOADS):
            load(qd)

        ww_raw = const.tile([P, D_OUT // P, D_IN + D_HID], BF16)
        hn_raw = const.tile([P, GROUPS, D_IN], BF16)
        bw_all = const.tile([P, D_OUT], BF16)

        def load_second_layer(i):
            if i == 0:
                nc.sync.dma_start(out=ww_raw[:], in_=Ww.rearrange("(b p) c -> p b c", p=P))
            elif i == 1:
                nc.sync.dma_start(out=hn_raw[:], in_=h_node.rearrange("(g p) i -> p g i", p=P))
            elif i == 4:
                nc.sync.dma_start(out=bw_all[:], in_=bw.partition_broadcast(P))

        def words_T(words, half, pool, tag):
            bank = pool.tile([P, 2, 2, P], F32, tag=tag, name="bank")
            for b in range(2):
                for u in range(2):
                    nc.tensor.transpose(bank[:, b, u, :], words[:, 2 * half + b, u * P : (u + 1) * P], ident_f[:])
            return bank

        def words_copy(bank, grouped, half, copy, first=0):
            rows = slice(first + 2 * half * P, first + (2 * half + 2) * P)
            copy(
                out=grouped[:].bitcast(F32)[:, rows, :].rearrange("p (b c) u -> p b c u", b=2),
                in_=bank[:].rearrange("p b u c -> p b c u"),
            )

        def quantise(grouped, codes, scales):
            nc.vector.quantize_mx(
                out=codes.bitcast(FP8X4), scales=scales, in_=grouped.rearrange("p c t -> p (c t)")
            )

        wq_c = const.tile([P, D_HID], U32, align_bytes=64)
        wq_s = const.tile([P, D_HID], U8, align_bytes=64)

        w0_c = const.tile([P, D_OUT], U32, align_bytes=64)
        w0_s = const.tile([P, D_OUT], U8, align_bytes=64)
        w1_c = const.tile([P, D_OUT], U32, align_bytes=64)
        w1_s = const.tile([P, D_OUT], U8, align_bytes=64)
        hn_c = const.tile([P, N_NODES], U32, align_bytes=64)
        hn_s = const.tile([P, N_NODES], U8, align_bytes=64)
        prep_g = {}
        prep_bank = {}

        def prep_T(job):
            if job in (0, 2, 4):
                prep_g[job] = prep.tile([P, 4 * P, 4], BF16, align_bytes=64, tag="prep_g", name="prep_g")
            if job < 2:
                prep_bank[job] = words_T(ww_raw[:].bitcast(F32)[:, :, 0 : D_IN // 2], job, pe, "eT")
            elif job < 4:
                prep_bank[job] = words_T(hn_raw[:].bitcast(F32), job - 2, pe, "eT")
            else:
                bank = pe.tile([P, 4, P], BF16, tag="eT", name="wt")
                for t in range(4):
                    cols = slice(D_IN + t * P, D_IN + (t + 1) * P)
                    nc.tensor.transpose(bank[:, t, :], ww_raw[:, job - 4, cols], ident_b[:])
                prep_bank[job] = bank

        def prep_copy(job):
            if job < 4:
                words_copy(prep_bank[job], prep_g[job - job % 2], job % 2, nc.scalar.copy)
            else:
                rows = slice((job - 4) * P, (job - 3) * P)
                nc.scalar.copy(out=prep_g[4][:, rows, :], in_=prep_bank[job][:].rearrange("p t c -> p c t"))

        def prep_quant(job):
            if job == 1:
                quantise(prep_g[0][:], w0_c[:], w0_s[:])
            elif job == 3:
                quantise(prep_g[2][:], hn_c[:], hn_s[:])
            elif job == 7:
                quantise(prep_g[4][:], w1_c[:], w1_s[:])

        grouped = {}
        x_bank = {}
        x_codes = {}
        z_bank = {}
        e_sb = {}
        eT_bank = {}
        acc = {}

        def x_T(qd, half):
            lead = lead_of(qd)
            if half == 0 and lead == qd:
                grouped[lead] = grp.tile(
                    [P, count_of(lead) * COLS, 4], BF16, align_bytes=64, tag="grouped", name="grouped"
                )
            x_bank[(qd, half)] = words_T(x_sb[qd][:].bitcast(F32), half, pe, "eT")

        def x_copy(qd, half, copy=nc.scalar.copy):
            lead = lead_of(qd)
            words_copy(x_bank[(qd, half)], grouped[lead], half, copy, (qd - lead) * COLS)

        def x_quant(lead):
            n = count_of(lead)
            codes = qnt.tile([P, n * COLS], U32, align_bytes=64, name="codes")
            scales = qnt.tile([P, n * COLS], U8, align_bytes=64, name="scales")
            quantise(grouped[lead][:], codes[:], scales[:])
            for j in range(n):
                cols = slice(j * COLS, (j + 1) * COLS)
                x_codes[lead + j] = (codes[:, cols], scales[:, cols])

        def mx(qd, hc):
            if hc == 0:
                e_sb[qd] = epool.tile([P, SLOTS, COLS], F32, name="e")
            cols = slice(hc * P, (hc + 1) * P)
            codes, scales = x_codes[qd]
            z_bank[hc] = pz.tile([P, COLS], F32, tag="z", name="z")
            nc.tensor.matmul_mx(
                out=z_bank[hc][:], lhsT=wq_c[:, cols].bitcast(FP8X4), lhsT_scale=wq_s[:, cols],
                rhs=codes.bitcast(FP8X4), rhs_scale=scales, start=True, stop=True,
            )

        def scalar_part(qd, hc):
            nc.scalar.activation(
                out=e_sb[qd][:, parts_of(hc)[-1], :], in_=z_bank[hc][:], func=ACT.Identity,
                bias=b_low[:, hc : hc + 1], scale=SLOPE,
            )
            if hc == PART_S:
                nc.scalar.activation(
                    out=e_sb[qd][:, hc, :], in_=z_bank[hc][:], func=ACT.Relu, bias=b_high[:, hc : hc + 1],
                    scale=1.0 - SLOPE,
                )

        def vector_whole(qd):
            e = e_sb[qd][:, 0:WHOLE, :]
            nc.vector.scalar_tensor_tensor(out=e, in0=e, scalar=1.0 / SLOPE, in1=e, op0=ALU.mult, op1=ALU.max)

        def vector_part(qd):
            upper, u = parts_of(PART_V)
            nc.vector.tensor_scalar(
                out=e_sb[qd][:, upper : upper + 1, :], in0=e_sb[qd][:, u : u + 1, :],
                scalar1=(1.0 - SLOPE) / SLOPE, scalar2=0.0, op0=ALU.mult, op1=ALU.max,
            )

        def neighbour_T(qd, kk, warm=False):
            bank = pe.tile([P, D_HID], F32, tag="eT", name="eT")
            eT_bank[(qd, kk)] = bank
            if warm:
                nc.tensor.matmul(
                    out=bank[:, 0:WARM_COLS], lhsT=ident_b[:], rhs=wq_raw[:, 0, 0:WARM_COLS], start=True, stop=True
                )
            parts = [(slot, hc) for hc in range(HC) for slot in parts_of(hc)]
            for j, (slot, hc) in enumerate(parts):
                nc.tensor.matmul(
                    out=bank[:, hc * P : (hc + 1) * P], lhsT=e_sb[qd][:, slot, kk * P : (kk + 1) * P],
                    rhs=ident_f[:], is_transpose=True, start=(j == 0), stop=(j == len(parts) - 1),
                )

        def weigh(qd, kk):
            g, q = divmod(qd, QUADS)
            k = q * KQ + kk
            key = (g, k % 2)
            weight = a_n[:, g, k : k + 1]
            bank = eT_bank[(qd, kk)]
            if key not in acc:
                acc[key] = const.tile([P, D_HID], F32, name="acc%d_%d" % key)
                nc.vector.tensor_scalar(
                    out=acc[key][:], in0=bank[:], scalar1=weight, scalar2=None, op0=ALU.mult
                )
            else:
                nc.vector.scalar_tensor_tensor(
                    out=acc[key][:], in0=bank[:], scalar=weight, in1=acc[key][:], op0=ALU.mult, op1=ALU.add
                )

        s2 = {}

        def l2_T(g):
            hT = pe.tile([P, HC, P], F32, tag="eT", name="hT")
            for j in range(2):
                for hc in range(HC):
                    nc.tensor.matmul(
                        out=hT[:, hc, :], lhsT=acc[(g, j)][:, hc * P : (hc + 1) * P], rhs=ident_f[:],
                        is_transpose=True, start=(j == 0 and hc == 0), stop=(j == 1 and hc == HC - 1),
                    )
            s2[(g, "hT")] = hT

        def l2_copy(g):
            hg = tail.tile([P, P, 4], BF16, align_bytes=64, name="hg")
            nc.scalar.copy(out=hg[:], in_=s2[(g, "hT")][:].rearrange("p t c -> p c t"))
            s2[(g, "hg")] = hg

        def l2_quant(g):
            ha_c = tail.tile([P, P], U32, align_bytes=64, name="ha_c")
            ha_s = tail.tile([P, P], U8, align_bytes=64, name="ha_s")
            quantise(s2[(g, "hg")][:], ha_c[:], ha_s[:])
            s2[(g, "ha")] = (ha_c, ha_s)

        def l2_mx_node(g):
            z2 = pz.tile([P, D_OUT], F32, tag="z", name="z2")
            cols = slice(g * P, (g + 1) * P)
            s2[(g, "z2")] = z2
            nc.tensor.matmul_mx(
                out=z2[:], lhsT=hn_c[:, cols].bitcast(FP8X4), lhsT_scale=hn_s[:, cols],
                rhs=w0_c[:].bitcast(FP8X4), rhs_scale=w0_s[:], start=True, stop=False,
            )

        def l2_mx_agg(g):
            ha_c, ha_s = s2[(g, "ha")]
            nc.tensor.matmul_mx(
                out=s2[(g, "z2")][:], lhsT=ha_c[:].bitcast(FP8X4), lhsT_scale=ha_s[:],
                rhs=w1_c[:].bitcast(FP8X4), rhs_scale=w1_s[:], start=False, stop=True,
            )

        def l2_bias(g):
            zc = tail.tile([P, D_OUT], F32, name="zc")
            nc.scalar.copy(out=zc[:], in_=s2[(g, "z2")][:])
            v2 = tail.tile([P, D_OUT], F32, name="v2")
            nc.gpsimd.tensor_tensor(out=v2[:], in0=zc[:], in1=bw_all[:], op=ALU.add)
            s2[(g, "v2")] = v2

        def l2_lrelu(g):
            v2 = s2[(g, "v2")]
            up = tail.tile([P, D_OUT], F32, name="up")
            nc.scalar.activation(out=up[:], in_=v2[:], func=ACT.Relu, scale=1.0 - SLOPE)
            nc.scalar.activation(out=v2[:], in_=v2[:], func=ACT.Copy, scale=SLOPE)
            h2 = tail.tile([P, D_OUT], F32, name="h2")
            nc.gpsimd.tensor_tensor(out=h2[:], in0=up[:], in1=v2[:], op=ALU.add)
            s2[(g, "h2")] = h2

        def l2_store(g):
            h2 = s2[(g, "h2")]
            sq = tail.tile([P, D_OUT], F32, name="sq")
            ss = tail.tile([P, 1], F32, name="ss")
            nc.scalar.activation(out=sq[:], in_=h2[:], func=ACT.Square, bias=tiny[:, 0:1], accum_out=ss[:])
            rs = tail.tile([P, 1], F32, name="rs")
            nc.scalar.activation(out=rs[:], in_=ss[:], func=ACT.Abs_reciprocal_sqrt)
            res = tail.tile([P, D_OUT], F32, name="res")
            nc.gpsimd.tensor_scalar(
                out=res[:], in0=h2[:], scalar1=rs[:, 0:1], scalar2=0.0, op0=ALU.mult, op1=ALU.add
            )
            nc.sync.dma_start(out=out[g * P : (g + 1) * P, :], in_=res[:])

        def l2_last(g):
            halves = [slice(0, D_OUT // 2), slice(D_OUT // 2, D_OUT)]
            z2 = s2[(g, "z2")]
            v2 = tail.tile([P, D_OUT], F32, name="v2")
            h2 = tail.tile([P, D_OUT], F32, name="h2")
            sq = tail.tile([P, D_OUT], F32, name="sq")
            ss = [tail.tile([P, 1], F32, name="ss0"), tail.tile([P, 1], F32, name="ss1")]
            for cols in halves:
                nc.vector.tensor_tensor(out=v2[:, cols], in0=z2[:, cols], in1=bw_all[:, cols], op=ALU.add)
            for j, cols in enumerate(halves):
                nc.vector.scalar_tensor_tensor(
                    out=h2[:, cols], in0=v2[:, cols], scalar=SLOPE, in1=v2[:, cols], op0=ALU.mult, op1=ALU.max
                )
                nc.scalar.activation(
                    out=sq[:, cols], in_=h2[:, cols], func=ACT.Square, bias=tiny[:, 0:1], accum_out=ss[j][:]
                )
            rs = tail.tile([P, 1], F32, name="rs")
            nc.scalar.activation(out=rs[:], in_=ss[0][:], func=ACT.Abs_reciprocal_sqrt, bias=ss[1][:, 0:1])
            res = [tail.tile([P, D_OUT // 2], F32, name="res0"), tail.tile([P, D_OUT // 2], F32, name="res1")]
            rows = slice(g * P, (g + 1) * P)
            nc.vector.tensor_scalar(
                out=res[0][:], in0=h2[:, halves[0]], scalar1=rs[:, 0:1], scalar2=None, op0=ALU.mult
            )
            nc.sync.dma_start(out=out[rows, halves[0]], in_=res[0][:])
            nc.scalar.activation(out=res[1][:], in_=h2[:, halves[1]], func=ACT.Copy, scale=rs[:, 0:1])
            nc.scalar.dma_start(out=out[rows, halves[1]], in_=res[1][:])

        b_low = const.tile([P, HC], F32)
        b_high = const.tile([P, HC], F32)
        wq_g = grp.tile([P, 4 * P, 4], BF16, align_bytes=64, tag="grouped", name="wq_g")
        wq_words = wq_raw[:].bitcast(F32)

        def wq_quant(half):
            cols = slice(2 * half * P, (2 * half + 2) * P)
            quantise(wq_g[:, cols, :], wq_c[:, cols], wq_s[:, cols])

        wq_bank0 = words_T(wq_words, 0, pz, "z")
        x_T(0, 0)
        x_T(0, 1)
        wq_bank1 = words_T(wq_words, 1, pz, "z")
        bT = pz.tile([P, P], BF16, tag="z", name="bT")
        nc.tensor.transpose(bT[:], b_rows[:], ident_b[:])
        words_copy(wq_bank0, wq_g, 0, nc.scalar.copy)
        wq_quant(0)
        x_copy(0, 0)
        x_copy(0, 1, nc.vector.tensor_copy)
        nc.vector.tensor_scalar(out=b_low[:], in0=bT[:, 0:HC], scalar1=SLOPE, scalar2=None, op0=ALU.mult)
        nc.vector.tensor_scalar(out=b_high[:], in0=bT[:, 0:HC], scalar1=1.0 - SLOPE, scalar2=None, op0=ALU.mult)
        x_quant(0)
        words_copy(wq_bank1, wq_g, 1, nc.scalar.copy)
        wq_quant(1)
        x_T(1, 0)
        x_T(1, 1)
        x_copy(1, 0, nc.vector.tensor_copy)
        x_copy(1, 1, nc.vector.tensor_copy)

        a_n = const.tile([P, GROUPS, K_NGB], F32)

        def normalise_weights():
            a_f = const.tile([P, GROUPS, K_NGB], F32)
            nc.vector.tensor_copy(out=a_f[:], in_=a_raw[:])
            a_sum = const.tile([P, GROUPS], F32)
            nc.vector.tensor_reduce(out=a_sum[:], in_=a_f[:], axis=AX.X, op=ALU.add)
            a_den = const.tile([P, GROUPS], F32)
            nc.vector.scalar_tensor_tensor(
                out=a_den[:], in0=a_sum[:], scalar=0.0, in1=a_sum[:], op0=ALU.is_equal, op1=ALU.add
            )
            a_rec = const.tile([P, GROUPS], F32)
            nc.vector.reciprocal(out=a_rec[:], in_=a_den[:])
            nc.vector.tensor_tensor(
                out=a_n[:], in0=a_f[:], in1=a_rec[:].unsqueeze(2).to_broadcast([P, GROUPS, K_NGB]), op=ALU.mult
            )

        def due(i, lag):
            g, r = divmod(i - lag, QUADS)
            return g - 1 if r == 0 and g >= 1 else None

        for i in range(NQ):
            old = i - 1
            new = i + AHEAD
            job = i - PREP_FIRST
            if i + LOADS < NQ:
                load(i + LOADS)
            load_second_layer(i)
            g_T, g_quant, g_mx, g_lrelu, g_store = (due(i, lag) for lag in (2, 3, 4, 5, 6))
            if g_quant is not None:
                l2_copy(g_quant)

            mx(i, 0)
            mx(i, 1)
            if i > 0:
                neighbour_T(old, 2, warm=True)
                if new < NQ:
                    x_T(new, 0)
                    x_T(new, 1)
            mx(i, 2)
            mx(i, 3)
            if i > 0:
                neighbour_T(old, 3, warm=True)
                if g_mx is not None:
                    l2_mx_node(g_mx)
                    l2_mx_agg(g_mx)
                neighbour_T(old, 0)
                if 0 <= job < PREP_JOBS:
                    prep_T(job)
                if g_T is not None:
                    l2_T(g_T)
                neighbour_T(old, 1)

            if i > 0 and new - 1 < NQ:
                x_copy(new - 1, 1)
            scalar_part(i, 0)
            scalar_part(i, 1)
            if i > 0 and new < NQ:
                x_copy(new, 0)
            scalar_part(i, 2)
            scalar_part(i, 3)

            if i + 1 < NQ and lead_of(i + 1) == i + 1:
                x_quant(i + 1)
            if g_quant is not None:
                l2_quant(g_quant)
            if 0 <= job - 1 < PREP_JOBS:
                prep_quant(job - 1)
            if i == 0 or i == NQ - 1:
                vector_whole(i)
                vector_part(i)
                if i > 0:
                    weigh(old, 2)
            else:
                weigh(old, 2)
                vector_whole(i)
                vector_part(i)
            if i > 0:
                weigh(old, 3)
                weigh(old, 0)
                weigh(old, 1)
            else:
                normalise_weights()
                for qd in range(2, AHEAD + 1):
                    x_T(qd, 0)
                    x_T(qd, 1)
                    x_copy(qd, 0)
                    if qd < AHEAD:
                        x_copy(qd, 1)

            if g_mx is not None:
                l2_bias(g_mx)
            if g_lrelu is not None:
                l2_lrelu(g_lrelu)
            if g_store is not None:
                l2_store(g_store)
            if 0 <= job < PREP_JOBS:
                prep_copy(job)

        for kk in range(KQ):
            neighbour_T(NQ - 1, kk, warm=kk >= 2)
            weigh(NQ - 1, kk)
        g = GROUPS - 1
        l2_mx_node(g)
        l2_T(g)
        l2_copy(g)
        l2_quant(g)
        l2_mx_agg(g)
        l2_last(g)
